import numpy as np
import ml_dtypes


def mxq(x, axis, fmt="e4m3"):
    dtype, down = {"e4m3": (ml_dtypes.float8_e4m3fn, 7), "e5m2": (ml_dtypes.float8_e5m2, 14)}[fmt]
    v = np.moveaxis(np.asarray(x, np.float32).astype(ml_dtypes.bfloat16).astype(np.float64), axis, -1)
    blocks = v.reshape(v.shape[:-1] + (-1, 32))
    amax = np.abs(blocks).max(-1, keepdims=True)
    byte = np.maximum(np.where(amax > 0, np.frexp(amax)[1] - 1 + 127, 0) - down, 1)
    scale = np.exp2(byte - 127.0)
    codes = (blocks / scale).astype(np.float32).astype(dtype).astype(np.float64)
    return np.moveaxis((codes * scale).reshape(v.shape), -1, axis)


WIDE = False


def mx_kscale(k):
    if not WIDE:
        return np.ones(k)
    levels = np.array([10, -10, 5, -5, 0])
    if k % 512:
        return np.exp2(np.random.permutation(np.resize(levels, k // 32))).repeat(32)
    a = np.empty((k // 512, 16))
    for p in range(k // 512):
        a[p, :8] = np.random.permutation(np.resize(levels, 8))
        for g in range(8):
            far = levels[np.abs(levels - a[p, g]) >= 10]
            a[p, g + 8] = far[np.random.randint(len(far))]
    return np.exp2(a.ravel()).repeat(32)


BF16 = ml_dtypes.bfloat16


def bf(x):
    return np.asarray(x, np.float32).astype(BF16)


def f64(x):
    return np.asarray(x).astype(np.float64)


B, L, DIM, H, D, QB = 1, 512, 2048, 16, 128, 512
HD = H * D
HALF = D // 2
EPS = 1e-6


def apply_rotary_emb(u, cos, sin):
    u1, u2 = u[..., :HALF], u[..., HALF:]
    return np.concatenate([u1 * cos + u2 * sin, u1 * -sin + u2 * cos], axis=-1)


def rms_norm(u):
    return u * (1.0 / np.sqrt(np.mean(u * u, axis=-1, keepdims=True) + EPS))


def draw0():
    s = mx_kscale(DIM)
    inv_freq = 1.0 / (10000.0 ** (np.arange(HALF) / HALF))
    ang = np.arange(L)[:, None] * inv_freq[None, :]
    return {"x": bf(np.random.standard_normal((B, L, DIM)) * s),
            "cos": bf(np.cos(ang)[:, None, :]),
            "sin": bf(np.sin(ang)[:, None, :]),
            "Wq": bf(np.random.standard_normal((DIM, HD)) / np.sqrt(DIM) / s[:, None]),
            "Wk": bf(np.random.standard_normal((DIM, D)) / np.sqrt(DIM) / s[:, None]),
            "Wv": bf(np.random.standard_normal((DIM, D)) / np.sqrt(DIM) / s[:, None])}


def core(x, cos, sin, Wq, Wk, Wv):
    xq = mxq(f64(x), 2, "e4m3")
    c, sn = f64(cos), f64(sin)
    q = (xq @ mxq(f64(Wq), 0, "e4m3")).reshape(B, L, H, D)
    k = xq @ mxq(f64(Wk), 0, "e4m3")
    v = xq @ mxq(f64(Wv), 0, "e4m3")
    q = rms_norm(apply_rotary_emb(q, c, sn))
    k = rms_norm(apply_rotary_emb(k[:, :, None, :], c, sn))[:, :, 0, :]
    return q, k, v


def e4m3fn_bytes(y):
    return np.clip(np.asarray(y, np.float64), -448.0, 448.0).astype(np.float32).astype(ml_dtypes.float8_e4m3fn).view(np.uint8)


def e4m3fn_values(b):
    return np.asarray(b, np.uint8).view(ml_dtypes.float8_e4m3fn).astype(np.float64)


def setup_inputs():
    d = draw0()
    x0 = np.asarray(d['Wq']).astype(np.float64)
    s = (np.max(np.abs(x0), axis=(1,), keepdims=True) / 448.0).astype(np.float32)
    out = {}
    for k, v in d.items():
        if k == 'Wq':
            out['Wq_bytes'] = e4m3fn_bytes(x0 / s.astype(np.float64))
            out['Wq_scale'] = s
        else:
            out[k] = v
    return out


def reference(x, cos, sin, Wq_bytes, Wq_scale, Wk, Wv):
    return core(x, cos, sin, e4m3fn_values(Wq_bytes) * Wq_scale.astype(np.float64), Wk, Wv)

@@ -1,0 +1,317 @@
+from contextlib import ExitStack
+
+import concourse.mybir as mybir
+from concourse.masks import make_identity
+
+F32 = mybir.dt.float32
+BF16 = mybir.dt.bfloat16
+U32 = mybir.dt.uint32
+U8 = mybir.dt.uint8
+FP8 = mybir.dt.float8_e4m3fn
+FP8X4 = mybir.dt.float8_e4m3fn_x4
+ACT = mybir.ActivationFunctionType
+ALU = mybir.AluOpType
+
+L, DIM, H, D = 512, 2048, 16, 128
+HALF = D // 2
+EPS = 1e-6
+P = 128
+PACK = 4
+G = DIM // (P * PACK)
+MT = L // P
+NC = 512
+CH = (H * D) // NC
+UNITS = CH * G
+
+FLOPS = 2 * L * DIM * (H * D + 2 * D)
+
+VW = [2, 0, 0, 0, 0, 0, 0, 0, 0, 0, 0, 0, 0, 0, 0, 0]
+ADD_G_FROM = 10
+
+
+def tile_multiqueryattention_pa_kernel(tc, x, cos, sin, Wq_bytes, Wq_scale, Wk, Wv, out_0, out_1, out_2):
+    nc = tc.nc
+    with ExitStack() as ctx:
+        keep = ctx.enter_context(tc.tile_pool(name="keep", bufs=1))
+        wd_pool = ctx.enter_context(tc.tile_pool(name="wdp", bufs=6))
+        wi_pool = ctx.enter_context(tc.tile_pool(name="wip", bufs=4))
+        xg_pool = ctx.enter_context(tc.tile_pool(name="xgp", bufs=2))
+        a_pool = ctx.enter_context(tc.tile_pool(name="ap", bufs=6))
+        b_pool = ctx.enter_context(tc.tile_pool(name="bp", bufs=3))
+        st_pool = ctx.enter_context(tc.tile_pool(name="stp", bufs=4))
+        psum = ctx.enter_context(tc.psum_pool(name="psum", bufs=8))
+        ctx.enter_context(tc.manual_schedule())
+
+        x_v = x[0].rearrange("(m p) k -> m p k", p=P)
+        cos_v = cos.rearrange("(m p) o j -> p m (o j)", p=P)
+        sin_v = sin.rearrange("(m p) o j -> p m (o j)", p=P)
+        wqb_v = Wq_bytes.rearrange("(g p t) n -> g p t n", p=P, t=PACK)
+        wqs_v = Wq_scale.rearrange("(g p t) o -> p g (t o)", p=P, t=PACK)
+        wk_v = Wk.rearrange("(g p t) n -> p g (t n)", p=P, t=PACK)
+        wv_v = Wv.rearrange("(g p t) n -> p g (t n)", p=P, t=PACK)
+        o0_v = out_0[0].rearrange("(m p) h d -> m p (h d)", p=P)
+        o1_v = out_1[0].rearrange("(m p) d -> p m d", p=P)
+        o2_v = out_2[0].rearrange("(m p) d -> p m d", p=P)
+
+        ident = keep.tile([P, P], F32, name="ident")
+        one = keep.tile([P, 1], F32, name="one")
+        warm = keep.tile([P, 1], F32, name="warm")
+        junk = keep.tile([P, D], BF16, name="junk")
+        wsc = keep.tile([P, G, PACK], F32, name="wsc")
+        cos_t = keep.tile([P, MT, HALF], BF16, name="cos_t")
+        sin_t = keep.tile([P, MT, HALF], BF16, name="sin_t")
+        nsin_t = keep.tile([P, MT, HALF], BF16, name="nsin_t")
+        wq_bytes_t = [keep.tile([P, G, PACK, NC], U8, name="wq_bytes_t%d" % c) for c in range(CH)]
+        x_sb = [keep.tile([P, DIM], BF16, name="x_sb%d" % m) for m in range(MT)]
+        x_codes = [keep.tile([P, G * P], U32, name="x_codes%d" % m, align_bytes=64) for m in range(MT)]
+        x_scales = [keep.tile([P, G * P], U8, name="x_scales%d" % m, align_bytes=64) for m in range(MT)]
+        wq_codes = [keep.tile([P, G, NC], U32, name="wq_codes%d" % c, align_bytes=64) for c in range(CH)]
+        wq_scales = [keep.tile([P, G, NC], U8, name="wq_scales%d" % c, align_bytes=64) for c in range(CH)]
+        wk_raw = keep.tile([P, G, PACK, D], BF16, name="wk_raw")
+        wv_raw = keep.tile([P, G, PACK, D], BF16, name="wv_raw")
+        kv_int = keep.tile([P, G, 2 * D, PACK], BF16, name="kv_int", align_bytes=64)
+        kv_codes = keep.tile([P, G, 2 * D], U32, name="kv_codes", align_bytes=64)
+        kv_scales = keep.tile([P, G, 2 * D], U8, name="kv_scales", align_bytes=64)
+
+        make_identity(nc, ident[:])
+        nc.vector.memset(one[:], 1.0)
+        nc.scalar.activation(out=warm[:], in_=one[:], func=ACT.Abs_reciprocal_sqrt)
+
+        def load_wq(u):
+            c, g = divmod(u, G)
+            nc.sync.dma_start(out=wq_bytes_t[c][:, g, :, :], in_=wqb_v[g][:, :, c * NC:(c + 1) * NC])
+
+        def load_x(m):
+            nc.sync.dma_start(out=x_sb[m][:], in_=x_v[m])
+
+        nc.sync.dma_start(out=wsc[:], in_=wqs_v)
+        load_wq(0)
+        load_wq(1)
+        load_x(0)
+        load_wq(2)
+        load_x(1)
+        load_x(2)
+        load_wq(3)
+        load_x(3)
+        load_wq(4)
+        nc.sync.dma_start(out=wk_raw[:].rearrange("p g t n -> p g (t n)"), in_=wk_v)
+        nc.sync.dma_start(out=wv_raw[:].rearrange("p g t n -> p g (t n)"), in_=wv_v)
+        load_wq(5)
+        nc.sync.dma_start(out=cos_t[:], in_=cos_v)
+        nc.sync.dma_start(out=sin_t[:], in_=sin_v)
+        for u in range(6, UNITS):
+            load_wq(u)
+
+        xt = {}
+        xg = {}
+
+        def x_transpose(m):
+            words = x_sb[m][:].bitcast(F32)
+            for a in range(2):
+                xt[(m, a)] = psum.tile([P, 2, 2, P], F32, name="bank", tag="bank")
+                for gg in range(2):
+                    g = 2 * a + gg
+                    for w in range(2):
+                        nc.tensor.transpose(
+                            out=xt[(m, a)][:, gg, w, :],
+                            in_=words[:, 256 * g + w:256 * (g + 1):2],
+                            identity=ident[:],
+                        )
+
+        def x_copy(m, a, eng):
+            if a == 0:
+                xg[m] = xg_pool.tile([P, DIM], BF16, name="xg", tag="xg", align_bytes=64)
+            dst = xg[m][:].bitcast(F32).rearrange("p (g r w) -> p g r w", g=G, w=2)[:, 2 * a:2 * a + 2, :, :]
+            src = xt[(m, a)][:].rearrange("p g w r -> p g r w")
+            if eng == "S":
+                nc.scalar.copy(out=dst, in_=src)
+            else:
+                nc.vector.tensor_copy(out=dst, in_=src)
+
+        def x_quant(m):
+            nc.vector.quantize_mx(out=x_codes[m][:].bitcast(FP8X4), scales=x_scales[m][:], in_=xg[m][:])
+
+        wd = {}
+        wi = {}
+
+        def widen(u, eng):
+            c, g = divmod(u, G)
+            if u not in wd:
+                wd[u] = wd_pool.tile([P, PACK, NC], BF16, name="wd", tag="wd")
+            for t in range(PACK):
+                on_v = t >= PACK - VW[u]
+                src = wq_bytes_t[c][:, g, t, :].bitcast(FP8)
+                if eng == "S" and not on_v:
+                    nc.scalar.activation(out=wd[u][:, t, :], in_=src, func=ACT.Copy, scale=wsc[:, g, t:t + 1])
+                if eng == "V" and on_v:
+                    nc.vector.tensor_scalar(out=wd[u][:, t, :], in0=src, scalar1=wsc[:, g, t:t + 1], scalar2=None, op0=ALU.mult)
+
+        def interleave(u):
+            wi[u] = wi_pool.tile([P, NC * PACK], BF16, name="wi", tag="wi", align_bytes=64)
+            nc.vector.tensor_copy(
+                out=wi[u][:].rearrange("p (n t) -> p n t", t=PACK),
+                in_=wd[u][:].rearrange("p t n -> p n t"),
+            )
+
+        def quant(u):
+            c, g = divmod(u, G)
+            nc.vector.quantize_mx(out=wq_codes[c][:, g, :].bitcast(FP8X4), scales=wq_scales[c][:, g, :], in_=wi[u][:])
+
+        def kv_interleave(i):
+            raw = wk_raw if i == 0 else wv_raw
+            nc.vector.tensor_copy(out=kv_int[:, :, i * D:(i + 1) * D, :], in_=raw[:].rearrange("p g t n -> p g n t"))
+
+        def kv_quant():
+            nc.vector.quantize_mx(
+                out=kv_codes[:].rearrange("p g n -> p (g n)").bitcast(FP8X4),
+                scales=kv_scales[:].rearrange("p g n -> p (g n)"),
+                in_=kv_int[:].rearrange("p g n t -> p (g n t)"),
+            )
+
+        banks = [("q", 0, m) for m in range(MT)] + [("kv", 0, 0), ("kv", 1, 0)]
+        for c in range(1, CH):
+            banks += [("q", c, m) for m in range(MT)]
+        bank_t = {}
+
+        def mm(out, m, g, rhs, rhs_scale):
+            nc.tensor.matmul_mx(
+                out=out,
+                lhsT=x_codes[m][:, g * P:(g + 1) * P].bitcast(FP8X4),
+                lhsT_scale=x_scales[m][:, g * P:(g + 1) * P],
+                rhs=rhs.bitcast(FP8X4),
+                rhs_scale=rhs_scale,
+                start=(g == 0),
+                stop=(g == G - 1),
+            )
+
+        def fill(i):
+            kind, c, m = banks[i]
+            bank_t[i] = psum.tile([P, NC], F32, name="bank", tag="bank")
+            if kind == "q":
+                for g in range(G):
+                    mm(bank_t[i][:], m, g, wq_codes[c][:, g, :], wq_scales[c][:, g, :])
+            else:
+                for mmi in range(2):
+                    for g in range(G):
+                        mm(bank_t[i][:, mmi * 2 * D:(mmi + 1) * 2 * D], 2 * c + mmi, g, kv_codes[:, g, :], kv_scales[:, g, :])
+
+        a_t = {}
+        b_t = {}
+
+        def rope_mults(i):
+            kind, c, m = banks[i]
+            if kind == "q":
+                nh = NC // D
+                pv = bank_t[i][:].rearrange("p (h w j) -> p h w j", w=2, j=HALF)
+                cb = cos_t[:, m, :].unsqueeze(1).unsqueeze(1).to_broadcast([P, nh, 2, HALF])
+                sb = sin_t[:, m, :].unsqueeze(1).to_broadcast([P, nh, HALF])
+                nb = nsin_t[:, m, :].unsqueeze(1).to_broadcast([P, nh, HALF])
+            else:
+                nh = 2
+                pv = bank_t[i][:].rearrange("p (h e w j) -> p h e w j", e=2, w=2, j=HALF)[:, :, 0, :, :]
+                cb = cos_t[:, 2 * c:2 * c + 2, :].unsqueeze(2).to_broadcast([P, nh, 2, HALF])
+                sb = sin_t[:, 2 * c:2 * c + 2, :]
+                nb = nsin_t[:, 2 * c:2 * c + 2, :]
+            a_t[i] = a_pool.tile([P, NC], F32, name="a", tag="a")
+            b_t[i] = b_pool.tile([P, NC], F32, name="b", tag="b")
+            av = a_t[i][:, 0:nh * D].rearrange("p (h w j) -> p h w j", w=2, j=HALF)
+            bv = b_t[i][:, 0:nh * D].rearrange("p (h w j) -> p h w j", w=2, j=HALF)
+            nc.vector.tensor_tensor(out=av, in0=pv, in1=cb, op=ALU.mult)
+            nc.vector.tensor_tensor(out=bv[:, :, 0, :], in0=pv[:, :, 1, :], in1=sb, op=ALU.mult)
+            nc.vector.tensor_tensor(out=bv[:, :, 1, :], in0=pv[:, :, 0, :], in1=nb, op=ALU.mult)
+
+        def rope_add(i):
+            nh = NC // D if banks[i][0] == "q" else 2
+            eng = nc.gpsimd if i >= ADD_G_FROM else nc.vector
+            eng.tensor_tensor(out=a_t[i][:, 0:nh * D], in0=a_t[i][:, 0:nh * D], in1=b_t[i][:, 0:nh * D], op=ALU.add)
+
+        ss_t = {}
+        rs_t = {}
+        v_t = {}
+
+        def v_copy(i):
+            c = banks[i][1]
+            v_t[i] = st_pool.tile([P, 2, D], F32, name="vt", tag="vt")
+            nc.scalar.copy(out=v_t[i][:], in_=bank_t[i][:].rearrange("p (h e d) -> p h e d", e=2, d=D)[:, :, 1, :])
+            nc.sync.dma_start(out=o2_v[:, 2 * c:2 * c + 2, :], in_=v_t[i][:])
+
+        def squares(i):
+            nh = NC // D if banks[i][0] == "q" else 2
+            ss_t[i] = st_pool.tile([P, 4], F32, name="ss", tag="ss")
+            rs_t[i] = st_pool.tile([P, 4], F32, name="rs", tag="rs")
+            for h in range(nh):
+                nc.scalar.activation(out=junk[:], in_=a_t[i][:, h * D:(h + 1) * D], func=ACT.Square, accum_out=ss_t[i][:, h:h + 1])
+
+        def rsqrt(i):
+            nh = NC // D if banks[i][0] == "q" else 2
+            nc.scalar.activation(out=rs_t[i][:, 0:nh], in_=ss_t[i][:, 0:nh], func=ACT.Abs_reciprocal_sqrt, scale=1.0 / D, bias=EPS)
+
+        def scale_store(i):
+            kind, c, m = banks[i]
+            nh = NC // D if kind == "q" else 2
+            for h in range(nh):
+                nc.scalar.activation(out=a_t[i][:, h * D:(h + 1) * D], in_=a_t[i][:, h * D:(h + 1) * D], func=ACT.Copy, scale=rs_t[i][:, h:h + 1])
+            if kind == "q":
+                nc.sync.dma_start(out=o0_v[m][:, c * NC:(c + 1) * NC], in_=a_t[i][:])
+            else:
+                nc.sync.dma_start(out=o1_v[:, 2 * c:2 * c + 2, :], in_=a_t[i][:, 0:2 * D].rearrange("p (h d) -> p h d", d=D))
+
+        pend = []
+
+        def s_epilogue(i):
+            if pend:
+                rsqrt(pend[0])
+            if i is not None:
+                if banks[i][0] == "kv":
+                    v_copy(i)
+                squares(i)
+            if pend:
+                scale_store(pend[0])
+                pend.clear()
+            if i is not None:
+                pend.append(i)
+
+        NB = len(banks)
+        r_slot = {0: 8, 1: 9, 2: 10, 3: 11, 4: 12, 5: 12, 6: 13, 7: 14, 8: 15, 9: 16}
+        for i in range(10, NB):
+            r_slot[i] = 17 + (i - 10)
+        fill_slot = {0: 6, 1: 6, 2: 6, 3: 6, 4: 8, 5: 8, 6: 9, 7: 9, 8: 9, 9: 10, 10: 13, 11: 13, 12: 13, 13: 13, 14: 17, 15: 17, 16: 17, 17: 17}
+        last_slot = r_slot[NB - 1] + 2
+
+        for m in range(MT):
+            x_transpose(m)
+
+        for s in range(last_slot + 1):
+            if s < UNITS:
+                widen(s, "S")
+                widen(s, "V")
+            if 1 <= s <= MT:
+                x_copy(s - 1, 0, "S")
+                x_copy(s - 1, 1, "V")
+            if s > UNITS and s - 2 < UNITS:
+                quant(s - 2)
+            rs_here = [i for i in range(NB) if r_slot[i] == s]
+            for i in rs_here:
+                rope_mults(i)
+            if 1 <= s <= UNITS:
+                interleave(s - 1)
+            for i in rs_here:
+                rope_add(i)
+            if 2 <= s <= UNITS:
+                quant(s - 2)
+            if 2 <= s <= MT + 1:
+                x_quant(s - 2)
+            if s == 6:
+                kv_interleave(0)
+                nc.vector.tensor_scalar(out=nsin_t[:], in0=sin_t[:], scalar1=-1.0, scalar2=None, op0=ALU.mult)
+            if s == 7:
+                kv_interleave(1)
+            if s == 8:
+                kv_quant()
+            for i in range(NB):
+                if r_slot[i] + 1 == s:
+                    s_epilogue(i)
+            for i in range(NB):
+                if fill_slot[i] == s:
+                    fill(i)
+        s_epilogue(None)

@@ -12,34 +12,54 @@ FP8X4 = mybir.dt.float8_e4m3fn_x4
 ACT = mybir.ActivationFunctionType
 ALU = mybir.AluOpType
 
-L, DIM, H, D = 512, 2048, 16, 128
+TOKENS, DIM, HEADS, D = 512, 2048, 16, 128
 HALF = D // 2
 EPS = 1e-6
 P = 128
 PACK = 4
-G = DIM // (P * PACK)
-MT = L // P
-NC = 512
-CH = (H * D) // NC
-UNITS = CH * G
+PASSES = DIM // (P * PACK)
+TOKEN_TILES = TOKENS // P
+BANK = 512
+UNIT_COLS = 1024
+UNIT_CHUNKS = (HEADS * D) // UNIT_COLS
+UNITS = UNIT_CHUNKS * PASSES
+BANKS_PER_UNIT_CHUNK = UNIT_COLS // BANK
+PSUM_BANKS = 8
 
-FLOPS = 2 * L * DIM * (H * D + 2 * D)
+FLOPS = 2 * TOKENS * DIM * (HEADS * D + 2 * D)
 
-VW = [2, 0, 0, 0, 0, 0, 0, 0, 0, 0, 0, 0, 0, 0, 0, 0]
-ADD_G_FROM = 10
+VECTOR_WIDENS = {0: 3, 2: 4, 6: 1, 7: 2}
+SCALAR_INTERLEAVES = (5, 7)
+X_COPY_AFTER_PLANE = (8, 14, 17, 23)
+X_QUANT_SLOT = (1, 2, 3, 5)
+KV_INTERLEAVE_SLOT = (2, 4)
+KV_QUANT_SLOT = 4
+ROPE_SLOT = {3: (0, 1), 5: (2,), 6: (3, 4, 5)}
+NORM_AFTER_PLANE = {27: (0, 1)}
+VECTOR_ADDS = (1, 5)
+LOADS = (("wsc",), ("wqp", 0, 0), ("wqp", 0, 1), ("wqp", 0, 2), ("wqp", 0, 3), ("wq", 1), ("wq", 2), ("x", 0), ("wq", 3), ("x", 1), ("x", 2), ("wq", 4), ("wk",), ("x", 3), ("wq", 5), ("wv",), ("cs",), ("wq", 6), ("wq", 7))
+WD_BUFS, WI_BUFS, A_BUFS, B_BUFS = 4, 3, 8, 3
+FAST_INTERLEAVE = True
+VECTOR_SCALES = {}
+VECTOR_SCALES_DEFAULT = 0
+FINISH_LAG = 3
+V_COPY_ON_VECTOR = True
 
 
 def tile_multiqueryattention_pa_kernel(tc, x, cos, sin, Wq_bytes, Wq_scale, Wk, Wv, out_0, out_1, out_2):
     nc = tc.nc
+    q_banks = [("q", c, m) for c in range(HEADS * D // BANK) for m in range(TOKEN_TILES)]
+    banks = q_banks + [("kv", i, 0) for i in range(TOKEN_TILES // 2)]
+    n_banks = len(banks)
+
     with ExitStack() as ctx:
         keep = ctx.enter_context(tc.tile_pool(name="keep", bufs=1))
-        wd_pool = ctx.enter_context(tc.tile_pool(name="wdp", bufs=6))
-        wi_pool = ctx.enter_context(tc.tile_pool(name="wip", bufs=4))
-        xg_pool = ctx.enter_context(tc.tile_pool(name="xgp", bufs=2))
-        a_pool = ctx.enter_context(tc.tile_pool(name="ap", bufs=6))
-        b_pool = ctx.enter_context(tc.tile_pool(name="bp", bufs=3))
-        st_pool = ctx.enter_context(tc.tile_pool(name="stp", bufs=4))
-        psum = ctx.enter_context(tc.psum_pool(name="psum", bufs=8))
+        wd_pool = ctx.enter_context(tc.tile_pool(name="wdp", bufs=WD_BUFS))
+        wi_pool = ctx.enter_context(tc.tile_pool(name="wip", bufs=WI_BUFS))
+        a_pool = ctx.enter_context(tc.tile_pool(name="ap", bufs=A_BUFS))
+        b_pool = ctx.enter_context(tc.tile_pool(name="bp", bufs=B_BUFS))
+        st_pool = ctx.enter_context(tc.tile_pool(name="stp", bufs=A_BUFS))
+        psum = ctx.enter_context(tc.psum_pool(name="psum", bufs=PSUM_BANKS))
         ctx.enter_context(tc.manual_schedule())
 
         x_v = x[0].rearrange("(m p) k -> m p k", p=P)
@@ -57,53 +77,58 @@ def tile_multiqueryattention_pa_kernel(tc, x, cos, sin, Wq_bytes, Wq_scale, Wk, 
         one = keep.tile([P, 1], F32, name="one")
         warm = keep.tile([P, 1], F32, name="warm")
         junk = keep.tile([P, D], BF16, name="junk")
-        wsc = keep.tile([P, G, PACK], F32, name="wsc")
-        cos_t = keep.tile([P, MT, HALF], BF16, name="cos_t")
-        sin_t = keep.tile([P, MT, HALF], BF16, name="sin_t")
-        nsin_t = keep.tile([P, MT, HALF], BF16, name="nsin_t")
-        wq_bytes_t = [keep.tile([P, G, PACK, NC], U8, name="wq_bytes_t%d" % c) for c in range(CH)]
-        x_sb = [keep.tile([P, DIM], BF16, name="x_sb%d" % m) for m in range(MT)]
-        x_codes = [keep.tile([P, G * P], U32, name="x_codes%d" % m, align_bytes=64) for m in range(MT)]
-        x_scales = [keep.tile([P, G * P], U8, name="x_scales%d" % m, align_bytes=64) for m in range(MT)]
-        wq_codes = [keep.tile([P, G, NC], U32, name="wq_codes%d" % c, align_bytes=64) for c in range(CH)]
-        wq_scales = [keep.tile([P, G, NC], U8, name="wq_scales%d" % c, align_bytes=64) for c in range(CH)]
-        wk_raw = keep.tile([P, G, PACK, D], BF16, name="wk_raw")
-        wv_raw = keep.tile([P, G, PACK, D], BF16, name="wv_raw")
-        kv_int = keep.tile([P, G, 2 * D, PACK], BF16, name="kv_int", align_bytes=64)
-        kv_codes = keep.tile([P, G, 2 * D], U32, name="kv_codes", align_bytes=64)
-        kv_scales = keep.tile([P, G, 2 * D], U8, name="kv_scales", align_bytes=64)
+        vjunk = keep.tile([P, 1], F32, name="vjunk")
+        wsc = keep.tile([P, PASSES, PACK], F32, name="wsc")
+        cos_t = keep.tile([P, TOKEN_TILES, HALF], BF16, name="cos_t")
+        sn_t = keep.tile([P, TOKEN_TILES, 2, HALF], BF16, name="sn_t")
+        wq_bytes_t = [keep.tile([P, PASSES, PACK, UNIT_COLS], U8, name="wq_bytes_t%d" % c) for c in range(UNIT_CHUNKS)]
+        x_sb = [keep.tile([P, DIM], BF16, name="x_sb%d" % m) for m in range(TOKEN_TILES)]
+        x_int = [keep.tile([P, DIM], BF16, name="x_int%d" % m, align_bytes=64) for m in range(TOKEN_TILES)]
+        x_codes = [keep.tile([P, PASSES * P], U32, name="x_codes%d" % m, align_bytes=64) for m in range(TOKEN_TILES)]
+        x_scales = [keep.tile([P, PASSES * P], U8, name="x_scales%d" % m, align_bytes=64) for m in range(TOKEN_TILES)]
+        wq_codes = [keep.tile([P, PASSES, UNIT_COLS], U32, name="wq_codes%d" % c, align_bytes=64) for c in range(UNIT_CHUNKS)]
+        wq_scales = [keep.tile([P, PASSES, UNIT_COLS], U8, name="wq_scales%d" % c, align_bytes=64) for c in range(UNIT_CHUNKS)]
+        wk_raw = keep.tile([P, PASSES, PACK, D], BF16, name="wk_raw")
+        wv_raw = keep.tile([P, PASSES, PACK, D], BF16, name="wv_raw")
+        kv_int = keep.tile([P, PASSES, 2 * D, PACK], BF16, name="kv_int", align_bytes=64)
+        kv_codes = keep.tile([P, PASSES, 2 * D], U32, name="kv_codes", align_bytes=64)
+        kv_scales = keep.tile([P, PASSES, 2 * D], U8, name="kv_scales", align_bytes=64)
 
         make_identity(nc, ident[:])
         nc.vector.memset(one[:], 1.0)
         nc.scalar.activation(out=warm[:], in_=one[:], func=ACT.Abs_reciprocal_sqrt)
 
-        def load_wq(u):
-            c, g = divmod(u, G)
-            nc.sync.dma_start(out=wq_bytes_t[c][:, g, :, :], in_=wqb_v[g][:, :, c * NC:(c + 1) * NC])
+        for ld in LOADS:
+            if ld[0] == "wsc":
+                nc.sync.dma_start(out=wsc[:], in_=wqs_v)
+            elif ld[0] == "wq":
+                c, g = divmod(ld[1], PASSES)
+                nc.sync.dma_start(out=wq_bytes_t[c][:, g, :, :], in_=wqb_v[g][:, :, c * UNIT_COLS:(c + 1) * UNIT_COLS])
+            elif ld[0] == "wqp":
+                c, g = divmod(ld[1], PASSES)
+                nc.sync.dma_start(out=wq_bytes_t[c][:, g, ld[2], :], in_=wqb_v[g][:, ld[2], c * UNIT_COLS:(c + 1) * UNIT_COLS])
+            elif ld[0] == "x":
+                nc.sync.dma_start(out=x_sb[ld[1]][:], in_=x_v[ld[1]])
+            elif ld[0] == "wk":
+                nc.sync.dma_start(out=wk_raw[:].rearrange("p g t n -> p g (t n)"), in_=wk_v)
+            elif ld[0] == "wv":
+                nc.sync.dma_start(out=wv_raw[:].rearrange("p g t n -> p g (t n)"), in_=wv_v)
+            elif ld[0] == "cs":
+                nc.sync.dma_start(out=cos_t[:], in_=cos_v)
+                nc.sync.dma_start(out=sn_t[:, :, 0, :], in_=sin_v)
 
-        def load_x(m):
-            nc.sync.dma_start(out=x_sb[m][:], in_=x_v[m])
-
-        nc.sync.dma_start(out=wsc[:], in_=wqs_v)
-        load_wq(0)
-        load_wq(1)
-        load_x(0)
-        load_wq(2)
-        load_x(1)
-        load_x(2)
-        load_wq(3)
-        load_x(3)
-        load_wq(4)
-        nc.sync.dma_start(out=wk_raw[:].rearrange("p g t n -> p g (t n)"), in_=wk_v)
-        nc.sync.dma_start(out=wv_raw[:].rearrange("p g t n -> p g (t n)"), in_=wv_v)
-        load_wq(5)
-        nc.sync.dma_start(out=cos_t[:], in_=cos_v)
-        nc.sync.dma_start(out=sin_t[:], in_=sin_v)
-        for u in range(6, UNITS):
-            load_wq(u)
+        x_quantised = set()
+        units_quantised = set()
+        kv_quantised = set()
+        x_copied = set()
+        read_out = set()
+        filled = set()
+        roped = set()
+        normed = set()
+        scaled = set()
+        finished = set()
 
         xt = {}
-        xg = {}
 
         def x_transpose(m):
             words = x_sb[m][:].bitcast(F32)
@@ -112,50 +137,48 @@ def tile_multiqueryattention_pa_kernel(tc, x, cos, sin, Wq_bytes, Wq_scale, Wk, 
                 for gg in range(2):
                     g = 2 * a + gg
                     for w in range(2):
-                        nc.tensor.transpose(
-                            out=xt[(m, a)][:, gg, w, :],
-                            in_=words[:, 256 * g + w:256 * (g + 1):2],
-                            identity=ident[:],
-                        )
+                        nc.tensor.transpose(out=xt[(m, a)][:, gg, w, :], in_=words[:, 256 * g + w:256 * (g + 1):2], identity=ident[:])
 
-        def x_copy(m, a, eng):
-            if a == 0:
-                xg[m] = xg_pool.tile([P, DIM], BF16, name="xg", tag="xg", align_bytes=64)
-            dst = xg[m][:].bitcast(F32).rearrange("p (g r w) -> p g r w", g=G, w=2)[:, 2 * a:2 * a + 2, :, :]
-            src = xt[(m, a)][:].rearrange("p g w r -> p g r w")
+        def x_copy(m):
+            for a in range(2):
+                dst = x_int[m][:].bitcast(F32).rearrange("p (g r w) -> p g r w", g=PASSES, w=2)[:, 2 * a:2 * a + 2, :, :]
+                nc.scalar.copy(out=dst, in_=xt[(m, a)][:].rearrange("p g w r -> p g r w"))
+                x_copied.add(2 * m + a)
+
+        def x_quant(m):
+            nc.vector.quantize_mx(out=x_codes[m][:].bitcast(FP8X4), scales=x_scales[m][:], in_=x_int[m][:])
+            x_quantised.add(m)
+
+        wd = {}
+        wi = {}
+
+        def widen(u, t, eng):
+            c, g = divmod(u, PASSES)
+            if u not in wd:
+                wd[u] = wd_pool.tile([P, PACK, UNIT_COLS], BF16, name="wd", tag="wd")
+            src = wq_bytes_t[c][:, g, t, :].bitcast(FP8)
+            if eng == "S":
+                nc.scalar.activation(out=wd[u][:, t, :], in_=src, func=ACT.Copy, scale=wsc[:, g, t:t + 1])
+            else:
+                nc.vector.tensor_scalar(out=wd[u][:, t, :], in0=src, scalar1=wsc[:, g, t:t + 1], scalar2=None, op0=ALU.mult)
+
+        def interleave(u, eng):
+            wi[u] = wi_pool.tile([P, UNIT_COLS * PACK], BF16, name="wi", tag="wi", align_bytes=64)
+            if FAST_INTERLEAVE:
+                dst = wi[u][:].rearrange("p (c i t) -> p c t i", i=4, t=PACK)
+                src = wd[u][:].rearrange("p t (c i) -> p c t i", i=4)
+            else:
+                dst = wi[u][:].rearrange("p (n t) -> p n t", t=PACK)
+                src = wd[u][:].rearrange("p t n -> p n t")
             if eng == "S":
                 nc.scalar.copy(out=dst, in_=src)
             else:
                 nc.vector.tensor_copy(out=dst, in_=src)
 
-        def x_quant(m):
-            nc.vector.quantize_mx(out=x_codes[m][:].bitcast(FP8X4), scales=x_scales[m][:], in_=xg[m][:])
-
-        wd = {}
-        wi = {}
-
-        def widen(u, eng):
-            c, g = divmod(u, G)
-            if u not in wd:
-                wd[u] = wd_pool.tile([P, PACK, NC], BF16, name="wd", tag="wd")
-            for t in range(PACK):
-                on_v = t >= PACK - VW[u]
-                src = wq_bytes_t[c][:, g, t, :].bitcast(FP8)
-                if eng == "S" and not on_v:
-                    nc.scalar.activation(out=wd[u][:, t, :], in_=src, func=ACT.Copy, scale=wsc[:, g, t:t + 1])
-                if eng == "V" and on_v:
-                    nc.vector.tensor_scalar(out=wd[u][:, t, :], in0=src, scalar1=wsc[:, g, t:t + 1], scalar2=None, op0=ALU.mult)
-
-        def interleave(u):
-            wi[u] = wi_pool.tile([P, NC * PACK], BF16, name="wi", tag="wi", align_bytes=64)
-            nc.vector.tensor_copy(
-                out=wi[u][:].rearrange("p (n t) -> p n t", t=PACK),
-                in_=wd[u][:].rearrange("p t n -> p n t"),
-            )
-
         def quant(u):
-            c, g = divmod(u, G)
+            c, g = divmod(u, PASSES)
             nc.vector.quantize_mx(out=wq_codes[c][:, g, :].bitcast(FP8X4), scales=wq_scales[c][:, g, :], in_=wi[u][:])
+            units_quantised.add(u)
 
         def kv_interleave(i):
             raw = wk_raw if i == 0 else wv_raw
@@ -167,10 +190,8 @@ def tile_multiqueryattention_pa_kernel(tc, x, cos, sin, Wq_bytes, Wq_scale, Wk, 
                 scales=kv_scales[:].rearrange("p g n -> p (g n)"),
                 in_=kv_int[:].rearrange("p g n t -> p (g n t)"),
             )
+            kv_quantised.add(0)
 
-        banks = [("q", 0, m) for m in range(MT)] + [("kv", 0, 0), ("kv", 1, 0)]
-        for c in range(1, CH):
-            banks += [("q", c, m) for m in range(MT)]
         bank_t = {}
 
         def mm(out, m, g, rhs, rhs_scale):
@@ -181,137 +202,190 @@ def tile_multiqueryattention_pa_kernel(tc, x, cos, sin, Wq_bytes, Wq_scale, Wk, 
                 rhs=rhs.bitcast(FP8X4),
                 rhs_scale=rhs_scale,
                 start=(g == 0),
-                stop=(g == G - 1),
+                stop=(g == PASSES - 1),
             )
+
+        def can_fill(i):
+            kind, c, m = banks[i]
+            free = (i in x_copied) if i < PSUM_BANKS else (i - PSUM_BANKS in read_out)
+            if kind == "q":
+                uc = c // BANKS_PER_UNIT_CHUNK
+                ready = m in x_quantised and all(uc * PASSES + g in units_quantised for g in range(PASSES))
+            else:
+                ready = 0 in kv_quantised and 2 * c in x_quantised and 2 * c + 1 in x_quantised
+            return free and ready
 
         def fill(i):
             kind, c, m = banks[i]
-            bank_t[i] = psum.tile([P, NC], F32, name="bank", tag="bank")
+            bank_t[i] = psum.tile([P, BANK], F32, name="bank", tag="bank")
             if kind == "q":
-                for g in range(G):
-                    mm(bank_t[i][:], m, g, wq_codes[c][:, g, :], wq_scales[c][:, g, :])
+                uc, cc = divmod(c, BANKS_PER_UNIT_CHUNK)
+                cols = slice(cc * BANK, (cc + 1) * BANK)
+                for g in range(PASSES):
+                    mm(bank_t[i][:], m, g, wq_codes[uc][:, g, cols], wq_scales[uc][:, g, cols])
             else:
                 for mmi in range(2):
-                    for g in range(G):
+                    for g in range(PASSES):
                         mm(bank_t[i][:, mmi * 2 * D:(mmi + 1) * 2 * D], 2 * c + mmi, g, kv_codes[:, g, :], kv_scales[:, g, :])
+            filled.add(i)
+
+        def fill_ready():
+            for i in range(n_banks):
+                if i not in filled and (i == 0 or i - 1 in filled) and can_fill(i):
+                    fill(i)
 
         a_t = {}
         b_t = {}
+        v_t = {}
+
+        def heads_of(i):
+            return BANK // D if banks[i][0] == "q" else 2
 
         def rope_mults(i):
             kind, c, m = banks[i]
+            nh = heads_of(i)
+            if not roped:
+                nc.vector.tensor_scalar(out=sn_t[:, :, 1, :], in0=sn_t[:, :, 0, :], scalar1=-1.0, scalar2=None, op0=ALU.mult)
             if kind == "q":
-                nh = NC // D
                 pv = bank_t[i][:].rearrange("p (h w j) -> p h w j", w=2, j=HALF)
                 cb = cos_t[:, m, :].unsqueeze(1).unsqueeze(1).to_broadcast([P, nh, 2, HALF])
-                sb = sin_t[:, m, :].unsqueeze(1).to_broadcast([P, nh, HALF])
-                nb = nsin_t[:, m, :].unsqueeze(1).to_broadcast([P, nh, HALF])
+                sb = sn_t[:, m, :, :].unsqueeze(1).to_broadcast([P, nh, 2, HALF])
             else:
-                nh = 2
                 pv = bank_t[i][:].rearrange("p (h e w j) -> p h e w j", e=2, w=2, j=HALF)[:, :, 0, :, :]
                 cb = cos_t[:, 2 * c:2 * c + 2, :].unsqueeze(2).to_broadcast([P, nh, 2, HALF])
-                sb = sin_t[:, 2 * c:2 * c + 2, :]
-                nb = nsin_t[:, 2 * c:2 * c + 2, :]
-            a_t[i] = a_pool.tile([P, NC], F32, name="a", tag="a")
-            b_t[i] = b_pool.tile([P, NC], F32, name="b", tag="b")
+                sb = sn_t[:, 2 * c:2 * c + 2, :, :]
+            a_t[i] = a_pool.tile([P, BANK], F32, name="a", tag="a")
+            b_t[i] = b_pool.tile([P, BANK], F32, name="b", tag="b")
             av = a_t[i][:, 0:nh * D].rearrange("p (h w j) -> p h w j", w=2, j=HALF)
             bv = b_t[i][:, 0:nh * D].rearrange("p (h w j) -> p h w j", w=2, j=HALF)
             nc.vector.tensor_tensor(out=av, in0=pv, in1=cb, op=ALU.mult)
-            nc.vector.tensor_tensor(out=bv[:, :, 0, :], in0=pv[:, :, 1, :], in1=sb, op=ALU.mult)
-            nc.vector.tensor_tensor(out=bv[:, :, 1, :], in0=pv[:, :, 0, :], in1=nb, op=ALU.mult)
+            nc.vector.tensor_tensor(out=bv, in0=pv[:, :, ::-1, :], in1=sb, op=ALU.mult)
+            roped.add(i)
+            if kind == "q":
+                read_out.add(i)
+            elif V_COPY_ON_VECTOR:
+                v_copy(i)
 
         def rope_add(i):
-            nh = NC // D if banks[i][0] == "q" else 2
-            eng = nc.gpsimd if i >= ADD_G_FROM else nc.vector
-            eng.tensor_tensor(out=a_t[i][:, 0:nh * D], in0=a_t[i][:, 0:nh * D], in1=b_t[i][:, 0:nh * D], op=ALU.add)
-
-        ss_t = {}
-        rs_t = {}
-        v_t = {}
+            w = heads_of(i) * D
+            eng = nc.vector if i in VECTOR_ADDS else nc.gpsimd
+            eng.tensor_tensor(out=a_t[i][:, 0:w], in0=a_t[i][:, 0:w], in1=b_t[i][:, 0:w], op=ALU.add)
 
         def v_copy(i):
             c = banks[i][1]
             v_t[i] = st_pool.tile([P, 2, D], F32, name="vt", tag="vt")
-            nc.scalar.copy(out=v_t[i][:], in_=bank_t[i][:].rearrange("p (h e d) -> p h e d", e=2, d=D)[:, :, 1, :])
+            src = bank_t[i][:].rearrange("p (h e d) -> p h e d", e=2, d=D)[:, :, 1, :]
+            if V_COPY_ON_VECTOR:
+                nc.vector.tensor_copy(out=v_t[i][:], in_=src)
+            else:
+                nc.scalar.copy(out=v_t[i][:], in_=src)
             nc.sync.dma_start(out=o2_v[:, 2 * c:2 * c + 2, :], in_=v_t[i][:])
+            read_out.add(i)
+
+        ss_t = {}
+        rs_t = {}
 
         def squares(i):
-            nh = NC // D if banks[i][0] == "q" else 2
             ss_t[i] = st_pool.tile([P, 4], F32, name="ss", tag="ss")
             rs_t[i] = st_pool.tile([P, 4], F32, name="rs", tag="rs")
-            for h in range(nh):
+            for h in range(heads_of(i)):
                 nc.scalar.activation(out=junk[:], in_=a_t[i][:, h * D:(h + 1) * D], func=ACT.Square, accum_out=ss_t[i][:, h:h + 1])
 
         def rsqrt(i):
-            nh = NC // D if banks[i][0] == "q" else 2
+            nh = heads_of(i)
             nc.scalar.activation(out=rs_t[i][:, 0:nh], in_=ss_t[i][:, 0:nh], func=ACT.Abs_reciprocal_sqrt, scale=1.0 / D, bias=EPS)
 
-        def scale_store(i):
-            kind, c, m = banks[i]
-            nh = NC // D if kind == "q" else 2
-            for h in range(nh):
+        def vector_heads(i):
+            return min(heads_of(i), VECTOR_SCALES.get(i, VECTOR_SCALES_DEFAULT))
+
+        def scalar_scale(i):
+            for h in range(heads_of(i) - vector_heads(i)):
                 nc.scalar.activation(out=a_t[i][:, h * D:(h + 1) * D], in_=a_t[i][:, h * D:(h + 1) * D], func=ACT.Copy, scale=rs_t[i][:, h:h + 1])
+            scaled.add(i)
+
+        def finish(i):
+            kind, c, m = banks[i]
+            for h in range(heads_of(i) - vector_heads(i), heads_of(i)):
+                nc.vector.tensor_scalar(out=a_t[i][:, h * D:(h + 1) * D], in0=a_t[i][:, h * D:(h + 1) * D], scalar1=rs_t[i][:, h:h + 1], scalar2=None, op0=ALU.mult, op1=ALU.add, accum_out=vjunk[:])
             if kind == "q":
-                nc.sync.dma_start(out=o0_v[m][:, c * NC:(c + 1) * NC], in_=a_t[i][:])
+                nc.sync.dma_start(out=o0_v[m][:, c * BANK:(c + 1) * BANK], in_=a_t[i][:])
             else:
                 nc.sync.dma_start(out=o1_v[:, 2 * c:2 * c + 2, :], in_=a_t[i][:, 0:2 * D].rearrange("p (h d) -> p h d", d=D))
+            finished.add(i)
 
-        pend = []
+        def finish_ready(upto):
+            for i in range(n_banks):
+                if i <= upto and i in scaled and i not in finished:
+                    finish(i)
 
-        def s_epilogue(i):
-            if pend:
-                rsqrt(pend[0])
+        waiting = []
+
+        def norm(i):
+            if waiting:
+                rsqrt(waiting[0])
             if i is not None:
-                if banks[i][0] == "kv":
+                if banks[i][0] == "kv" and not V_COPY_ON_VECTOR:
                     v_copy(i)
                 squares(i)
-            if pend:
-                scale_store(pend[0])
-                pend.clear()
+                normed.add(i)
+            if waiting:
+                scalar_scale(waiting[0])
+                waiting.clear()
             if i is not None:
-                pend.append(i)
+                waiting.append(i)
 
-        NB = len(banks)
-        r_slot = {0: 8, 1: 9, 2: 10, 3: 11, 4: 12, 5: 12, 6: 13, 7: 14, 8: 15, 9: 16}
-        for i in range(10, NB):
-            r_slot[i] = 17 + (i - 10)
-        fill_slot = {0: 6, 1: 6, 2: 6, 3: 6, 4: 8, 5: 8, 6: 9, 7: 9, 8: 9, 9: 10, 10: 13, 11: 13, 12: 13, 13: 13, 14: 17, 15: 17, 16: 17, 17: 17}
-        last_slot = r_slot[NB - 1] + 2
+        def on_vector(u, t):
+            return t >= PACK - VECTOR_WIDENS.get(u, 0)
 
-        for m in range(MT):
+        def vector_widens(u):
+            for t in range(PACK):
+                if u < UNITS and on_vector(u, t):
+                    widen(u, t, "V")
+
+        for m in range(TOKEN_TILES):
             x_transpose(m)
 
-        for s in range(last_slot + 1):
-            if s < UNITS:
-                widen(s, "S")
-                widen(s, "V")
-            if 1 <= s <= MT:
-                x_copy(s - 1, 0, "S")
-                x_copy(s - 1, 1, "V")
-            if s > UNITS and s - 2 < UNITS:
-                quant(s - 2)
-            rs_here = [i for i in range(NB) if r_slot[i] == s]
-            for i in rs_here:
+        for s in range(UNITS + 1):
+            for t in range(PACK):
+                if s < UNITS:
+                    if not on_vector(s, t):
+                        widen(s, t, "S")
+                    if t == PACK - 1 and s in SCALAR_INTERLEAVES:
+                        interleave(s, "S")
+                    for m in range(TOKEN_TILES):
+                        if X_COPY_AFTER_PLANE[m] == PACK * s + t:
+                            x_copy(m)
+                    for i in NORM_AFTER_PLANE.get(PACK * s + t, ()):
+                        norm(i)
+            if s == 0:
+                vector_widens(0)
+            vector_widens(s + 1)
+            if s < UNITS and s not in SCALAR_INTERLEAVES:
+                interleave(s, "V")
+            if s >= 1:
+                quant(s - 1)
+                for m in range(TOKEN_TILES):
+                    if X_QUANT_SLOT[m] == s - 1:
+                        x_quant(m)
+                for i in range(2):
+                    if KV_INTERLEAVE_SLOT[i] == s - 1:
+                        kv_interleave(i)
+                if KV_QUANT_SLOT == s - 1:
+                    kv_quant()
+                fill_ready()
+                for i in ROPE_SLOT.get(s - 1, ()):
+                    rope_mults(i)
+                for i in ROPE_SLOT.get(s - 1, ()):
+                    rope_add(i)
+            fill_ready()
+
+        for i in range(n_banks + 1):
+            if i < n_banks and i not in roped:
                 rope_mults(i)
-            if 1 <= s <= UNITS:
-                interleave(s - 1)
-            for i in rs_here:
                 rope_add(i)
-            if 2 <= s <= UNITS:
-                quant(s - 2)
-            if 2 <= s <= MT + 1:
-                x_quant(s - 2)
-            if s == 6:
-                kv_interleave(0)
-                nc.vector.tensor_scalar(out=nsin_t[:], in0=sin_t[:], scalar1=-1.0, scalar2=None, op0=ALU.mult)
-            if s == 7:
-                kv_interleave(1)
-            if s == 8:
-                kv_quant()
-            for i in range(NB):
-                if r_slot[i] + 1 == s:
-                    s_epilogue(i)
-            for i in range(NB):
-                if fill_slot[i] == s:
-                    fill(i)
-        s_epilogue(None)
+            finish_ready(i - FINISH_LAG)
+            if i >= 1 and i - 1 not in normed:
+                norm(i - 1)
+            fill_ready()
+        norm(None)
+        finish_ready(n_banks)

@@ -58,6 +58,7 @@ def tile_multiqueryattention_pa_kernel(tc, x, cos, sin, Wq_bytes, Wq_scale, Wk, 
         wi_pool = ctx.enter_context(tc.tile_pool(name="wip", bufs=WI_BUFS))
         a_pool = ctx.enter_context(tc.tile_pool(name="ap", bufs=A_BUFS))
         b_pool = ctx.enter_context(tc.tile_pool(name="bp", bufs=B_BUFS))
+        junk_pool = ctx.enter_context(tc.tile_pool(name="junkp", bufs=8))
         st_pool = ctx.enter_context(tc.tile_pool(name="stp", bufs=A_BUFS))
         psum = ctx.enter_context(tc.psum_pool(name="psum", bufs=PSUM_BANKS))
         ctx.enter_context(tc.manual_schedule())
@@ -76,7 +77,6 @@ def tile_multiqueryattention_pa_kernel(tc, x, cos, sin, Wq_bytes, Wq_scale, Wk, 
         ident = keep.tile([P, P], F32, name="ident")
         one = keep.tile([P, 1], F32, name="one")
         warm = keep.tile([P, 1], F32, name="warm")
-        junk = keep.tile([P, D], BF16, name="junk")
         vjunk = keep.tile([P, 1], F32, name="vjunk")
         wsc = keep.tile([P, PASSES, PACK], F32, name="wsc")
         cos_t = keep.tile([P, TOKEN_TILES, HALF], BF16, name="cos_t")
@@ -289,6 +289,7 @@ def tile_multiqueryattention_pa_kernel(tc, x, cos, sin, Wq_bytes, Wq_scale, Wk, 
             ss_t[i] = st_pool.tile([P, 4], F32, name="ss", tag="ss")
             rs_t[i] = st_pool.tile([P, 4], F32, name="rs", tag="rs")
             for h in range(heads_of(i)):
+                junk = junk_pool.tile([P, D], BF16, name="junk", tag="junk")
                 nc.scalar.activation(out=junk[:], in_=a_t[i][:, h * D:(h + 1) * D], func=ACT.Square, accum_out=ss_t[i][:, h:h + 1])
 
         def rsqrt(i):

@@ -19,374 +19,358 @@ P = 128
 PACK = 4
 PASSES = DIM // (P * PACK)
 TOKEN_TILES = TOKENS // P
-BANK = 512
-UNIT_COLS = 1024
-UNIT_CHUNKS = (HEADS * D) // UNIT_COLS
-UNITS = UNIT_CHUNKS * PASSES
-BANKS_PER_UNIT_CHUNK = UNIT_COLS // BANK
+BANK_COLS = 512
 PSUM_BANKS = 8
+UNIT_COLS = 1024
+UNITS = PASSES * (HEADS * D // UNIT_COLS)
+BANKS_PER_UNIT = UNIT_COLS // BANK_COLS
 
 FLOPS = 2 * TOKENS * DIM * (HEADS * D + 2 * D)
 
-VECTOR_WIDENS = {0: 3, 2: 4, 6: 1, 7: 2}
+VECTOR_WIDENS = {0: 2, 2: 4, 4: 1, 6: 1}
 SCALAR_INTERLEAVES = (5, 7)
-X_COPY_AFTER_PLANE = (8, 14, 17, 23)
-X_QUANT_SLOT = (1, 2, 3, 5)
-KV_INTERLEAVE_SLOT = (2, 4)
-KV_QUANT_SLOT = 4
-ROPE_SLOT = {3: (0, 1), 5: (2,), 6: (3, 4, 5)}
-NORM_AFTER_PLANE = {27: (0, 1)}
-VECTOR_ADDS = (1, 5)
-LOADS = (("wsc",), ("wqp", 0, 0), ("wqp", 0, 1), ("wqp", 0, 2), ("wqp", 0, 3), ("wq", 1), ("wq", 2), ("x", 0), ("wq", 3), ("x", 1), ("x", 2), ("wq", 4), ("wk",), ("x", 3), ("wq", 5), ("wv",), ("cs",), ("wq", 6), ("wq", 7))
-WD_BUFS, WI_BUFS, A_BUFS, B_BUFS = 4, 3, 8, 3
-FAST_INTERLEAVE = True
-VECTOR_SCALES = {}
-VECTOR_SCALES_DEFAULT = 0
+X_COPY_AFTER_PLANE = (8, 16, 20, 27)
+X_QUANT_AFTER_UNIT = (1, 3, 5, 5)
+KV_INTERLEAVE_AFTER_UNIT = (2, 3)
+KV_QUANT_AFTER_UNIT = 5
+ROPE_AFTER_UNIT = {4: (0, 1), 5: (2, 3)}
+VECTOR_ADDS = (1, 3)
+VECTOR_SCALED_HEADS = 1
 FINISH_LAG = 3
-V_COPY_ON_VECTOR = True
+
+WIDE_BUFS = 4
+INTERLEAVED_BUFS = 3
+ROTATED_BUFS = 8
+SWAPPED_BUFS = 3
+SCRATCH_BUFS = 8
 
 
 def tile_multiqueryattention_pa_kernel(tc, x, cos, sin, Wq_bytes, Wq_scale, Wk, Wv, out_0, out_1, out_2):
     nc = tc.nc
-    q_banks = [("q", c, m) for c in range(HEADS * D // BANK) for m in range(TOKEN_TILES)]
-    banks = q_banks + [("kv", i, 0) for i in range(TOKEN_TILES // 2)]
+    banks = [("q", block, m) for block in range(HEADS * D // BANK_COLS) for m in range(TOKEN_TILES)]
+    banks += [("kv", pair) for pair in range(TOKEN_TILES // 2)]
     n_banks = len(banks)
 
     with ExitStack() as ctx:
         keep = ctx.enter_context(tc.tile_pool(name="keep", bufs=1))
-        wd_pool = ctx.enter_context(tc.tile_pool(name="wdp", bufs=WD_BUFS))
-        wi_pool = ctx.enter_context(tc.tile_pool(name="wip", bufs=WI_BUFS))
-        a_pool = ctx.enter_context(tc.tile_pool(name="ap", bufs=A_BUFS))
-        b_pool = ctx.enter_context(tc.tile_pool(name="bp", bufs=B_BUFS))
-        junk_pool = ctx.enter_context(tc.tile_pool(name="junkp", bufs=8))
-        st_pool = ctx.enter_context(tc.tile_pool(name="stp", bufs=A_BUFS))
+        wide_pool = ctx.enter_context(tc.tile_pool(name="wide", bufs=WIDE_BUFS))
+        interleaved_pool = ctx.enter_context(tc.tile_pool(name="interleaved", bufs=INTERLEAVED_BUFS))
+        rotated_pool = ctx.enter_context(tc.tile_pool(name="rotated", bufs=ROTATED_BUFS))
+        swapped_pool = ctx.enter_context(tc.tile_pool(name="swapped", bufs=SWAPPED_BUFS))
+        stats_pool = ctx.enter_context(tc.tile_pool(name="stats", bufs=ROTATED_BUFS))
+        scratch_pool = ctx.enter_context(tc.tile_pool(name="scratch", bufs=SCRATCH_BUFS))
+        v_pool = ctx.enter_context(tc.tile_pool(name="v", bufs=2))
         psum = ctx.enter_context(tc.psum_pool(name="psum", bufs=PSUM_BANKS))
         ctx.enter_context(tc.manual_schedule())
 
-        x_v = x[0].rearrange("(m p) k -> m p k", p=P)
-        cos_v = cos.rearrange("(m p) o j -> p m (o j)", p=P)
-        sin_v = sin.rearrange("(m p) o j -> p m (o j)", p=P)
-        wqb_v = Wq_bytes.rearrange("(g p t) n -> g p t n", p=P, t=PACK)
-        wqs_v = Wq_scale.rearrange("(g p t) o -> p g (t o)", p=P, t=PACK)
-        wk_v = Wk.rearrange("(g p t) n -> p g (t n)", p=P, t=PACK)
-        wv_v = Wv.rearrange("(g p t) n -> p g (t n)", p=P, t=PACK)
-        o0_v = out_0[0].rearrange("(m p) h d -> m p (h d)", p=P)
-        o1_v = out_1[0].rearrange("(m p) d -> p m d", p=P)
-        o2_v = out_2[0].rearrange("(m p) d -> p m d", p=P)
+        x_rows = x[0].rearrange("(m p) k -> m p k", p=P)
+        cos_rows = cos.rearrange("(m p) o j -> p m (o j)", p=P)
+        sin_rows = sin.rearrange("(m p) o j -> p m (o j)", p=P)
+        wq_planes = Wq_bytes.rearrange("(g p t) n -> g p t n", p=P, t=PACK)
+        wq_plane_scales = Wq_scale.rearrange("(g p t) o -> p g (t o)", p=P, t=PACK)
+        wk_planes = Wk.rearrange("(g p t) n -> p g (t n)", p=P, t=PACK)
+        wv_planes = Wv.rearrange("(g p t) n -> p g (t n)", p=P, t=PACK)
+        q_out = out_0[0].rearrange("(m p) h d -> m p (h d)", p=P)
+        k_out = out_1[0].rearrange("(m p) d -> p m d", p=P)
+        v_out = out_2[0].rearrange("(m p) d -> p m d", p=P)
 
-        ident = keep.tile([P, P], F32, name="ident")
+        identity = keep.tile([P, P], F32, name="identity")
         one = keep.tile([P, 1], F32, name="one")
-        warm = keep.tile([P, 1], F32, name="warm")
-        vjunk = keep.tile([P, 1], F32, name="vjunk")
-        wsc = keep.tile([P, PASSES, PACK], F32, name="wsc")
+        warm_up = keep.tile([P, 1], F32, name="warm_up")
+        unread_sums = keep.tile([P, SCRATCH_BUFS], F32, name="unread_sums")
+        plane_scales = keep.tile([P, PASSES, PACK], F32, name="plane_scales")
         cos_t = keep.tile([P, TOKEN_TILES, HALF], BF16, name="cos_t")
-        sn_t = keep.tile([P, TOKEN_TILES, 2, HALF], BF16, name="sn_t")
-        wq_bytes_t = [keep.tile([P, PASSES, PACK, UNIT_COLS], U8, name="wq_bytes_t%d" % c) for c in range(UNIT_CHUNKS)]
-        x_sb = [keep.tile([P, DIM], BF16, name="x_sb%d" % m) for m in range(TOKEN_TILES)]
-        x_int = [keep.tile([P, DIM], BF16, name="x_int%d" % m, align_bytes=64) for m in range(TOKEN_TILES)]
+        sin_t = keep.tile([P, TOKEN_TILES, 2, HALF], BF16, name="sin_t")
+        wq_bytes_t = [keep.tile([P, PASSES, PACK, UNIT_COLS], U8, name="wq_bytes_t%d" % half) for half in range(UNITS // PASSES)]
+        x_t = [keep.tile([P, DIM], BF16, name="x_t%d" % m) for m in range(TOKEN_TILES)]
+        x_interleaved = [keep.tile([P, DIM], BF16, name="x_interleaved%d" % m, align_bytes=64) for m in range(TOKEN_TILES)]
         x_codes = [keep.tile([P, PASSES * P], U32, name="x_codes%d" % m, align_bytes=64) for m in range(TOKEN_TILES)]
         x_scales = [keep.tile([P, PASSES * P], U8, name="x_scales%d" % m, align_bytes=64) for m in range(TOKEN_TILES)]
-        wq_codes = [keep.tile([P, PASSES, UNIT_COLS], U32, name="wq_codes%d" % c, align_bytes=64) for c in range(UNIT_CHUNKS)]
-        wq_scales = [keep.tile([P, PASSES, UNIT_COLS], U8, name="wq_scales%d" % c, align_bytes=64) for c in range(UNIT_CHUNKS)]
-        wk_raw = keep.tile([P, PASSES, PACK, D], BF16, name="wk_raw")
-        wv_raw = keep.tile([P, PASSES, PACK, D], BF16, name="wv_raw")
-        kv_int = keep.tile([P, PASSES, 2 * D, PACK], BF16, name="kv_int", align_bytes=64)
+        wq_codes = [keep.tile([P, PASSES, UNIT_COLS], U32, name="wq_codes%d" % half, align_bytes=64) for half in range(UNITS // PASSES)]
+        wq_scales = [keep.tile([P, PASSES, UNIT_COLS], U8, name="wq_scales%d" % half, align_bytes=64) for half in range(UNITS // PASSES)]
+        wk_t = keep.tile([P, PASSES, PACK, D], BF16, name="wk_t")
+        wv_t = keep.tile([P, PASSES, PACK, D], BF16, name="wv_t")
+        kv_interleaved = keep.tile([P, PASSES, 2 * D, PACK], BF16, name="kv_interleaved", align_bytes=64)
         kv_codes = keep.tile([P, PASSES, 2 * D], U32, name="kv_codes", align_bytes=64)
         kv_scales = keep.tile([P, PASSES, 2 * D], U8, name="kv_scales", align_bytes=64)
 
-        make_identity(nc, ident[:])
+        make_identity(nc, identity[:])
         nc.vector.memset(one[:], 1.0)
-        nc.scalar.activation(out=warm[:], in_=one[:], func=ACT.Abs_reciprocal_sqrt)
+        nc.scalar.activation(out=warm_up[:], in_=one[:], func=ACT.Abs_reciprocal_sqrt)
 
-        for ld in LOADS:
-            if ld[0] == "wsc":
-                nc.sync.dma_start(out=wsc[:], in_=wqs_v)
-            elif ld[0] == "wq":
-                c, g = divmod(ld[1], PASSES)
-                nc.sync.dma_start(out=wq_bytes_t[c][:, g, :, :], in_=wqb_v[g][:, :, c * UNIT_COLS:(c + 1) * UNIT_COLS])
-            elif ld[0] == "wqp":
-                c, g = divmod(ld[1], PASSES)
-                nc.sync.dma_start(out=wq_bytes_t[c][:, g, ld[2], :], in_=wqb_v[g][:, ld[2], c * UNIT_COLS:(c + 1) * UNIT_COLS])
-            elif ld[0] == "x":
-                nc.sync.dma_start(out=x_sb[ld[1]][:], in_=x_v[ld[1]])
-            elif ld[0] == "wk":
-                nc.sync.dma_start(out=wk_raw[:].rearrange("p g t n -> p g (t n)"), in_=wk_v)
-            elif ld[0] == "wv":
-                nc.sync.dma_start(out=wv_raw[:].rearrange("p g t n -> p g (t n)"), in_=wv_v)
-            elif ld[0] == "cs":
-                nc.sync.dma_start(out=cos_t[:], in_=cos_v)
-                nc.sync.dma_start(out=sn_t[:, :, 0, :], in_=sin_v)
+        def load_plane(u, t):
+            half, g = divmod(u, PASSES)
+            nc.sync.dma_start(out=wq_bytes_t[half][:, g, t, :], in_=wq_planes[g][:, t, half * UNIT_COLS:(half + 1) * UNIT_COLS])
 
+        def load_unit(u):
+            half, g = divmod(u, PASSES)
+            nc.sync.dma_start(out=wq_bytes_t[half][:, g, :, :], in_=wq_planes[g][:, :, half * UNIT_COLS:(half + 1) * UNIT_COLS])
+
+        def load_x(m):
+            nc.sync.dma_start(out=x_t[m][:], in_=x_rows[m])
+
+        nc.sync.dma_start(out=plane_scales[:], in_=wq_plane_scales)
+        for t in range(PACK):
+            load_plane(0, t)
+        load_unit(1)
+        load_unit(2)
+        load_x(0)
+        load_unit(3)
+        nc.sync.dma_start(out=wk_t[:].rearrange("p g t n -> p g (t n)"), in_=wk_planes)
+        load_unit(4)
+        load_x(1)
+        nc.sync.dma_start(out=wv_t[:].rearrange("p g t n -> p g (t n)"), in_=wv_planes)
+        load_unit(5)
+        load_x(2)
+        load_x(3)
+        nc.sync.dma_start(out=cos_t[:], in_=cos_rows)
+        nc.sync.dma_start(out=sin_t[:, :, 0, :], in_=sin_rows)
+        load_unit(6)
+        load_unit(7)
+
+        x_tiles_copied = set()
         x_quantised = set()
         units_quantised = set()
         kv_quantised = set()
-        x_copied = set()
-        read_out = set()
-        filled = set()
-        roped = set()
-        normed = set()
-        scaled = set()
-        finished = set()
+        banks_filled = set()
+        banks_roped = set()
+        banks_read = set()
 
-        xt = {}
+        x_transposed = {}
 
         def x_transpose(m):
-            words = x_sb[m][:].bitcast(F32)
+            words = x_t[m][:].bitcast(F32)
             for a in range(2):
-                xt[(m, a)] = psum.tile([P, 2, 2, P], F32, name="bank", tag="bank")
+                x_transposed[(m, a)] = psum.tile([P, 2, 2, P], F32, name="bank", tag="bank")
                 for gg in range(2):
                     g = 2 * a + gg
                     for w in range(2):
-                        nc.tensor.transpose(out=xt[(m, a)][:, gg, w, :], in_=words[:, 256 * g + w:256 * (g + 1):2], identity=ident[:])
+                        nc.tensor.transpose(
+                            out=x_transposed[(m, a)][:, gg, w, :],
+                            in_=words[:, 256 * g + w:256 * (g + 1):2],
+                            identity=identity[:],
+                        )
 
         def x_copy(m):
+            words = x_interleaved[m][:].bitcast(F32).rearrange("p (g r w) -> p g r w", g=PASSES, w=2)
             for a in range(2):
-                dst = x_int[m][:].bitcast(F32).rearrange("p (g r w) -> p g r w", g=PASSES, w=2)[:, 2 * a:2 * a + 2, :, :]
-                nc.scalar.copy(out=dst, in_=xt[(m, a)][:].rearrange("p g w r -> p g r w"))
-                x_copied.add(2 * m + a)
+                nc.scalar.copy(out=words[:, 2 * a:2 * a + 2, :, :], in_=x_transposed[(m, a)][:].rearrange("p g w r -> p g r w"))
+                x_tiles_copied.add(2 * m + a)
 
-        def x_quant(m):
-            nc.vector.quantize_mx(out=x_codes[m][:].bitcast(FP8X4), scales=x_scales[m][:], in_=x_int[m][:])
+        def x_quantise(m):
+            nc.vector.quantize_mx(out=x_codes[m][:].bitcast(FP8X4), scales=x_scales[m][:], in_=x_interleaved[m][:])
             x_quantised.add(m)
 
-        wd = {}
-        wi = {}
+        wide = {}
+        interleaved = {}
 
-        def widen(u, t, eng):
-            c, g = divmod(u, PASSES)
-            if u not in wd:
-                wd[u] = wd_pool.tile([P, PACK, UNIT_COLS], BF16, name="wd", tag="wd")
-            src = wq_bytes_t[c][:, g, t, :].bitcast(FP8)
-            if eng == "S":
-                nc.scalar.activation(out=wd[u][:, t, :], in_=src, func=ACT.Copy, scale=wsc[:, g, t:t + 1])
-            else:
-                nc.vector.tensor_scalar(out=wd[u][:, t, :], in0=src, scalar1=wsc[:, g, t:t + 1], scalar2=None, op0=ALU.mult)
+        def on_vector(u, t):
+            return t >= PACK - VECTOR_WIDENS.get(u, 0)
 
-        def interleave(u, eng):
-            wi[u] = wi_pool.tile([P, UNIT_COLS * PACK], BF16, name="wi", tag="wi", align_bytes=64)
-            if FAST_INTERLEAVE:
-                dst = wi[u][:].rearrange("p (c i t) -> p c t i", i=4, t=PACK)
-                src = wd[u][:].rearrange("p t (c i) -> p c t i", i=4)
+        def widen(u, t):
+            half, g = divmod(u, PASSES)
+            if u not in wide:
+                wide[u] = wide_pool.tile([P, PACK, UNIT_COLS], BF16, name="wide", tag="wide")
+            codes = wq_bytes_t[half][:, g, t, :].bitcast(FP8)
+            scale = plane_scales[:, g, t:t + 1]
+            if on_vector(u, t):
+                nc.vector.tensor_scalar(out=wide[u][:, t, :], in0=codes, scalar1=scale, scalar2=None, op0=ALU.mult)
             else:
-                dst = wi[u][:].rearrange("p (n t) -> p n t", t=PACK)
-                src = wd[u][:].rearrange("p t n -> p n t")
-            if eng == "S":
+                nc.scalar.activation(out=wide[u][:, t, :], in_=codes, func=ACT.Copy, scale=scale)
+
+        def vector_widens(u):
+            for t in range(PACK):
+                if u < UNITS and on_vector(u, t):
+                    widen(u, t)
+
+        def interleave(u):
+            interleaved[u] = interleaved_pool.tile([P, UNIT_COLS * PACK], BF16, name="interleaved", tag="interleaved", align_bytes=64)
+            dst = interleaved[u][:].rearrange("p (c i t) -> p c t i", i=4, t=PACK)
+            src = wide[u][:].rearrange("p t (c i) -> p c t i", i=4)
+            if u in SCALAR_INTERLEAVES:
                 nc.scalar.copy(out=dst, in_=src)
             else:
                 nc.vector.tensor_copy(out=dst, in_=src)
 
-        def quant(u):
-            c, g = divmod(u, PASSES)
-            nc.vector.quantize_mx(out=wq_codes[c][:, g, :].bitcast(FP8X4), scales=wq_scales[c][:, g, :], in_=wi[u][:])
+        def quantise(u):
+            half, g = divmod(u, PASSES)
+            nc.vector.quantize_mx(out=wq_codes[half][:, g, :].bitcast(FP8X4), scales=wq_scales[half][:, g, :], in_=interleaved[u][:])
             units_quantised.add(u)
 
-        def kv_interleave(i):
-            raw = wk_raw if i == 0 else wv_raw
-            nc.vector.tensor_copy(out=kv_int[:, :, i * D:(i + 1) * D, :], in_=raw[:].rearrange("p g t n -> p g n t"))
+        def kv_interleave(which):
+            planes = wk_t if which == 0 else wv_t
+            nc.vector.tensor_copy(out=kv_interleaved[:, :, which * D:(which + 1) * D, :], in_=planes[:].rearrange("p g t n -> p g n t"))
 
-        def kv_quant():
+        def kv_quantise():
             nc.vector.quantize_mx(
                 out=kv_codes[:].rearrange("p g n -> p (g n)").bitcast(FP8X4),
                 scales=kv_scales[:].rearrange("p g n -> p (g n)"),
-                in_=kv_int[:].rearrange("p g n t -> p (g n t)"),
+                in_=kv_interleaved[:].rearrange("p g n t -> p (g n t)"),
             )
             kv_quantised.add(0)
 
         bank_t = {}
 
-        def mm(out, m, g, rhs, rhs_scale):
-            nc.tensor.matmul_mx(
-                out=out,
-                lhsT=x_codes[m][:, g * P:(g + 1) * P].bitcast(FP8X4),
-                lhsT_scale=x_scales[m][:, g * P:(g + 1) * P],
-                rhs=rhs.bitcast(FP8X4),
-                rhs_scale=rhs_scale,
-                start=(g == 0),
-                stop=(g == PASSES - 1),
-            )
+        def matmul_passes(out, m, codes, scales):
+            for g in range(PASSES):
+                nc.tensor.matmul_mx(
+                    out=out,
+                    lhsT=x_codes[m][:, g * P:(g + 1) * P].bitcast(FP8X4),
+                    lhsT_scale=x_scales[m][:, g * P:(g + 1) * P],
+                    rhs=codes[:, g, :].bitcast(FP8X4),
+                    rhs_scale=scales[:, g, :],
+                    start=(g == 0),
+                    stop=(g == PASSES - 1),
+                )
 
         def can_fill(i):
-            kind, c, m = banks[i]
-            free = (i in x_copied) if i < PSUM_BANKS else (i - PSUM_BANKS in read_out)
-            if kind == "q":
-                uc = c // BANKS_PER_UNIT_CHUNK
-                ready = m in x_quantised and all(uc * PASSES + g in units_quantised for g in range(PASSES))
-            else:
-                ready = 0 in kv_quantised and 2 * c in x_quantised and 2 * c + 1 in x_quantised
-            return free and ready
+            buffer_free = (i in x_tiles_copied) if i < PSUM_BANKS else (i - PSUM_BANKS in banks_read)
+            if banks[i][0] == "q":
+                block, m = banks[i][1:]
+                first_unit = (block // BANKS_PER_UNIT) * PASSES
+                return buffer_free and m in x_quantised and all(first_unit + g in units_quantised for g in range(PASSES))
+            pair = banks[i][1]
+            return buffer_free and 0 in kv_quantised and 2 * pair in x_quantised and 2 * pair + 1 in x_quantised
 
         def fill(i):
-            kind, c, m = banks[i]
-            bank_t[i] = psum.tile([P, BANK], F32, name="bank", tag="bank")
-            if kind == "q":
-                uc, cc = divmod(c, BANKS_PER_UNIT_CHUNK)
-                cols = slice(cc * BANK, (cc + 1) * BANK)
-                for g in range(PASSES):
-                    mm(bank_t[i][:], m, g, wq_codes[uc][:, g, cols], wq_scales[uc][:, g, cols])
+            bank_t[i] = psum.tile([P, BANK_COLS], F32, name="bank", tag="bank")
+            if banks[i][0] == "q":
+                block, m = banks[i][1:]
+                half, part = divmod(block, BANKS_PER_UNIT)
+                cols = slice(part * BANK_COLS, (part + 1) * BANK_COLS)
+                matmul_passes(bank_t[i][:], m, wq_codes[half][:, :, cols], wq_scales[half][:, :, cols])
             else:
-                for mmi in range(2):
-                    for g in range(PASSES):
-                        mm(bank_t[i][:, mmi * 2 * D:(mmi + 1) * 2 * D], 2 * c + mmi, g, kv_codes[:, g, :], kv_scales[:, g, :])
-            filled.add(i)
+                pair = banks[i][1]
+                for r in range(2):
+                    matmul_passes(bank_t[i][:, r * 2 * D:(r + 1) * 2 * D], 2 * pair + r, kv_codes, kv_scales)
+            banks_filled.add(i)
 
         def fill_ready():
             for i in range(n_banks):
-                if i not in filled and (i == 0 or i - 1 in filled) and can_fill(i):
+                if i not in banks_filled and (i == 0 or i - 1 in banks_filled) and can_fill(i):
                     fill(i)
 
-        a_t = {}
-        b_t = {}
-        v_t = {}
+        rotated = {}
+        swapped = {}
 
         def heads_of(i):
-            return BANK // D if banks[i][0] == "q" else 2
+            return BANK_COLS // D if banks[i][0] == "q" else 2
 
-        def rope_mults(i):
-            kind, c, m = banks[i]
-            nh = heads_of(i)
-            if not roped:
-                nc.vector.tensor_scalar(out=sn_t[:, :, 1, :], in0=sn_t[:, :, 0, :], scalar1=-1.0, scalar2=None, op0=ALU.mult)
-            if kind == "q":
-                pv = bank_t[i][:].rearrange("p (h w j) -> p h w j", w=2, j=HALF)
-                cb = cos_t[:, m, :].unsqueeze(1).unsqueeze(1).to_broadcast([P, nh, 2, HALF])
-                sb = sn_t[:, m, :, :].unsqueeze(1).to_broadcast([P, nh, 2, HALF])
+        def rope(i):
+            heads = heads_of(i)
+            if not banks_roped:
+                nc.vector.tensor_scalar(out=sin_t[:, :, 1, :], in0=sin_t[:, :, 0, :], scalar1=-1.0, scalar2=None, op0=ALU.mult)
+            if banks[i][0] == "q":
+                m = banks[i][2]
+                halves = bank_t[i][:].rearrange("p (h w j) -> p h w j", w=2, j=HALF)
+                cos_b = cos_t[:, m, :].unsqueeze(1).unsqueeze(1).to_broadcast([P, heads, 2, HALF])
+                sin_b = sin_t[:, m, :, :].unsqueeze(1).to_broadcast([P, heads, 2, HALF])
             else:
-                pv = bank_t[i][:].rearrange("p (h e w j) -> p h e w j", e=2, w=2, j=HALF)[:, :, 0, :, :]
-                cb = cos_t[:, 2 * c:2 * c + 2, :].unsqueeze(2).to_broadcast([P, nh, 2, HALF])
-                sb = sn_t[:, 2 * c:2 * c + 2, :, :]
-            a_t[i] = a_pool.tile([P, BANK], F32, name="a", tag="a")
-            b_t[i] = b_pool.tile([P, BANK], F32, name="b", tag="b")
-            av = a_t[i][:, 0:nh * D].rearrange("p (h w j) -> p h w j", w=2, j=HALF)
-            bv = b_t[i][:, 0:nh * D].rearrange("p (h w j) -> p h w j", w=2, j=HALF)
-            nc.vector.tensor_tensor(out=av, in0=pv, in1=cb, op=ALU.mult)
-            nc.vector.tensor_tensor(out=bv, in0=pv[:, :, ::-1, :], in1=sb, op=ALU.mult)
-            roped.add(i)
-            if kind == "q":
-                read_out.add(i)
-            elif V_COPY_ON_VECTOR:
-                v_copy(i)
+                pair = banks[i][1]
+                halves = bank_t[i][:].rearrange("p (h e w j) -> p h e w j", e=2, w=2, j=HALF)[:, :, 0, :, :]
+                cos_b = cos_t[:, 2 * pair:2 * pair + 2, :].unsqueeze(2).to_broadcast([P, heads, 2, HALF])
+                sin_b = sin_t[:, 2 * pair:2 * pair + 2, :, :]
+            rotated[i] = rotated_pool.tile([P, BANK_COLS], F32, name="rotated", tag="rotated")
+            swapped[i] = swapped_pool.tile([P, BANK_COLS], F32, name="swapped", tag="swapped")
+            width = heads * D
+            nc.vector.tensor_tensor(out=rotated[i][:, 0:width].rearrange("p (h w j) -> p h w j", w=2, j=HALF), in0=halves, in1=cos_b, op=ALU.mult)
+            nc.vector.tensor_tensor(out=swapped[i][:, 0:width].rearrange("p (h w j) -> p h w j", w=2, j=HALF), in0=halves[:, :, ::-1, :], in1=sin_b, op=ALU.mult)
+            if banks[i][0] == "kv":
+                v_t = v_pool.tile([P, 2, D], F32, name="v_t", tag="v_t")
+                nc.vector.tensor_copy(out=v_t[:], in_=bank_t[i][:].rearrange("p (h e d) -> p h e d", e=2, d=D)[:, :, 1, :])
+                nc.sync.dma_start(out=v_out[:, 2 * pair:2 * pair + 2, :], in_=v_t[:])
+            banks_roped.add(i)
+            banks_read.add(i)
 
         def rope_add(i):
-            w = heads_of(i) * D
-            eng = nc.vector if i in VECTOR_ADDS else nc.gpsimd
-            eng.tensor_tensor(out=a_t[i][:, 0:w], in0=a_t[i][:, 0:w], in1=b_t[i][:, 0:w], op=ALU.add)
+            width = heads_of(i) * D
+            engine = nc.vector if i in VECTOR_ADDS else nc.gpsimd
+            engine.tensor_tensor(out=rotated[i][:, 0:width], in0=rotated[i][:, 0:width], in1=swapped[i][:, 0:width], op=ALU.add)
 
-        def v_copy(i):
-            c = banks[i][1]
-            v_t[i] = st_pool.tile([P, 2, D], F32, name="vt", tag="vt")
-            src = bank_t[i][:].rearrange("p (h e d) -> p h e d", e=2, d=D)[:, :, 1, :]
-            if V_COPY_ON_VECTOR:
-                nc.vector.tensor_copy(out=v_t[i][:], in_=src)
-            else:
-                nc.scalar.copy(out=v_t[i][:], in_=src)
-            nc.sync.dma_start(out=o2_v[:, 2 * c:2 * c + 2, :], in_=v_t[i][:])
-            read_out.add(i)
+        square_sums = {}
+        inverse_rms = {}
 
-        ss_t = {}
-        rs_t = {}
+        def head_cols(h):
+            return slice(h * D, (h + 1) * D)
 
-        def squares(i):
-            ss_t[i] = st_pool.tile([P, 4], F32, name="ss", tag="ss")
-            rs_t[i] = st_pool.tile([P, 4], F32, name="rs", tag="rs")
+        def sum_squares(i):
+            square_sums[i] = stats_pool.tile([P, BANK_COLS // D], F32, name="square_sums", tag="square_sums")
             for h in range(heads_of(i)):
-                junk = junk_pool.tile([P, D], BF16, name="junk", tag="junk")
-                nc.scalar.activation(out=junk[:], in_=a_t[i][:, h * D:(h + 1) * D], func=ACT.Square, accum_out=ss_t[i][:, h:h + 1])
+                unread = scratch_pool.tile([P, D], BF16, name="unread", tag="unread")
+                nc.scalar.activation(out=unread[:], in_=rotated[i][:, head_cols(h)], func=ACT.Square, accum_out=square_sums[i][:, h:h + 1])
 
-        def rsqrt(i):
-            nh = heads_of(i)
-            nc.scalar.activation(out=rs_t[i][:, 0:nh], in_=ss_t[i][:, 0:nh], func=ACT.Abs_reciprocal_sqrt, scale=1.0 / D, bias=EPS)
+        def take_inverse_rms(i):
+            heads = heads_of(i)
+            inverse_rms[i] = stats_pool.tile([P, BANK_COLS // D], F32, name="inverse_rms", tag="inverse_rms")
+            nc.scalar.activation(out=inverse_rms[i][:, 0:heads], in_=square_sums[i][:, 0:heads], func=ACT.Abs_reciprocal_sqrt, scale=1.0 / D, bias=EPS)
 
-        def vector_heads(i):
-            return min(heads_of(i), VECTOR_SCALES.get(i, VECTOR_SCALES_DEFAULT))
-
-        def scalar_scale(i):
-            for h in range(heads_of(i) - vector_heads(i)):
-                nc.scalar.activation(out=a_t[i][:, h * D:(h + 1) * D], in_=a_t[i][:, h * D:(h + 1) * D], func=ACT.Copy, scale=rs_t[i][:, h:h + 1])
-            scaled.add(i)
+        def scalar_scales(i):
+            for h in range(heads_of(i) - VECTOR_SCALED_HEADS):
+                nc.scalar.activation(out=rotated[i][:, head_cols(h)], in_=rotated[i][:, head_cols(h)], func=ACT.Copy, scale=inverse_rms[i][:, h:h + 1])
 
         def finish(i):
-            kind, c, m = banks[i]
-            for h in range(heads_of(i) - vector_heads(i), heads_of(i)):
-                nc.vector.tensor_scalar(out=a_t[i][:, h * D:(h + 1) * D], in0=a_t[i][:, h * D:(h + 1) * D], scalar1=rs_t[i][:, h:h + 1], scalar2=None, op0=ALU.mult, op1=ALU.add, accum_out=vjunk[:])
-            if kind == "q":
-                nc.sync.dma_start(out=o0_v[m][:, c * BANK:(c + 1) * BANK], in_=a_t[i][:])
+            for h in range(heads_of(i) - VECTOR_SCALED_HEADS, heads_of(i)):
+                nc.vector.tensor_scalar(
+                    out=rotated[i][:, head_cols(h)],
+                    in0=rotated[i][:, head_cols(h)],
+                    scalar1=inverse_rms[i][:, h:h + 1],
+                    scalar2=None,
+                    op0=ALU.mult,
+                    op1=ALU.add,
+                    accum_out=unread_sums[:, i % SCRATCH_BUFS:i % SCRATCH_BUFS + 1],
+                )
+            if banks[i][0] == "q":
+                block, m = banks[i][1:]
+                nc.sync.dma_start(out=q_out[m][:, block * BANK_COLS:(block + 1) * BANK_COLS], in_=rotated[i][:])
             else:
-                nc.sync.dma_start(out=o1_v[:, 2 * c:2 * c + 2, :], in_=a_t[i][:, 0:2 * D].rearrange("p (h d) -> p h d", d=D))
-            finished.add(i)
-
-        def finish_ready(upto):
-            for i in range(n_banks):
-                if i <= upto and i in scaled and i not in finished:
-                    finish(i)
-
-        waiting = []
-
-        def norm(i):
-            if waiting:
-                rsqrt(waiting[0])
-            if i is not None:
-                if banks[i][0] == "kv" and not V_COPY_ON_VECTOR:
-                    v_copy(i)
-                squares(i)
-                normed.add(i)
-            if waiting:
-                scalar_scale(waiting[0])
-                waiting.clear()
-            if i is not None:
-                waiting.append(i)
-
-        def on_vector(u, t):
-            return t >= PACK - VECTOR_WIDENS.get(u, 0)
-
-        def vector_widens(u):
-            for t in range(PACK):
-                if u < UNITS and on_vector(u, t):
-                    widen(u, t, "V")
+                pair = banks[i][1]
+                nc.sync.dma_start(out=k_out[:, 2 * pair:2 * pair + 2, :], in_=rotated[i][:, 0:2 * D].rearrange("p (h d) -> p h d", d=D))
 
         for m in range(TOKEN_TILES):
             x_transpose(m)
 
         for s in range(UNITS + 1):
-            for t in range(PACK):
-                if s < UNITS:
+            if s < UNITS:
+                for t in range(PACK):
                     if not on_vector(s, t):
-                        widen(s, t, "S")
+                        widen(s, t)
                     if t == PACK - 1 and s in SCALAR_INTERLEAVES:
-                        interleave(s, "S")
+                        interleave(s)
                     for m in range(TOKEN_TILES):
                         if X_COPY_AFTER_PLANE[m] == PACK * s + t:
                             x_copy(m)
-                    for i in NORM_AFTER_PLANE.get(PACK * s + t, ()):
-                        norm(i)
             if s == 0:
                 vector_widens(0)
             vector_widens(s + 1)
             if s < UNITS and s not in SCALAR_INTERLEAVES:
-                interleave(s, "V")
+                interleave(s)
             if s >= 1:
-                quant(s - 1)
+                quantise(s - 1)
                 for m in range(TOKEN_TILES):
-                    if X_QUANT_SLOT[m] == s - 1:
-                        x_quant(m)
-                for i in range(2):
-                    if KV_INTERLEAVE_SLOT[i] == s - 1:
-                        kv_interleave(i)
-                if KV_QUANT_SLOT == s - 1:
-                    kv_quant()
+                    if X_QUANT_AFTER_UNIT[m] == s - 1:
+                        x_quantise(m)
+                for which in range(2):
+                    if KV_INTERLEAVE_AFTER_UNIT[which] == s - 1:
+                        kv_interleave(which)
+                if KV_QUANT_AFTER_UNIT == s - 1:
+                    kv_quantise()
                 fill_ready()
-                for i in ROPE_SLOT.get(s - 1, ()):
-                    rope_mults(i)
-                for i in ROPE_SLOT.get(s - 1, ()):
+                for i in ROPE_AFTER_UNIT.get(s - 1, ()):
+                    rope(i)
+                for i in ROPE_AFTER_UNIT.get(s - 1, ()):
                     rope_add(i)
             fill_ready()
 
-        for i in range(n_banks + 1):
-            if i < n_banks and i not in roped:
-                rope_mults(i)
+        for i in range(n_banks + FINISH_LAG):
+            if i < n_banks and i not in banks_roped:
+                rope(i)
                 rope_add(i)
-            finish_ready(i - FINISH_LAG)
-            if i >= 1 and i - 1 not in normed:
-                norm(i - 1)
+            if i >= FINISH_LAG:
+                finish(i - FINISH_LAG)
+            if 2 <= i < n_banks + 2:
+                take_inverse_rms(i - 2)
+            if 1 <= i < n_banks + 1:
+                sum_squares(i - 1)
+            if 2 <= i < n_banks + 2:
+                scalar_scales(i - 2)
             fill_ready()
-        norm(None)
-        finish_ready(n_banks)

@@ -20,29 +20,87 @@ PACK = 4
 PASSES = DIM // (P * PACK)
 TOKEN_TILES = TOKENS // P
 BANK_COLS = 512
-PSUM_BANKS = 8
 UNIT_COLS = 1024
 UNITS = PASSES * (HEADS * D // UNIT_COLS)
 BANKS_PER_UNIT = UNIT_COLS // BANK_COLS
+IL_COLS = 256
+IL_PARTS = UNIT_COLS // IL_COLS
 
 FLOPS = 2 * TOKENS * DIM * (HEADS * D + 2 * D)
 
-VECTOR_WIDENS = {0: 2, 2: 4, 4: 1, 6: 1}
-SCALAR_INTERLEAVES = (5, 7)
-X_COPY_AFTER_PLANE = (8, 16, 20, 27)
-X_QUANT_AFTER_UNIT = (1, 3, 5, 5)
-KV_INTERLEAVE_AFTER_UNIT = (2, 3)
-KV_QUANT_AFTER_UNIT = 5
-ROPE_AFTER_UNIT = {4: (0, 1), 5: (2, 3)}
-VECTOR_ADDS = (1, 3)
-VECTOR_SCALED_HEADS = 1
-FINISH_LAG = 3
-
-WIDE_BUFS = 4
-INTERLEAVED_BUFS = 3
+WIDEN = ('AABB', 'AAAA', 'AABB', 'ABBB', 'AAAA', 'AAAB', 'AABB', 'AAAA')
+INTERLEAVE = 'VPVVPVVP'
+EVACUATE = ('SSSS', 'SSSS', 'SSSS', 'SSSS', 'SSSS', 'SSSS', 'SSSS', 'SSSS')
+STREAMS = ((0, 3, 2, 5, 6), (1, 4, 7))
+VECTOR_ADDS = (6,)
+VECTOR_SCALED_HEADS = {0: 0, 1: 0, 2: 0, 3: 0, 4: 0, 5: 0, 6: 0, 7: 0, 8: 1, 9: 1, 10: 1, 11: 1, 12: 1, 13: 1, 14: 1, 15: 1, 16: 1, 17: 1}
+VECTOR_SCALED_HEADS_DEFAULT = 0
+LOAD_ORDER = (('u', 1), ('u', 3), ('u', 2), ('x', 0), ('c',), ('u', 5), ('k',), ('u', 6), ('u', 4), ('x', 1), ('u', 7), ('x', 2), ('x', 3), ('v',))
+WIDE_BUFS = (2, 2)
+INTERLEAVED_BUFS = (2, 2)
 ROTATED_BUFS = 8
 SWAPPED_BUFS = 3
 SCRATCH_BUFS = 8
+BANK_BUFS = 6
+IL_BUFS = 2
+QUEUE_NAMES = ("scalar", "vector", "tensor", "gpsimd", "sync")
+QUEUES = {
+    'scalar': [
+        ('widen', 0, 0), ('widen', 0, 1), ('widen', 1, 0), ('widen', 1, 1), ('widen', 1, 2), ('widen', 1, 3),
+        ('widen', 3, 0), ('x_copy', 0), ('evacuate', 1, 0), ('evacuate', 1, 1), ('evacuate', 1, 2), ('evacuate', 1, 3),
+        ('widen', 2, 0), ('widen', 2, 1), ('widen', 4, 0), ('x_copy', 1), ('widen', 5, 0), ('widen', 5, 1),
+        ('x_copy', 2), ('x_copy', 3), ('widen', 5, 2), ('widen', 6, 0), ('widen', 6, 1), ('widen', 4, 1),
+        ('widen', 4, 2), ('widen', 4, 3), ('widen', 7, 0), ('evacuate', 4, 0), ('widen', 7, 1), ('widen', 7, 2),
+        ('evacuate', 4, 1), ('evacuate', 4, 2), ('evacuate', 4, 3), ('widen', 7, 3), ('sum_squares', 0), ('evacuate', 7, 0),
+        ('evacuate', 7, 1), ('evacuate', 7, 2), ('evacuate', 7, 3), ('take_inverse_rms', 0), ('sum_squares', 1), ('scalar_scales', 0),
+        ('take_inverse_rms', 1), ('sum_squares', 2), ('scalar_scales', 1), ('take_inverse_rms', 2), ('sum_squares', 3), ('scalar_scales', 2),
+        ('take_inverse_rms', 3), ('sum_squares', 4), ('scalar_scales', 3), ('take_inverse_rms', 4), ('sum_squares', 5), ('scalar_scales', 4),
+        ('take_inverse_rms', 5), ('sum_squares', 6), ('scalar_scales', 5), ('take_inverse_rms', 6), ('sum_squares', 7), ('scalar_scales', 6),
+        ('take_inverse_rms', 7), ('sum_squares', 8), ('scalar_scales', 7), ('take_inverse_rms', 8), ('sum_squares', 9), ('scalar_scales', 8),
+        ('take_inverse_rms', 9), ('sum_squares', 10), ('scalar_scales', 9), ('take_inverse_rms', 10), ('sum_squares', 11), ('scalar_scales', 10),
+        ('take_inverse_rms', 11), ('sum_squares', 12), ('scalar_scales', 11), ('take_inverse_rms', 12), ('sum_squares', 13), ('scalar_scales', 12),
+        ('take_inverse_rms', 13), ('sum_squares', 14), ('scalar_scales', 13), ('take_inverse_rms', 14), ('sum_squares', 15), ('scalar_scales', 14),
+        ('take_inverse_rms', 15), ('sum_squares', 16), ('scalar_scales', 15), ('take_inverse_rms', 16), ('sum_squares', 17), ('scalar_scales', 16),
+        ('take_inverse_rms', 17), ('scalar_scales', 17),
+    ],
+    'vector': [
+        ('vector_scales', 0), ('vector_scales', 1), ('vector_scales', 2), ('vector_scales', 3), ('vector_scales', 4), ('vector_scales', 5),
+        ('vector_scales', 6), ('vector_scales', 7), ('widen', 0, 2), ('widen', 0, 3), ('interleave', 0), ('widen', 3, 1),
+        ('quantise', 0), ('widen', 3, 2), ('negate_sin',), ('widen', 3, 3), ('widen', 2, 2), ('interleave', 3),
+        ('x_quantise', 0), ('quantise', 3), ('quantise', 1), ('widen', 2, 3), ('widen', 5, 3), ('interleave', 2),
+        ('x_quantise', 1), ('quantise', 2), ('x_quantise', 2), ('kv_interleave', 0), ('x_quantise', 3), ('interleave', 5),
+        ('widen', 6, 2), ('quantise', 5), ('rope', 0), ('rope', 1), ('rope', 2), ('rope', 3),
+        ('rope', 4), ('rope', 5), ('rope', 6), ('rope', 7), ('add', 6), ('widen', 6, 3),
+        ('quantise', 4), ('interleave', 6), ('quantise', 7), ('quantise', 6), ('kv_interleave', 1), ('rope', 8),
+        ('rope', 9), ('rope', 10), ('rope', 11), ('rope', 12), ('vector_scales', 8), ('rope', 13),
+        ('vector_scales', 9), ('rope', 14), ('vector_scales', 10), ('rope', 15), ('vector_scales', 11), ('kv_quantise',),
+        ('vector_scales', 12), ('vector_scales', 13), ('rope', 16), ('vector_scales', 14), ('rope', 17), ('vector_scales', 15),
+        ('vector_scales', 16), ('vector_scales', 17),
+    ],
+    'tensor': [
+        ('transpose', 0), ('pe_interleave', 1, 0), ('pe_interleave', 1, 1), ('pe_interleave', 1, 2), ('pe_interleave', 1, 3), ('transpose', 1),
+        ('transpose', 2), ('transpose', 3), ('fill', 0), ('fill', 1), ('fill', 2), ('fill', 3),
+        ('fill', 4), ('fill', 5), ('pe_interleave', 4, 0), ('fill', 6), ('fill', 7), ('pe_interleave', 4, 1),
+        ('pe_interleave', 4, 2), ('pe_interleave', 4, 3), ('pe_interleave', 7, 0), ('pe_interleave', 7, 1), ('pe_interleave', 7, 2), ('pe_interleave', 7, 3),
+        ('fill', 8), ('fill', 9), ('fill', 10), ('fill', 11), ('fill', 12), ('fill', 13),
+        ('fill', 14), ('fill', 15), ('fill', 16), ('fill', 17),
+    ],
+    'gpsimd': [
+        ('add', 0), ('add', 1), ('add', 2), ('add', 3), ('add', 4), ('add', 5),
+        ('add', 7), ('add', 8), ('add', 9), ('add', 10), ('add', 11), ('add', 12),
+        ('add', 13), ('add', 14), ('add', 15), ('add', 16), ('add', 17),
+    ],
+    'sync': [
+        ('store', 0), ('store', 1), ('store', 2), ('store', 3), ('store', 4), ('store', 5),
+        ('store', 6), ('store', 7), ('store', 8), ('store', 9), ('store', 10), ('store', 11),
+        ('store', 12), ('store', 13), ('store_v', 16), ('store_v', 17), ('store', 14), ('store', 15),
+        ('store', 16), ('store', 17),
+    ],
+}
+
+
+def make_queues(n_banks):
+    return QUEUES
 
 
 def tile_multiqueryattention_pa_kernel(tc, x, cos, sin, Wq_bytes, Wq_scale, Wk, Wv, out_0, out_1, out_2):
@@ -53,14 +111,14 @@ def tile_multiqueryattention_pa_kernel(tc, x, cos, sin, Wq_bytes, Wq_scale, Wk, 
 
     with ExitStack() as ctx:
         keep = ctx.enter_context(tc.tile_pool(name="keep", bufs=1))
-        wide_pool = ctx.enter_context(tc.tile_pool(name="wide", bufs=WIDE_BUFS))
-        interleaved_pool = ctx.enter_context(tc.tile_pool(name="interleaved", bufs=INTERLEAVED_BUFS))
+        wide_pool = ctx.enter_context(tc.tile_pool(name="wide", bufs=1))
+        interleaved_pool = ctx.enter_context(tc.tile_pool(name="interleaved", bufs=1))
         rotated_pool = ctx.enter_context(tc.tile_pool(name="rotated", bufs=ROTATED_BUFS))
         swapped_pool = ctx.enter_context(tc.tile_pool(name="swapped", bufs=SWAPPED_BUFS))
         stats_pool = ctx.enter_context(tc.tile_pool(name="stats", bufs=ROTATED_BUFS))
         scratch_pool = ctx.enter_context(tc.tile_pool(name="scratch", bufs=SCRATCH_BUFS))
         v_pool = ctx.enter_context(tc.tile_pool(name="v", bufs=2))
-        psum = ctx.enter_context(tc.psum_pool(name="psum", bufs=PSUM_BANKS))
+        psum = ctx.enter_context(tc.psum_pool(name="psum", bufs=BANK_BUFS))
         ctx.enter_context(tc.manual_schedule())
 
         x_rows = x[0].rearrange("(m p) k -> m p k", p=P)
@@ -75,6 +133,7 @@ def tile_multiqueryattention_pa_kernel(tc, x, cos, sin, Wq_bytes, Wq_scale, Wk, 
         v_out = out_2[0].rearrange("(m p) d -> p m d", p=P)
 
         identity = keep.tile([P, P], F32, name="identity")
+        identity_bf = keep.tile([P, P], BF16, name="identity_bf")
         one = keep.tile([P, 1], F32, name="one")
         warm_up = keep.tile([P, 1], F32, name="warm_up")
         unread_sums = keep.tile([P, SCRATCH_BUFS], F32, name="unread_sums")
@@ -95,6 +154,8 @@ def tile_multiqueryattention_pa_kernel(tc, x, cos, sin, Wq_bytes, Wq_scale, Wk, 
         kv_scales = keep.tile([P, PASSES, 2 * D], U8, name="kv_scales", align_bytes=64)
 
         make_identity(nc, identity[:])
+        if "P" in INTERLEAVE:
+            make_identity(nc, identity_bf[:])
         nc.vector.memset(one[:], 1.0)
         nc.scalar.activation(out=warm_up[:], in_=one[:], func=ACT.Abs_reciprocal_sqrt)
 
@@ -109,36 +170,26 @@ def tile_multiqueryattention_pa_kernel(tc, x, cos, sin, Wq_bytes, Wq_scale, Wk, 
         def load_x(m):
             nc.sync.dma_start(out=x_t[m][:], in_=x_rows[m])
 
+        def load_wk():
+            nc.sync.dma_start(out=wk_t[:].rearrange("p g t n -> p g (t n)"), in_=wk_planes)
+
+        def load_wv():
+            nc.sync.dma_start(out=wv_t[:].rearrange("p g t n -> p g (t n)"), in_=wv_planes)
+
+        def load_cos_sin():
+            nc.sync.dma_start(out=cos_t[:], in_=cos_rows)
+            nc.sync.dma_start(out=sin_t[:, :, 0, :], in_=sin_rows)
+
         nc.sync.dma_start(out=plane_scales[:], in_=wq_plane_scales)
         for t in range(PACK):
             load_plane(0, t)
-        load_unit(1)
-        load_unit(2)
-        load_x(0)
-        load_unit(3)
-        nc.sync.dma_start(out=wk_t[:].rearrange("p g t n -> p g (t n)"), in_=wk_planes)
-        load_unit(4)
-        load_x(1)
-        nc.sync.dma_start(out=wv_t[:].rearrange("p g t n -> p g (t n)"), in_=wv_planes)
-        load_unit(5)
-        load_x(2)
-        load_x(3)
-        nc.sync.dma_start(out=cos_t[:], in_=cos_rows)
-        nc.sync.dma_start(out=sin_t[:, :, 0, :], in_=sin_rows)
-        load_unit(6)
-        load_unit(7)
-
-        x_tiles_copied = set()
-        x_quantised = set()
-        units_quantised = set()
-        kv_quantised = set()
-        banks_filled = set()
-        banks_roped = set()
-        banks_read = set()
+        loaders = {"u": load_unit, "x": load_x, "k": load_wk, "v": load_wv, "c": load_cos_sin}
+        for item in LOAD_ORDER:
+            loaders[item[0]](*item[1:])
 
         x_transposed = {}
 
-        def x_transpose(m):
+        def transpose(m):
             words = x_t[m][:].bitcast(F32)
             for a in range(2):
                 x_transposed[(m, a)] = psum.tile([P, 2, 2, P], F32, name="bank", tag="bank")
@@ -155,47 +206,78 @@ def tile_multiqueryattention_pa_kernel(tc, x, cos, sin, Wq_bytes, Wq_scale, Wk, 
             words = x_interleaved[m][:].bitcast(F32).rearrange("p (g r w) -> p g r w", g=PASSES, w=2)
             for a in range(2):
                 nc.scalar.copy(out=words[:, 2 * a:2 * a + 2, :, :], in_=x_transposed[(m, a)][:].rearrange("p g w r -> p g r w"))
-                x_tiles_copied.add(2 * m + a)
 
         def x_quantise(m):
             nc.vector.quantize_mx(out=x_codes[m][:].bitcast(FP8X4), scales=x_scales[m][:], in_=x_interleaved[m][:])
-            x_quantised.add(m)
 
         wide = {}
         interleaved = {}
 
-        def on_vector(u, t):
-            return t >= PACK - VECTOR_WIDENS.get(u, 0)
+        def stream_of(u):
+            return [u in stream for stream in STREAMS].index(True)
+
+        def back(u, steps):
+            stream = STREAMS[stream_of(u)]
+            return [stream[stream.index(u) - steps]] if stream.index(u) >= steps else []
+
+        il_bank = {}
 
         def widen(u, t):
             half, g = divmod(u, PASSES)
             if u not in wide:
-                wide[u] = wide_pool.tile([P, PACK, UNIT_COLS], BF16, name="wide", tag="wide")
+                wide[u] = wide_pool.tile([P, PACK, UNIT_COLS], BF16, name="wide", tag="wide%d" % stream_of(u), bufs=WIDE_BUFS[stream_of(u)])
             codes = wq_bytes_t[half][:, g, t, :].bitcast(FP8)
             scale = plane_scales[:, g, t:t + 1]
-            if on_vector(u, t):
+            how = WIDEN[u][t]
+            if how == "B":
                 nc.vector.tensor_scalar(out=wide[u][:, t, :], in0=codes, scalar1=scale, scalar2=None, op0=ALU.mult)
-            else:
+            elif how == "A":
                 nc.scalar.activation(out=wide[u][:, t, :], in_=codes, func=ACT.Copy, scale=scale)
+            else:
+                nc.scalar.copy(out=wide[u][:, t, :], in_=codes)
 
-        def vector_widens(u):
-            for t in range(PACK):
-                if u < UNITS and on_vector(u, t):
-                    widen(u, t)
+        def scale_plane(u, t):
+            g = u % PASSES
+            nc.vector.tensor_scalar(out=wide[u][:, t, :], in0=wide[u][:, t, :], scalar1=plane_scales[:, g, t:t + 1], scalar2=None, op0=ALU.mult)
+
+        def new_interleaved(u):
+            interleaved[u] = interleaved_pool.tile(
+                [P, UNIT_COLS * PACK], BF16, name="interleaved", tag="interleaved%d" % stream_of(u), bufs=INTERLEAVED_BUFS[stream_of(u)], align_bytes=64
+            )
 
         def interleave(u):
-            interleaved[u] = interleaved_pool.tile([P, UNIT_COLS * PACK], BF16, name="interleaved", tag="interleaved", align_bytes=64)
+            new_interleaved(u)
             dst = interleaved[u][:].rearrange("p (c i t) -> p c t i", i=4, t=PACK)
             src = wide[u][:].rearrange("p t (c i) -> p c t i", i=4)
-            if u in SCALAR_INTERLEAVES:
+            if INTERLEAVE[u] == "S":
                 nc.scalar.copy(out=dst, in_=src)
             else:
                 nc.vector.tensor_copy(out=dst, in_=src)
 
+        def pe_interleave(u, b):
+            il_bank[(u, b)] = psum.tile([P, IL_COLS * PACK], BF16, name="il", tag="il", bufs=IL_BUFS)
+            for r in range(2):
+                n0 = b * IL_COLS + r * (IL_COLS // 2)
+                nc.tensor.matmul(
+                    out=il_bank[(u, b)][:, r * BANK_COLS:(r + 1) * BANK_COLS],
+                    lhsT=identity_bf[:],
+                    rhs=wide[u][:, :, n0:n0 + IL_COLS // 2].rearrange("p t n -> p n t"),
+                    start=True,
+                    stop=True,
+                )
+
+        def evacuate(u, b):
+            if b == 0:
+                new_interleaved(u)
+            dst = interleaved[u][:, b * IL_COLS * PACK:(b + 1) * IL_COLS * PACK]
+            if EVACUATE[u][b] == "S":
+                nc.scalar.copy(out=dst, in_=il_bank[(u, b)][:])
+            else:
+                nc.vector.tensor_copy(out=dst, in_=il_bank[(u, b)][:])
+
         def quantise(u):
             half, g = divmod(u, PASSES)
             nc.vector.quantize_mx(out=wq_codes[half][:, g, :].bitcast(FP8X4), scales=wq_scales[half][:, g, :], in_=interleaved[u][:])
-            units_quantised.add(u)
 
         def kv_interleave(which):
             planes = wk_t if which == 0 else wv_t
@@ -207,7 +289,6 @@ def tile_multiqueryattention_pa_kernel(tc, x, cos, sin, Wq_bytes, Wq_scale, Wk, 
                 scales=kv_scales[:].rearrange("p g n -> p (g n)"),
                 in_=kv_interleaved[:].rearrange("p g n t -> p (g n t)"),
             )
-            kv_quantised.add(0)
 
         bank_t = {}
 
@@ -223,15 +304,6 @@ def tile_multiqueryattention_pa_kernel(tc, x, cos, sin, Wq_bytes, Wq_scale, Wk, 
                     stop=(g == PASSES - 1),
                 )
 
-        def can_fill(i):
-            buffer_free = (i in x_tiles_copied) if i < PSUM_BANKS else (i - PSUM_BANKS in banks_read)
-            if banks[i][0] == "q":
-                block, m = banks[i][1:]
-                first_unit = (block // BANKS_PER_UNIT) * PASSES
-                return buffer_free and m in x_quantised and all(first_unit + g in units_quantised for g in range(PASSES))
-            pair = banks[i][1]
-            return buffer_free and 0 in kv_quantised and 2 * pair in x_quantised and 2 * pair + 1 in x_quantised
-
         def fill(i):
             bank_t[i] = psum.tile([P, BANK_COLS], F32, name="bank", tag="bank")
             if banks[i][0] == "q":
@@ -243,23 +315,19 @@ def tile_multiqueryattention_pa_kernel(tc, x, cos, sin, Wq_bytes, Wq_scale, Wk, 
                 pair = banks[i][1]
                 for r in range(2):
                     matmul_passes(bank_t[i][:, r * 2 * D:(r + 1) * 2 * D], 2 * pair + r, kv_codes, kv_scales)
-            banks_filled.add(i)
-
-        def fill_ready():
-            for i in range(n_banks):
-                if i not in banks_filled and (i == 0 or i - 1 in banks_filled) and can_fill(i):
-                    fill(i)
 
         rotated = {}
         swapped = {}
+        v_tiles = {}
 
         def heads_of(i):
             return BANK_COLS // D if banks[i][0] == "q" else 2
 
+        def negate_sin():
+            nc.vector.tensor_scalar(out=sin_t[:, :, 1, :], in0=sin_t[:, :, 0, :], scalar1=-1.0, scalar2=None, op0=ALU.mult)
+
         def rope(i):
             heads = heads_of(i)
-            if not banks_roped:
-                nc.vector.tensor_scalar(out=sin_t[:, :, 1, :], in0=sin_t[:, :, 0, :], scalar1=-1.0, scalar2=None, op0=ALU.mult)
             if banks[i][0] == "q":
                 m = banks[i][2]
                 halves = bank_t[i][:].rearrange("p (h w j) -> p h w j", w=2, j=HALF)
@@ -278,11 +346,9 @@ def tile_multiqueryattention_pa_kernel(tc, x, cos, sin, Wq_bytes, Wq_scale, Wk, 
             if banks[i][0] == "kv":
                 v_t = v_pool.tile([P, 2, D], F32, name="v_t", tag="v_t")
                 nc.vector.tensor_copy(out=v_t[:], in_=bank_t[i][:].rearrange("p (h e d) -> p h e d", e=2, d=D)[:, :, 1, :])
-                nc.sync.dma_start(out=v_out[:, 2 * pair:2 * pair + 2, :], in_=v_t[:])
-            banks_roped.add(i)
-            banks_read.add(i)
+                v_tiles[i] = v_t
 
-        def rope_add(i):
+        def add(i):
             width = heads_of(i) * D
             engine = nc.vector if i in VECTOR_ADDS else nc.gpsimd
             engine.tensor_tensor(out=rotated[i][:, 0:width], in0=rotated[i][:, 0:width], in1=swapped[i][:, 0:width], op=ALU.add)
@@ -304,12 +370,15 @@ def tile_multiqueryattention_pa_kernel(tc, x, cos, sin, Wq_bytes, Wq_scale, Wk, 
             inverse_rms[i] = stats_pool.tile([P, BANK_COLS // D], F32, name="inverse_rms", tag="inverse_rms")
             nc.scalar.activation(out=inverse_rms[i][:, 0:heads], in_=square_sums[i][:, 0:heads], func=ACT.Abs_reciprocal_sqrt, scale=1.0 / D, bias=EPS)
 
+        def vector_heads(i):
+            return VECTOR_SCALED_HEADS.get(i, VECTOR_SCALED_HEADS_DEFAULT)
+
         def scalar_scales(i):
-            for h in range(heads_of(i) - VECTOR_SCALED_HEADS):
+            for h in range(heads_of(i) - vector_heads(i)):
                 nc.scalar.activation(out=rotated[i][:, head_cols(h)], in_=rotated[i][:, head_cols(h)], func=ACT.Copy, scale=inverse_rms[i][:, h:h + 1])
 
-        def finish(i):
-            for h in range(heads_of(i) - VECTOR_SCALED_HEADS, heads_of(i)):
+        def vector_scales(i):
+            for h in range(heads_of(i) - vector_heads(i), heads_of(i)):
                 nc.vector.tensor_scalar(
                     out=rotated[i][:, head_cols(h)],
                     in0=rotated[i][:, head_cols(h)],
@@ -319,6 +388,8 @@ def tile_multiqueryattention_pa_kernel(tc, x, cos, sin, Wq_bytes, Wq_scale, Wk, 
                     op1=ALU.add,
                     accum_out=unread_sums[:, i % SCRATCH_BUFS:i % SCRATCH_BUFS + 1],
                 )
+
+        def store(i):
             if banks[i][0] == "q":
                 block, m = banks[i][1:]
                 nc.sync.dma_start(out=q_out[m][:, block * BANK_COLS:(block + 1) * BANK_COLS], in_=rotated[i][:])
@@ -326,51 +397,111 @@ def tile_multiqueryattention_pa_kernel(tc, x, cos, sin, Wq_bytes, Wq_scale, Wk, 
                 pair = banks[i][1]
                 nc.sync.dma_start(out=k_out[:, 2 * pair:2 * pair + 2, :], in_=rotated[i][:, 0:2 * D].rearrange("p (h d) -> p h d", d=D))
 
-        for m in range(TOKEN_TILES):
-            x_transpose(m)
+        def store_v(i):
+            pair = banks[i][1]
+            nc.sync.dma_start(out=v_out[:, 2 * pair:2 * pair + 2, :], in_=v_tiles[i][:])
 
-        for s in range(UNITS + 1):
-            if s < UNITS:
-                for t in range(PACK):
-                    if not on_vector(s, t):
-                        widen(s, t)
-                    if t == PACK - 1 and s in SCALAR_INTERLEAVES:
-                        interleave(s)
-                    for m in range(TOKEN_TILES):
-                        if X_COPY_AFTER_PLANE[m] == PACK * s + t:
-                            x_copy(m)
-            if s == 0:
-                vector_widens(0)
-            vector_widens(s + 1)
-            if s < UNITS and s not in SCALAR_INTERLEAVES:
-                interleave(s)
-            if s >= 1:
-                quantise(s - 1)
-                for m in range(TOKEN_TILES):
-                    if X_QUANT_AFTER_UNIT[m] == s - 1:
-                        x_quantise(m)
-                for which in range(2):
-                    if KV_INTERLEAVE_AFTER_UNIT[which] == s - 1:
-                        kv_interleave(which)
-                if KV_QUANT_AFTER_UNIT == s - 1:
-                    kv_quantise()
-                fill_ready()
-                for i in ROPE_AFTER_UNIT.get(s - 1, ()):
-                    rope(i)
-                for i in ROPE_AFTER_UNIT.get(s - 1, ()):
-                    rope_add(i)
-            fill_ready()
+        actions = {
+            "store_v": store_v,
+            "transpose": transpose, "x_copy": x_copy, "x_quantise": x_quantise, "widen": widen, "scale_plane": scale_plane,
+            "interleave": interleave, "pe_interleave": pe_interleave, "evacuate": evacuate, "quantise": quantise,
+            "kv_interleave": kv_interleave, "kv_quantise": kv_quantise, "fill": fill, "negate_sin": negate_sin, "rope": rope, "add": add,
+            "sum_squares": sum_squares, "take_inverse_rms": take_inverse_rms, "scalar_scales": scalar_scales,
+            "vector_scales": vector_scales, "store": store,
+        }
 
-        for i in range(n_banks + FINISH_LAG):
-            if i < n_banks and i not in banks_roped:
-                rope(i)
-                rope_add(i)
-            if i >= FINISH_LAG:
-                finish(i - FINISH_LAG)
-            if 2 <= i < n_banks + 2:
-                take_inverse_rms(i - 2)
-            if 1 <= i < n_banks + 1:
-                sum_squares(i - 1)
-            if 2 <= i < n_banks + 2:
-                scalar_scales(i - 2)
-            fill_ready()
+        queues = make_queues(n_banks)
+        il_jobs = [job for job in queues["tensor"] if job[0] == "pe_interleave"]
+
+        def planes_ready(u):
+            return [("scale_plane", u, t) if WIDEN[u][t] == "C" else ("widen", u, t) for t in range(PACK)]
+
+        def planes_read(u):
+            return [("pe_interleave", u, b) for b in range(IL_PARTS)] if INTERLEAVE[u] == "P" else [("interleave", u)]
+
+        def interleaved_made(u):
+            return [("evacuate", u, b) for b in range(IL_PARTS)] if INTERLEAVE[u] == "P" else [("interleave", u)]
+
+        def bank_buffer_free(index):
+            before = index - BANK_BUFS
+            if before < 0:
+                return []
+            if before < 2 * TOKEN_TILES:
+                return [("x_copy", before // 2)]
+            return [("rope", before - 2 * TOKEN_TILES)]
+
+        def needs(job):
+            kind = job[0]
+            if kind == "transpose":
+                return bank_buffer_free(2 * job[1]) + bank_buffer_free(2 * job[1] + 1) + ([("transpose", job[1] - 1)] if job[1] else [])
+            if kind == "x_copy":
+                return [("transpose", job[1])]
+            if kind == "x_quantise":
+                return [("x_copy", job[1])]
+            if kind == "widen":
+                u = job[1]
+                out = [("widen", v, t) for v in back(u, 1) for t in range(PACK)]
+                for v in back(u, WIDE_BUFS[stream_of(u)]):
+                    out = out + planes_read(v)
+                return out
+            if kind == "scale_plane":
+                return [("widen", job[1], job[2])]
+            if kind == "interleave" or (kind == "evacuate" and job[2] == 0):
+                u = job[1]
+                out = planes_ready(u) if kind == "interleave" else [("pe_interleave", u, 0)]
+                for v in back(u, 1):
+                    out = out + interleaved_made(v)[0:1]
+                return out + [("quantise", v) for v in back(u, INTERLEAVED_BUFS[stream_of(u)])]
+            if kind == "evacuate":
+                return [("pe_interleave", job[1], job[2]), ("evacuate", job[1], 0)]
+            if kind == "pe_interleave":
+                index = il_jobs.index(job)
+                out = planes_ready(job[1]) + ([il_jobs[index - 1]] if index else [])
+                return out + ([("evacuate",) + il_jobs[index - IL_BUFS][1:]] if index >= IL_BUFS else [])
+            if kind == "quantise":
+                return interleaved_made(job[1])
+            if kind == "kv_quantise":
+                return [("kv_interleave", 0), ("kv_interleave", 1)]
+            if kind == "fill":
+                i = job[1]
+                out = bank_buffer_free(2 * TOKEN_TILES + i) + ([("fill", i - 1)] if i else [("transpose", TOKEN_TILES - 1)])
+                if banks[i][0] == "q":
+                    block, m = banks[i][1:]
+                    first_unit = (block // BANKS_PER_UNIT) * PASSES
+                    return out + [("x_quantise", m)] + [("quantise", first_unit + g) for g in range(PASSES)]
+                return out + [("kv_quantise",), ("x_quantise", 2 * banks[i][1]), ("x_quantise", 2 * banks[i][1] + 1)]
+            if kind == "rope":
+                i = job[1]
+                out = [("fill", i), ("negate_sin",)] + ([("rope", i - 1)] if i else [])
+                out = out + ([("store", i - ROTATED_BUFS)] if i >= ROTATED_BUFS else [])
+                return out + ([("add", i - SWAPPED_BUFS)] if i >= SWAPPED_BUFS else [])
+            if kind == "add":
+                return [("rope", job[1])]
+            if kind == "sum_squares":
+                return [("add", job[1])]
+            if kind == "take_inverse_rms":
+                return [("sum_squares", job[1])]
+            if kind == "vector_scales" and vector_heads(job[1]) == 0:
+                return []
+            if kind in ("scalar_scales", "vector_scales"):
+                return [("take_inverse_rms", job[1])]
+            if kind == "store_v":
+                return [("rope", job[1])]
+            if kind == "store":
+                return [("scalar_scales", job[1]), ("vector_scales", job[1])] + ([("store", job[1] - 1)] if job[1] else [])
+            return []
+
+        written = set()
+        place = dict((name, 0) for name in queues)
+        left = sum(len(queues[name]) for name in queues)
+        while left:
+            moved = False
+            for name in QUEUE_NAMES:
+                while place[name] < len(queues[name]) and all(need in written for need in needs(queues[name][place[name]])):
+                    job = queues[name][place[name]]
+                    actions[job[0]](*job[1:])
+                    written.add(job)
+                    place[name] += 1
+                    left -= 1
+                    moved = True
+            assert moved, "the queues wait for each other: %s" % str([queues[name][place[name]] for name in QUEUE_NAMES if place[name] < len(queues[name])])

@@ -28,62 +28,61 @@ IL_PARTS = UNIT_COLS // IL_COLS
 
 FLOPS = 2 * TOKENS * DIM * (HEADS * D + 2 * D)
 
-WIDEN = ('AABB', 'AAAA', 'AABB', 'ABBB', 'AAAA', 'AAAB', 'AABB', 'AAAA')
-INTERLEAVE = 'VPVVPVVP'
+WIDEN = ('AABB', 'ABBB', 'ABBB', 'AAAA', 'AABB', 'AAAB', 'AAAB', 'AAAA')
+INTERLEAVE = 'VVVVVPVP'
 EVACUATE = ('SSSS', 'SSSS', 'SSSS', 'SSSS', 'SSSS', 'SSSS', 'SSSS', 'SSSS')
-STREAMS = ((0, 3, 2, 5, 6), (1, 4, 7))
+STREAMS = ((0, 2, 1, 4, 3, 6), (5, 7))
 VECTOR_ADDS = (6,)
-VECTOR_SCALED_HEADS = {0: 0, 1: 0, 2: 0, 3: 0, 4: 0, 5: 0, 6: 0, 7: 0, 8: 1, 9: 1, 10: 1, 11: 1, 12: 1, 13: 1, 14: 1, 15: 1, 16: 1, 17: 1}
+KV_INTERLEAVE = 'SS'
+VECTOR_SCALED_HEADS = {0: 0, 1: 0, 2: 0, 3: 0, 4: 0, 5: 0, 6: 1, 7: 0, 8: 1, 9: 1, 10: 0, 11: 1, 12: 2, 13: 2, 14: 2, 15: 1, 16: 1, 17: 1}
 VECTOR_SCALED_HEADS_DEFAULT = 0
-LOAD_ORDER = (('u', 1), ('u', 3), ('u', 2), ('x', 0), ('c',), ('u', 5), ('k',), ('u', 6), ('u', 4), ('x', 1), ('u', 7), ('x', 2), ('x', 3), ('v',))
+LOAD_ORDER = (('u', 5), ('u', 2), ('u', 7), ('u', 3), ('u', 1), ('x', 0), ('x', 1), ('x', 2), ('x', 3), ('u', 6), ('c',), ('u', 4), ('k',), ('v',))
 WIDE_BUFS = (2, 2)
 INTERLEAVED_BUFS = (2, 2)
 ROTATED_BUFS = 8
 SWAPPED_BUFS = 3
 SCRATCH_BUFS = 8
-BANK_BUFS = 6
+BANK_BUFS = 8
 IL_BUFS = 2
 QUEUE_NAMES = ("scalar", "vector", "tensor", "gpsimd", "sync")
 QUEUES = {
     'scalar': [
-        ('widen', 0, 0), ('widen', 0, 1), ('widen', 1, 0), ('widen', 1, 1), ('widen', 1, 2), ('widen', 1, 3),
-        ('widen', 3, 0), ('x_copy', 0), ('evacuate', 1, 0), ('evacuate', 1, 1), ('evacuate', 1, 2), ('evacuate', 1, 3),
-        ('widen', 2, 0), ('widen', 2, 1), ('widen', 4, 0), ('x_copy', 1), ('widen', 5, 0), ('widen', 5, 1),
-        ('x_copy', 2), ('x_copy', 3), ('widen', 5, 2), ('widen', 6, 0), ('widen', 6, 1), ('widen', 4, 1),
-        ('widen', 4, 2), ('widen', 4, 3), ('widen', 7, 0), ('evacuate', 4, 0), ('widen', 7, 1), ('widen', 7, 2),
-        ('evacuate', 4, 1), ('evacuate', 4, 2), ('evacuate', 4, 3), ('widen', 7, 3), ('sum_squares', 0), ('evacuate', 7, 0),
-        ('evacuate', 7, 1), ('evacuate', 7, 2), ('evacuate', 7, 3), ('take_inverse_rms', 0), ('sum_squares', 1), ('scalar_scales', 0),
-        ('take_inverse_rms', 1), ('sum_squares', 2), ('scalar_scales', 1), ('take_inverse_rms', 2), ('sum_squares', 3), ('scalar_scales', 2),
-        ('take_inverse_rms', 3), ('sum_squares', 4), ('scalar_scales', 3), ('take_inverse_rms', 4), ('sum_squares', 5), ('scalar_scales', 4),
-        ('take_inverse_rms', 5), ('sum_squares', 6), ('scalar_scales', 5), ('take_inverse_rms', 6), ('sum_squares', 7), ('scalar_scales', 6),
-        ('take_inverse_rms', 7), ('sum_squares', 8), ('scalar_scales', 7), ('take_inverse_rms', 8), ('sum_squares', 9), ('scalar_scales', 8),
-        ('take_inverse_rms', 9), ('sum_squares', 10), ('scalar_scales', 9), ('take_inverse_rms', 10), ('sum_squares', 11), ('scalar_scales', 10),
-        ('take_inverse_rms', 11), ('sum_squares', 12), ('scalar_scales', 11), ('take_inverse_rms', 12), ('sum_squares', 13), ('scalar_scales', 12),
-        ('take_inverse_rms', 13), ('sum_squares', 14), ('scalar_scales', 13), ('take_inverse_rms', 14), ('sum_squares', 15), ('scalar_scales', 14),
-        ('take_inverse_rms', 15), ('sum_squares', 16), ('scalar_scales', 15), ('take_inverse_rms', 16), ('sum_squares', 17), ('scalar_scales', 16),
-        ('take_inverse_rms', 17), ('scalar_scales', 17),
+        ('widen', 0, 0), ('widen', 0, 1), ('widen', 5, 0), ('widen', 5, 1), ('widen', 2, 0), ('widen', 5, 2),
+        ('widen', 7, 0), ('widen', 1, 0), ('widen', 7, 1), ('widen', 7, 2), ('evacuate', 5, 0), ('widen', 7, 3),
+        ('x_copy', 0), ('x_copy', 1), ('x_copy', 2), ('x_copy', 3), ('widen', 4, 0), ('evacuate', 5, 1),
+        ('widen', 4, 1), ('evacuate', 5, 2), ('widen', 3, 0), ('widen', 3, 1), ('evacuate', 5, 3), ('widen', 3, 2),
+        ('widen', 3, 3), ('evacuate', 7, 0), ('widen', 6, 0), ('evacuate', 7, 1), ('widen', 6, 1), ('widen', 6, 2),
+        ('evacuate', 7, 2), ('evacuate', 7, 3), ('kv_interleave', 0), ('kv_interleave', 1), ('sum_squares', 0), ('sum_squares', 1),
+        ('take_inverse_rms', 0), ('take_inverse_rms', 1), ('scalar_scales', 0), ('scalar_scales', 1), ('sum_squares', 2), ('sum_squares', 3),
+        ('take_inverse_rms', 2), ('take_inverse_rms', 3), ('scalar_scales', 2), ('scalar_scales', 3), ('sum_squares', 4), ('sum_squares', 5),
+        ('take_inverse_rms', 4), ('take_inverse_rms', 5), ('scalar_scales', 4), ('scalar_scales', 5), ('sum_squares', 6), ('sum_squares', 7),
+        ('take_inverse_rms', 6), ('take_inverse_rms', 7), ('scalar_scales', 6), ('scalar_scales', 7), ('sum_squares', 8), ('sum_squares', 9),
+        ('take_inverse_rms', 8), ('take_inverse_rms', 9), ('scalar_scales', 8), ('scalar_scales', 9), ('sum_squares', 10), ('sum_squares', 11),
+        ('take_inverse_rms', 10), ('take_inverse_rms', 11), ('scalar_scales', 10), ('scalar_scales', 11), ('sum_squares', 12), ('sum_squares', 13),
+        ('take_inverse_rms', 12), ('take_inverse_rms', 13), ('scalar_scales', 12), ('scalar_scales', 13), ('sum_squares', 14), ('sum_squares', 15),
+        ('take_inverse_rms', 14), ('take_inverse_rms', 15), ('scalar_scales', 14), ('scalar_scales', 15), ('sum_squares', 16), ('sum_squares', 17),
+        ('take_inverse_rms', 16), ('take_inverse_rms', 17), ('scalar_scales', 16), ('scalar_scales', 17),
     ],
     'vector': [
         ('vector_scales', 0), ('vector_scales', 1), ('vector_scales', 2), ('vector_scales', 3), ('vector_scales', 4), ('vector_scales', 5),
-        ('vector_scales', 6), ('vector_scales', 7), ('widen', 0, 2), ('widen', 0, 3), ('interleave', 0), ('widen', 3, 1),
-        ('quantise', 0), ('widen', 3, 2), ('negate_sin',), ('widen', 3, 3), ('widen', 2, 2), ('interleave', 3),
-        ('x_quantise', 0), ('quantise', 3), ('quantise', 1), ('widen', 2, 3), ('widen', 5, 3), ('interleave', 2),
-        ('x_quantise', 1), ('quantise', 2), ('x_quantise', 2), ('kv_interleave', 0), ('x_quantise', 3), ('interleave', 5),
-        ('widen', 6, 2), ('quantise', 5), ('rope', 0), ('rope', 1), ('rope', 2), ('rope', 3),
-        ('rope', 4), ('rope', 5), ('rope', 6), ('rope', 7), ('add', 6), ('widen', 6, 3),
-        ('quantise', 4), ('interleave', 6), ('quantise', 7), ('quantise', 6), ('kv_interleave', 1), ('rope', 8),
-        ('rope', 9), ('rope', 10), ('rope', 11), ('rope', 12), ('vector_scales', 8), ('rope', 13),
-        ('vector_scales', 9), ('rope', 14), ('vector_scales', 10), ('rope', 15), ('vector_scales', 11), ('kv_quantise',),
-        ('vector_scales', 12), ('vector_scales', 13), ('rope', 16), ('vector_scales', 14), ('rope', 17), ('vector_scales', 15),
-        ('vector_scales', 16), ('vector_scales', 17),
+        ('widen', 0, 2), ('widen', 0, 3), ('interleave', 0), ('widen', 2, 1), ('quantise', 0), ('widen', 2, 2),
+        ('widen', 2, 3), ('widen', 5, 3), ('interleave', 2), ('widen', 1, 1), ('quantise', 2), ('widen', 1, 2),
+        ('widen', 1, 3), ('interleave', 1), ('x_quantise', 0), ('x_quantise', 1), ('x_quantise', 2), ('x_quantise', 3),
+        ('negate_sin',), ('quantise', 1), ('widen', 4, 2), ('widen', 4, 3), ('interleave', 4), ('quantise', 5),
+        ('quantise', 4), ('interleave', 3), ('widen', 6, 3), ('quantise', 3), ('interleave', 6), ('quantise', 7),
+        ('rope', 0), ('rope', 1), ('rope', 2), ('rope', 3), ('rope', 4), ('rope', 5),
+        ('rope', 6), ('rope', 7), ('add', 6), ('quantise', 6), ('kv_quantise',), ('rope', 8),
+        ('rope', 9), ('rope', 10), ('vector_scales', 6), ('vector_scales', 7), ('rope', 11), ('rope', 12),
+        ('vector_scales', 8), ('vector_scales', 9), ('vector_scales', 10), ('rope', 13), ('rope', 14), ('vector_scales', 11),
+        ('rope', 15), ('rope', 16), ('vector_scales', 12), ('vector_scales', 13), ('rope', 17), ('vector_scales', 14),
+        ('vector_scales', 15), ('vector_scales', 16), ('vector_scales', 17),
     ],
     'tensor': [
-        ('transpose', 0), ('pe_interleave', 1, 0), ('pe_interleave', 1, 1), ('pe_interleave', 1, 2), ('pe_interleave', 1, 3), ('transpose', 1),
-        ('transpose', 2), ('transpose', 3), ('fill', 0), ('fill', 1), ('fill', 2), ('fill', 3),
-        ('fill', 4), ('fill', 5), ('pe_interleave', 4, 0), ('fill', 6), ('fill', 7), ('pe_interleave', 4, 1),
-        ('pe_interleave', 4, 2), ('pe_interleave', 4, 3), ('pe_interleave', 7, 0), ('pe_interleave', 7, 1), ('pe_interleave', 7, 2), ('pe_interleave', 7, 3),
-        ('fill', 8), ('fill', 9), ('fill', 10), ('fill', 11), ('fill', 12), ('fill', 13),
-        ('fill', 14), ('fill', 15), ('fill', 16), ('fill', 17),
+        ('pe_interleave', 5, 0), ('transpose', 0), ('transpose', 1), ('transpose', 2), ('transpose', 3), ('pe_interleave', 5, 1),
+        ('pe_interleave', 5, 2), ('pe_interleave', 5, 3), ('pe_interleave', 7, 0), ('pe_interleave', 7, 1), ('pe_interleave', 7, 2), ('pe_interleave', 7, 3),
+        ('fill', 0), ('fill', 1), ('fill', 2), ('fill', 3), ('fill', 4), ('fill', 5),
+        ('fill', 6), ('fill', 7), ('fill', 8), ('fill', 9), ('fill', 10), ('fill', 11),
+        ('fill', 12), ('fill', 13), ('fill', 14), ('fill', 15), ('fill', 16), ('fill', 17),
     ],
     'gpsimd': [
         ('add', 0), ('add', 1), ('add', 2), ('add', 3), ('add', 4), ('add', 5),
@@ -93,7 +92,7 @@ QUEUES = {
     'sync': [
         ('store', 0), ('store', 1), ('store', 2), ('store', 3), ('store', 4), ('store', 5),
         ('store', 6), ('store', 7), ('store', 8), ('store', 9), ('store', 10), ('store', 11),
-        ('store', 12), ('store', 13), ('store_v', 16), ('store_v', 17), ('store', 14), ('store', 15),
+        ('store_v', 16), ('store', 12), ('store', 13), ('store_v', 17), ('store', 14), ('store', 15),
         ('store', 16), ('store', 17),
     ],
 }
@@ -255,7 +254,7 @@ def tile_multiqueryattention_pa_kernel(tc, x, cos, sin, Wq_bytes, Wq_scale, Wk, 
                 nc.vector.tensor_copy(out=dst, in_=src)
 
         def pe_interleave(u, b):
-            il_bank[(u, b)] = psum.tile([P, IL_COLS * PACK], BF16, name="il", tag="il", bufs=IL_BUFS)
+            il_bank[(u, b)] = psum.tile([P, IL_COLS * PACK], BF16, name="bank", tag="bank")
             for r in range(2):
                 n0 = b * IL_COLS + r * (IL_COLS // 2)
                 nc.tensor.matmul(
@@ -281,7 +280,10 @@ def tile_multiqueryattention_pa_kernel(tc, x, cos, sin, Wq_bytes, Wq_scale, Wk, 
 
         def kv_interleave(which):
             planes = wk_t if which == 0 else wv_t
-            nc.vector.tensor_copy(out=kv_interleaved[:, :, which * D:(which + 1) * D, :], in_=planes[:].rearrange("p g t n -> p g n t"))
+            if KV_INTERLEAVE[which] == "S":
+                nc.scalar.copy(out=kv_interleaved[:, :, which * D:(which + 1) * D, :], in_=planes[:].rearrange("p g t n -> p g n t"))
+            else:
+                nc.vector.tensor_copy(out=kv_interleaved[:, :, which * D:(which + 1) * D, :], in_=planes[:].rearrange("p g t n -> p g n t"))
 
         def kv_quantise():
             nc.vector.quantize_mx(
@@ -411,7 +413,19 @@ def tile_multiqueryattention_pa_kernel(tc, x, cos, sin, Wq_bytes, Wq_scale, Wk, 
         }
 
         queues = make_queues(n_banks)
-        il_jobs = [job for job in queues["tensor"] if job[0] == "pe_interleave"]
+        tile_readers = []
+        first_tile = {}
+        for job in queues["tensor"]:
+            first_tile[job] = len(tile_readers)
+            if job[0] == "transpose":
+                tile_readers.extend([("x_copy", job[1])] * 2)
+            elif job[0] == "pe_interleave":
+                tile_readers.append(("evacuate",) + job[1:])
+            else:
+                tile_readers.append(("rope", job[1]))
+
+        def buffers_free(job, tiles):
+            return [tile_readers[first_tile[job] + k - BANK_BUFS] for k in range(tiles) if first_tile[job] + k >= BANK_BUFS]
 
         def planes_ready(u):
             return [("scale_plane", u, t) if WIDEN[u][t] == "C" else ("widen", u, t) for t in range(PACK)]
@@ -422,18 +436,10 @@ def tile_multiqueryattention_pa_kernel(tc, x, cos, sin, Wq_bytes, Wq_scale, Wk, 
         def interleaved_made(u):
             return [("evacuate", u, b) for b in range(IL_PARTS)] if INTERLEAVE[u] == "P" else [("interleave", u)]
 
-        def bank_buffer_free(index):
-            before = index - BANK_BUFS
-            if before < 0:
-                return []
-            if before < 2 * TOKEN_TILES:
-                return [("x_copy", before // 2)]
-            return [("rope", before - 2 * TOKEN_TILES)]
-
         def needs(job):
             kind = job[0]
             if kind == "transpose":
-                return bank_buffer_free(2 * job[1]) + bank_buffer_free(2 * job[1] + 1) + ([("transpose", job[1] - 1)] if job[1] else [])
+                return buffers_free(job, 2)
             if kind == "x_copy":
                 return [("transpose", job[1])]
             if kind == "x_quantise":
@@ -455,16 +461,14 @@ def tile_multiqueryattention_pa_kernel(tc, x, cos, sin, Wq_bytes, Wq_scale, Wk, 
             if kind == "evacuate":
                 return [("pe_interleave", job[1], job[2]), ("evacuate", job[1], 0)]
             if kind == "pe_interleave":
-                index = il_jobs.index(job)
-                out = planes_ready(job[1]) + ([il_jobs[index - 1]] if index else [])
-                return out + ([("evacuate",) + il_jobs[index - IL_BUFS][1:]] if index >= IL_BUFS else [])
+                return planes_ready(job[1]) + buffers_free(job, 1)
             if kind == "quantise":
                 return interleaved_made(job[1])
             if kind == "kv_quantise":
                 return [("kv_interleave", 0), ("kv_interleave", 1)]
             if kind == "fill":
                 i = job[1]
-                out = bank_buffer_free(2 * TOKEN_TILES + i) + ([("fill", i - 1)] if i else [("transpose", TOKEN_TILES - 1)])
+                out = buffers_free(job, 1)
                 if banks[i][0] == "q":
                     block, m = banks[i][1:]
                     first_unit = (block // BANKS_PER_UNIT) * PASSES

@@ -28,15 +28,18 @@ IL_PARTS = UNIT_COLS // IL_COLS
 
 FLOPS = 2 * TOKENS * DIM * (HEADS * D + 2 * D)
 
-WIDEN = ('AABB', 'ABBB', 'ABBB', 'AAAA', 'AABB', 'AAAB', 'AAAB', 'AAAA')
-INTERLEAVE = 'VVVVVPVP'
-EVACUATE = ('SSSS', 'SSSS', 'SSSS', 'SSSS', 'SSSS', 'SSSS', 'SSSS', 'SSSS')
-STREAMS = ((0, 2, 1, 4, 3, 6), (5, 7))
-VECTOR_ADDS = (6,)
-KV_INTERLEAVE = 'SS'
-VECTOR_SCALED_HEADS = {0: 0, 1: 0, 2: 0, 3: 0, 4: 0, 5: 0, 6: 1, 7: 0, 8: 1, 9: 1, 10: 0, 11: 1, 12: 2, 13: 2, 14: 2, 15: 1, 16: 1, 17: 1}
-VECTOR_SCALED_HEADS_DEFAULT = 0
-LOAD_ORDER = (('u', 5), ('u', 2), ('u', 7), ('u', 3), ('u', 1), ('x', 0), ('x', 1), ('x', 2), ('x', 3), ('u', 6), ('c',), ('u', 4), ('k',), ('v',))
+WIDEN = ("AABB", "AAAA", "AABB", "AAAA", "AABB", "AABB", "AABB", "AABB")
+INTERLEAVE = "VPVPVVVV"
+EVACUATE = ("SSSS",) * 8
+STREAMS = ((0, 2, 4, 5, 6, 7), (1, 3))
+VECTOR_ADDS = ()
+KV_INTERLEAVE = "SS"
+FIRST_SHARED_BANK = 4
+VECTOR_SCALED_HEADS = dict((i, 0) for i in range(FIRST_SHARED_BANK))
+VECTOR_SCALED_HEADS_DEFAULT = 1
+FINISH_LAG = 3
+KV_QUANTISE_AFTER_ROPE = 7
+LOAD_ORDER = (("u", 2), ("u", 1), ("u", 4), ("u", 5), ("u", 3), ("u", 6), ("x", 0), ("x", 1), ("u", 7), ("x", 2), ("x", 3), ("k",), ("v",), ("c",))
 WIDE_BUFS = (2, 2)
 INTERLEAVED_BUFS = (2, 2)
 ROTATED_BUFS = 8
@@ -45,61 +48,53 @@ SCRATCH_BUFS = 8
 BANK_BUFS = 8
 IL_BUFS = 2
 QUEUE_NAMES = ("scalar", "vector", "tensor", "gpsimd", "sync")
-QUEUES = {
-    'scalar': [
-        ('widen', 0, 0), ('widen', 0, 1), ('widen', 5, 0), ('widen', 5, 1), ('widen', 2, 0), ('widen', 5, 2),
-        ('widen', 7, 0), ('widen', 1, 0), ('widen', 7, 1), ('widen', 7, 2), ('evacuate', 5, 0), ('widen', 7, 3),
-        ('x_copy', 0), ('x_copy', 1), ('x_copy', 2), ('x_copy', 3), ('widen', 4, 0), ('evacuate', 5, 1),
-        ('widen', 4, 1), ('evacuate', 5, 2), ('widen', 3, 0), ('widen', 3, 1), ('evacuate', 5, 3), ('widen', 3, 2),
-        ('widen', 3, 3), ('evacuate', 7, 0), ('widen', 6, 0), ('evacuate', 7, 1), ('widen', 6, 1), ('widen', 6, 2),
-        ('evacuate', 7, 2), ('evacuate', 7, 3), ('kv_interleave', 0), ('kv_interleave', 1), ('sum_squares', 0), ('sum_squares', 1),
-        ('take_inverse_rms', 0), ('take_inverse_rms', 1), ('scalar_scales', 0), ('scalar_scales', 1), ('sum_squares', 2), ('sum_squares', 3),
-        ('take_inverse_rms', 2), ('take_inverse_rms', 3), ('scalar_scales', 2), ('scalar_scales', 3), ('sum_squares', 4), ('sum_squares', 5),
-        ('take_inverse_rms', 4), ('take_inverse_rms', 5), ('scalar_scales', 4), ('scalar_scales', 5), ('sum_squares', 6), ('sum_squares', 7),
-        ('take_inverse_rms', 6), ('take_inverse_rms', 7), ('scalar_scales', 6), ('scalar_scales', 7), ('sum_squares', 8), ('sum_squares', 9),
-        ('take_inverse_rms', 8), ('take_inverse_rms', 9), ('scalar_scales', 8), ('scalar_scales', 9), ('sum_squares', 10), ('sum_squares', 11),
-        ('take_inverse_rms', 10), ('take_inverse_rms', 11), ('scalar_scales', 10), ('scalar_scales', 11), ('sum_squares', 12), ('sum_squares', 13),
-        ('take_inverse_rms', 12), ('take_inverse_rms', 13), ('scalar_scales', 12), ('scalar_scales', 13), ('sum_squares', 14), ('sum_squares', 15),
-        ('take_inverse_rms', 14), ('take_inverse_rms', 15), ('scalar_scales', 14), ('scalar_scales', 15), ('sum_squares', 16), ('sum_squares', 17),
-        ('take_inverse_rms', 16), ('take_inverse_rms', 17), ('scalar_scales', 16), ('scalar_scales', 17),
-    ],
-    'vector': [
-        ('vector_scales', 0), ('vector_scales', 1), ('vector_scales', 2), ('vector_scales', 3), ('vector_scales', 4), ('vector_scales', 5),
-        ('widen', 0, 2), ('widen', 0, 3), ('interleave', 0), ('widen', 2, 1), ('quantise', 0), ('widen', 2, 2),
-        ('widen', 2, 3), ('widen', 5, 3), ('interleave', 2), ('widen', 1, 1), ('quantise', 2), ('widen', 1, 2),
-        ('widen', 1, 3), ('interleave', 1), ('x_quantise', 0), ('x_quantise', 1), ('x_quantise', 2), ('x_quantise', 3),
-        ('negate_sin',), ('quantise', 1), ('widen', 4, 2), ('widen', 4, 3), ('interleave', 4), ('quantise', 5),
-        ('quantise', 4), ('interleave', 3), ('widen', 6, 3), ('quantise', 3), ('interleave', 6), ('quantise', 7),
-        ('rope', 0), ('rope', 1), ('rope', 2), ('rope', 3), ('rope', 4), ('rope', 5),
-        ('rope', 6), ('rope', 7), ('add', 6), ('quantise', 6), ('kv_quantise',), ('rope', 8),
-        ('rope', 9), ('rope', 10), ('vector_scales', 6), ('vector_scales', 7), ('rope', 11), ('rope', 12),
-        ('vector_scales', 8), ('vector_scales', 9), ('vector_scales', 10), ('rope', 13), ('rope', 14), ('vector_scales', 11),
-        ('rope', 15), ('rope', 16), ('vector_scales', 12), ('vector_scales', 13), ('rope', 17), ('vector_scales', 14),
-        ('vector_scales', 15), ('vector_scales', 16), ('vector_scales', 17),
-    ],
-    'tensor': [
-        ('pe_interleave', 5, 0), ('transpose', 0), ('transpose', 1), ('transpose', 2), ('transpose', 3), ('pe_interleave', 5, 1),
-        ('pe_interleave', 5, 2), ('pe_interleave', 5, 3), ('pe_interleave', 7, 0), ('pe_interleave', 7, 1), ('pe_interleave', 7, 2), ('pe_interleave', 7, 3),
-        ('fill', 0), ('fill', 1), ('fill', 2), ('fill', 3), ('fill', 4), ('fill', 5),
-        ('fill', 6), ('fill', 7), ('fill', 8), ('fill', 9), ('fill', 10), ('fill', 11),
-        ('fill', 12), ('fill', 13), ('fill', 14), ('fill', 15), ('fill', 16), ('fill', 17),
-    ],
-    'gpsimd': [
-        ('add', 0), ('add', 1), ('add', 2), ('add', 3), ('add', 4), ('add', 5),
-        ('add', 7), ('add', 8), ('add', 9), ('add', 10), ('add', 11), ('add', 12),
-        ('add', 13), ('add', 14), ('add', 15), ('add', 16), ('add', 17),
-    ],
-    'sync': [
-        ('store', 0), ('store', 1), ('store', 2), ('store', 3), ('store', 4), ('store', 5),
-        ('store', 6), ('store', 7), ('store', 8), ('store', 9), ('store', 10), ('store', 11),
-        ('store_v', 16), ('store', 12), ('store', 13), ('store_v', 17), ('store', 14), ('store', 15),
-        ('store', 16), ('store', 17),
-    ],
-}
+
+
+def w(u, how):
+    return [("widen", u, t) for t in range(PACK) if WIDEN[u][t] == how]
+
+
+def e(u):
+    return [("evacuate", u, b) for b in range(IL_PARTS)]
+
+
+def pe(u):
+    return [("pe_interleave", u, b) for b in range(IL_PARTS)]
+
+
+def j(kind, *numbers):
+    return [(kind, n) for n in numbers]
 
 
 def make_queues(n_banks):
-    return QUEUES
+    scalar, vector, tensor, gpsimd, sync = [], [], [], [], []
+    scalar += w(0, "A") + w(2, "A") + w(1, "A") + w(4, "A") + w(5, "A") + w(3, "A") + w(6, "A") + e(1) + w(7, "A")
+    scalar += j("x_copy", 0, 1) + e(3) + j("x_copy", 2, 3) + j("kv_interleave", 0, 1)
+    for i in range(n_banks + 2):
+        if i >= 2:
+            scalar.append(("take_inverse_rms", i - 2))
+        if 1 <= i < n_banks + 1:
+            scalar.append(("sum_squares", i - 1))
+        if i >= 2:
+            scalar.append(("scalar_scales", i - 2))
+    vector += w(0, "B") + w(2, "B") + j("interleave", 0) + w(4, "B") + j("interleave", 2) + j("quantise", 0) + w(5, "B") + j("interleave", 4) + j("quantise", 2)
+    vector += w(6, "B") + j("interleave", 5) + j("quantise", 4) + w(7, "B") + j("interleave", 6) + j("quantise", 5, 1) + j("interleave", 7) + j("quantise", 6)
+    vector += j("x_quantise", 0, 1) + j("quantise", 7, 3) + [("negate_sin",)] + j("x_quantise", 2, 3)
+    for i in range(n_banks + FINISH_LAG):
+        if i < n_banks:
+            vector.append(("rope", i))
+        if i == KV_QUANTISE_AFTER_ROPE:
+            vector.append(("kv_quantise",))
+        if i >= FINISH_LAG:
+            vector.append(("vector_scales", i - FINISH_LAG))
+    tensor += pe(1) + j("transpose", 0, 1) + pe(3) + j("transpose", 2, 3)
+    tensor.extend([("fill", i) for i in range(n_banks)])
+    gpsimd.extend([("add", i) for i in range(n_banks) if i not in VECTOR_ADDS])
+    for i in range(n_banks):
+        sync.append(("store", i))
+        if n_banks - 2 <= i + FINISH_LAG < n_banks:
+            sync.append(("store_v", i + FINISH_LAG))
+    return {"scalar": scalar, "vector": vector, "tensor": tensor, "gpsimd": gpsimd, "sync": sync}
 
 
 def tile_multiqueryattention_pa_kernel(tc, x, cos, sin, Wq_bytes, Wq_scale, Wk, Wv, out_0, out_1, out_2):
@@ -113,7 +108,7 @@ def tile_multiqueryattention_pa_kernel(tc, x, cos, sin, Wq_bytes, Wq_scale, Wk, 
         wide_pool = ctx.enter_context(tc.tile_pool(name="wide", bufs=1))
         interleaved_pool = ctx.enter_context(tc.tile_pool(name="interleaved", bufs=1))
         rotated_pool = ctx.enter_context(tc.tile_pool(name="rotated", bufs=ROTATED_BUFS))
-        swapped_pool = ctx.enter_context(tc.tile_pool(name="swapped", bufs=SWAPPED_BUFS))
+        products_pool = ctx.enter_context(tc.tile_pool(name="products", bufs=SWAPPED_BUFS))
         stats_pool = ctx.enter_context(tc.tile_pool(name="stats", bufs=ROTATED_BUFS))
         scratch_pool = ctx.enter_context(tc.tile_pool(name="scratch", bufs=SCRATCH_BUFS))
         v_pool = ctx.enter_context(tc.tile_pool(name="v", bufs=2))
@@ -137,8 +132,7 @@ def tile_multiqueryattention_pa_kernel(tc, x, cos, sin, Wq_bytes, Wq_scale, Wk, 
         warm_up = keep.tile([P, 1], F32, name="warm_up")
         unread_sums = keep.tile([P, SCRATCH_BUFS], F32, name="unread_sums")
         plane_scales = keep.tile([P, PASSES, PACK], F32, name="plane_scales")
-        cos_t = keep.tile([P, TOKEN_TILES, HALF], BF16, name="cos_t")
-        sin_t = keep.tile([P, TOKEN_TILES, 2, HALF], BF16, name="sin_t")
+        factors = keep.tile([P, TOKEN_TILES, 2, 2, HALF], BF16, name="factors")
         wq_bytes_t = [keep.tile([P, PASSES, PACK, UNIT_COLS], U8, name="wq_bytes_t%d" % half) for half in range(UNITS // PASSES)]
         x_t = [keep.tile([P, DIM], BF16, name="x_t%d" % m) for m in range(TOKEN_TILES)]
         x_interleaved = [keep.tile([P, DIM], BF16, name="x_interleaved%d" % m, align_bytes=64) for m in range(TOKEN_TILES)]
@@ -176,8 +170,8 @@ def tile_multiqueryattention_pa_kernel(tc, x, cos, sin, Wq_bytes, Wq_scale, Wk, 
             nc.sync.dma_start(out=wv_t[:].rearrange("p g t n -> p g (t n)"), in_=wv_planes)
 
         def load_cos_sin():
-            nc.sync.dma_start(out=cos_t[:], in_=cos_rows)
-            nc.sync.dma_start(out=sin_t[:, :, 0, :], in_=sin_rows)
+            nc.sync.dma_start(out=factors[:, :, 0, 0, :], in_=cos_rows)
+            nc.sync.dma_start(out=factors[:, :, 1, 0, :], in_=sin_rows)
 
         nc.sync.dma_start(out=plane_scales[:], in_=wq_plane_scales)
         for t in range(PACK):
@@ -319,41 +313,44 @@ def tile_multiqueryattention_pa_kernel(tc, x, cos, sin, Wq_bytes, Wq_scale, Wk, 
                     matmul_passes(bank_t[i][:, r * 2 * D:(r + 1) * 2 * D], 2 * pair + r, kv_codes, kv_scales)
 
         rotated = {}
-        swapped = {}
+        products = {}
         v_tiles = {}
 
         def heads_of(i):
             return BANK_COLS // D if banks[i][0] == "q" else 2
 
         def negate_sin():
-            nc.vector.tensor_scalar(out=sin_t[:, :, 1, :], in0=sin_t[:, :, 0, :], scalar1=-1.0, scalar2=None, op0=ALU.mult)
+            nc.vector.tensor_scalar(out=factors[:, :, 0, 1, :], in0=factors[:, :, 1, 0, :], scalar1=-1.0, scalar2=None, op0=ALU.mult)
+            nc.vector.tensor_copy(out=factors[:, :, 1, 1, :], in_=factors[:, :, 0, 0, :])
 
         def rope(i):
             heads = heads_of(i)
+            products[i] = products_pool.tile([P, BANK_COLS // D, 2, 2, HALF], F32, name="products", tag="products")
             if banks[i][0] == "q":
                 m = banks[i][2]
                 halves = bank_t[i][:].rearrange("p (h w j) -> p h w j", w=2, j=HALF)
-                cos_b = cos_t[:, m, :].unsqueeze(1).unsqueeze(1).to_broadcast([P, heads, 2, HALF])
-                sin_b = sin_t[:, m, :, :].unsqueeze(1).to_broadcast([P, heads, 2, HALF])
+                factor_b = factors[:, m, :, :, :].unsqueeze(1).to_broadcast([P, heads, 2, 2, HALF])
+                nc.vector.tensor_tensor(out=products[i][:], in0=halves.unsqueeze(3).to_broadcast([P, heads, 2, 2, HALF]), in1=factor_b, op=ALU.mult)
             else:
                 pair = banks[i][1]
-                halves = bank_t[i][:].rearrange("p (h e w j) -> p h e w j", e=2, w=2, j=HALF)[:, :, 0, :, :]
-                cos_b = cos_t[:, 2 * pair:2 * pair + 2, :].unsqueeze(2).to_broadcast([P, heads, 2, HALF])
-                sin_b = sin_t[:, 2 * pair:2 * pair + 2, :, :]
-            rotated[i] = rotated_pool.tile([P, BANK_COLS], F32, name="rotated", tag="rotated")
-            swapped[i] = swapped_pool.tile([P, BANK_COLS], F32, name="swapped", tag="swapped")
-            width = heads * D
-            nc.vector.tensor_tensor(out=rotated[i][:, 0:width].rearrange("p (h w j) -> p h w j", w=2, j=HALF), in0=halves, in1=cos_b, op=ALU.mult)
-            nc.vector.tensor_tensor(out=swapped[i][:, 0:width].rearrange("p (h w j) -> p h w j", w=2, j=HALF), in0=halves[:, :, ::-1, :], in1=sin_b, op=ALU.mult)
+                for h in range(heads):
+                    halves = bank_t[i][:, h * 2 * D:h * 2 * D + D].rearrange("p (w j) -> p w j", j=HALF)
+                    nc.vector.tensor_tensor(out=products[i][:, h, :, :, :], in0=halves.unsqueeze(2).to_broadcast([P, 2, 2, HALF]), in1=factors[:, 2 * pair + h, :, :, :], op=ALU.mult)
             if banks[i][0] == "kv":
                 v_t = v_pool.tile([P, 2, D], F32, name="v_t", tag="v_t")
                 nc.vector.tensor_copy(out=v_t[:], in_=bank_t[i][:].rearrange("p (h e d) -> p h e d", e=2, d=D)[:, :, 1, :])
                 v_tiles[i] = v_t
 
         def add(i):
-            width = heads_of(i) * D
+            heads = heads_of(i)
+            rotated[i] = rotated_pool.tile([P, BANK_COLS], F32, name="rotated", tag="rotated")
             engine = nc.vector if i in VECTOR_ADDS else nc.gpsimd
-            engine.tensor_tensor(out=rotated[i][:, 0:width], in0=rotated[i][:, 0:width], in1=swapped[i][:, 0:width], op=ALU.add)
+            engine.tensor_tensor(
+                out=rotated[i][:, 0:heads * D].rearrange("p (h d) -> p h d", d=D),
+                in0=products[i][:, 0:heads, 0, :, :].rearrange("p h r j -> p h (r j)"),
+                in1=products[i][:, 0:heads, 1, :, :].rearrange("p h r j -> p h (r j)"),
+                op=ALU.add,
+            )
 
         square_sums = {}
         inverse_rms = {}
@@ -477,10 +474,10 @@ def tile_multiqueryattention_pa_kernel(tc, x, cos, sin, Wq_bytes, Wq_scale, Wk, 
             if kind == "rope":
                 i = job[1]
                 out = [("fill", i), ("negate_sin",)] + ([("rope", i - 1)] if i else [])
-                out = out + ([("store", i - ROTATED_BUFS)] if i >= ROTATED_BUFS else [])
                 return out + ([("add", i - SWAPPED_BUFS)] if i >= SWAPPED_BUFS else [])
             if kind == "add":
-                return [("rope", job[1])]
+                i = job[1]
+                return [("rope", i)] + ([("add", i - 1)] if i else []) + ([("store", i - ROTATED_BUFS)] if i >= ROTATED_BUFS else [])
             if kind == "sum_squares":
                 return [("add", job[1])]
             if kind == "take_inverse_rms":

@@ -264,7 +264,7 @@ def tile_multiqueryattention_pa_kernel(tc, x, cos, sin, Wq_bytes, Wq_scale, Wk, 
                 new_interleaved(u)
             dst = interleaved[u][:, b * IL_COLS * PACK:(b + 1) * IL_COLS * PACK]
             if EVACUATE[u][b] == "S":
-                nc.scalar.copy(out=dst, in_=il_bank[(u, b)][:])
+                nc.scalar.copy(out=dst.bitcast(F32), in_=il_bank[(u, b)][:].bitcast(F32))
             else:
                 nc.vector.tensor_copy(out=dst, in_=il_bank[(u, b)][:])
 

@@ -28,8 +28,8 @@ IL_PARTS = UNIT_COLS // IL_COLS
 
 FLOPS = 2 * TOKENS * DIM * (HEADS * D + 2 * D)
 
-WIDEN = ("AABB", "AAAA", "AABB", "AAAA", "AABB", "AABB", "AABB", "AABB")
-INTERLEAVE = "VPVPVVVV"
+WIDEN = ("AABB", "AAAA", "AABB", "AAAA", "AABB", "AABB", "ABBB", "ABBB")
+INTERLEAVE = "VPVPVVVS"
 EVACUATE = ("SSSS",) * 8
 STREAMS = ((0, 2, 4, 5, 6, 7), (1, 3))
 VECTOR_ADDS = ()
@@ -38,8 +38,9 @@ FIRST_SHARED_BANK = 4
 VECTOR_SCALED_HEADS = dict((i, 0) for i in range(FIRST_SHARED_BANK))
 VECTOR_SCALED_HEADS_DEFAULT = 1
 FINISH_LAG = 3
+ADD_LAG = 0
 KV_QUANTISE_AFTER_ROPE = 7
-LOAD_ORDER = (("u", 2), ("u", 1), ("u", 4), ("u", 5), ("u", 3), ("u", 6), ("x", 0), ("x", 1), ("u", 7), ("x", 2), ("x", 3), ("k",), ("v",), ("c",))
+LOAD_ORDER = (("p", 0, 0), ("p", 0, 1), ("p", 0, 2), ("p", 0, 3), ("u", 2), ("u", 1), ("u", 4), ("u", 5), ("u", 3), ("u", 6), ("x", 0), ("x", 1), ("u", 7), ("x", 2), ("x", 3), ("k",), ("v",), ("c",))
 WIDE_BUFS = (2, 2)
 INTERLEAVED_BUFS = (2, 2)
 ROTATED_BUFS = 8
@@ -69,7 +70,7 @@ def j(kind, *numbers):
 def make_queues(n_banks):
     scalar, vector, tensor, gpsimd, sync = [], [], [], [], []
     scalar += w(0, "A") + w(2, "A") + w(1, "A") + w(4, "A") + w(5, "A") + w(3, "A") + w(6, "A") + e(1) + w(7, "A")
-    scalar += j("x_copy", 0, 1) + e(3) + j("x_copy", 2, 3) + j("kv_interleave", 0, 1)
+    scalar += j("x_copy", 0, 1) + e(3) + j("x_copy", 2, 3) + j("interleave", 7) + j("kv_interleave", 0, 1)
     for i in range(n_banks + 2):
         if i >= 2:
             scalar.append(("take_inverse_rms", i - 2))
@@ -78,13 +79,15 @@ def make_queues(n_banks):
         if i >= 2:
             scalar.append(("scalar_scales", i - 2))
     vector += w(0, "B") + w(2, "B") + j("interleave", 0) + w(4, "B") + j("interleave", 2) + j("quantise", 0) + w(5, "B") + j("interleave", 4) + j("quantise", 2)
-    vector += w(6, "B") + j("interleave", 5) + j("quantise", 4) + w(7, "B") + j("interleave", 6) + j("quantise", 5, 1) + j("interleave", 7) + j("quantise", 6)
-    vector += j("x_quantise", 0, 1) + j("quantise", 7, 3) + [("negate_sin",)] + j("x_quantise", 2, 3)
+    vector += w(6, "B") + j("interleave", 5) + j("quantise", 4) + w(7, "B") + j("interleave", 6) + j("quantise", 5, 1) + j("quantise", 6)
+    vector += j("x_quantise", 0, 1) + j("quantise", 3) + [("negate_sin",)] + j("x_quantise", 2, 3)
     for i in range(n_banks + FINISH_LAG):
         if i < n_banks:
             vector.append(("rope", i))
+        if ADD_LAG <= i < n_banks + ADD_LAG and i - ADD_LAG in VECTOR_ADDS:
+            vector.append(("add", i - ADD_LAG))
         if i == KV_QUANTISE_AFTER_ROPE:
-            vector.append(("kv_quantise",))
+            vector.extend([("quantise", 7), ("kv_quantise",)])
         if i >= FINISH_LAG:
             vector.append(("vector_scales", i - FINISH_LAG))
     tensor += pe(1) + j("transpose", 0, 1) + pe(3) + j("transpose", 2, 3)
@@ -174,9 +177,7 @@ def tile_multiqueryattention_pa_kernel(tc, x, cos, sin, Wq_bytes, Wq_scale, Wk, 
             nc.sync.dma_start(out=factors[:, :, 1, 0, :], in_=sin_rows)
 
         nc.sync.dma_start(out=plane_scales[:], in_=wq_plane_scales)
-        for t in range(PACK):
-            load_plane(0, t)
-        loaders = {"u": load_unit, "x": load_x, "k": load_wk, "v": load_wv, "c": load_cos_sin}
+        loaders = {"p": load_plane, "u": load_unit, "x": load_x, "k": load_wk, "v": load_wv, "c": load_cos_sin}
         for item in LOAD_ORDER:
             loaders[item[0]](*item[1:])
 
@@ -278,6 +279,23 @@ def tile_multiqueryattention_pa_kernel(tc, x, cos, sin, Wq_bytes, Wq_scale, Wk, 
                 nc.scalar.copy(out=kv_interleaved[:, :, which * D:(which + 1) * D, :], in_=planes[:].rearrange("p g t n -> p g n t"))
             else:
                 nc.vector.tensor_copy(out=kv_interleaved[:, :, which * D:(which + 1) * D, :], in_=planes[:].rearrange("p g t n -> p g n t"))
+
+        kv_bank = {}
+
+        def kv_pe_interleave(g):
+            kv_bank[g] = psum.tile([P, 2 * D * PACK], BF16, name="bank", tag="bank")
+            for which in range(2):
+                planes = wk_t if which == 0 else wv_t
+                nc.tensor.matmul(
+                    out=kv_bank[g][:, which * BANK_COLS:(which + 1) * BANK_COLS],
+                    lhsT=identity_bf[:],
+                    rhs=planes[:, g, :, :].rearrange("p t n -> p n t"),
+                    start=True,
+                    stop=True,
+                )
+
+        def kv_evacuate(g):
+            nc.scalar.copy(out=kv_interleaved[:, g, :, :].rearrange("p n t -> p (n t)").bitcast(F32), in_=kv_bank[g][:].bitcast(F32))
 
         def kv_quantise():
             nc.vector.quantize_mx(
@@ -401,7 +419,7 @@ def tile_multiqueryattention_pa_kernel(tc, x, cos, sin, Wq_bytes, Wq_scale, Wk, 
             nc.sync.dma_start(out=v_out[:, 2 * pair:2 * pair + 2, :], in_=v_tiles[i][:])
 
         actions = {
-            "store_v": store_v,
+            "store_v": store_v, "kv_pe_interleave": kv_pe_interleave, "kv_evacuate": kv_evacuate,
             "transpose": transpose, "x_copy": x_copy, "x_quantise": x_quantise, "widen": widen, "scale_plane": scale_plane,
             "interleave": interleave, "pe_interleave": pe_interleave, "evacuate": evacuate, "quantise": quantise,
             "kv_interleave": kv_interleave, "kv_quantise": kv_quantise, "fill": fill, "negate_sin": negate_sin, "rope": rope, "add": add,
@@ -418,6 +436,8 @@ def tile_multiqueryattention_pa_kernel(tc, x, cos, sin, Wq_bytes, Wq_scale, Wk, 
                 tile_readers.extend([("x_copy", job[1])] * 2)
             elif job[0] == "pe_interleave":
                 tile_readers.append(("evacuate",) + job[1:])
+            elif job[0] == "kv_pe_interleave":
+                tile_readers.append(("kv_evacuate", job[1]))
             else:
                 tile_readers.append(("rope", job[1]))
 
@@ -462,7 +482,11 @@ def tile_multiqueryattention_pa_kernel(tc, x, cos, sin, Wq_bytes, Wq_scale, Wk, 
             if kind == "quantise":
                 return interleaved_made(job[1])
             if kind == "kv_quantise":
-                return [("kv_interleave", 0), ("kv_interleave", 1)]
+                return [("kv_evacuate", g) for g in range(PASSES)] if KV_INTERLEAVE == "PP" else [("kv_interleave", 0), ("kv_interleave", 1)]
+            if kind == "kv_pe_interleave":
+                return buffers_free(job, 1)
+            if kind == "kv_evacuate":
+                return [("kv_pe_interleave", job[1])]
             if kind == "fill":
                 i = job[1]
                 out = buffers_free(job, 1)

@@ -22,100 +22,129 @@ TOKEN_TILES = TOKENS // P
 BANK_COLS = 512
 UNIT_COLS = 1024
 UNITS = PASSES * (HEADS * D // UNIT_COLS)
-BANKS_PER_UNIT = UNIT_COLS // BANK_COLS
+HEADS_PER_UNIT = UNIT_COLS // D
+HEADS_PER_BANK = BANK_COLS // D
 IL_COLS = 256
 IL_PARTS = UNIT_COLS // IL_COLS
 
 FLOPS = 2 * TOKENS * DIM * (HEADS * D + 2 * D)
 
-WIDEN = ("AABB", "AAAA", "AABB", "AAAA", "AABB", "AABB", "ABBB", "ABBB")
-INTERLEAVE = "VPVPVVVS"
-EVACUATE = ("SSSS",) * 8
-STREAMS = ((0, 2, 4, 5, 6, 7), (1, 3))
-VECTOR_ADDS = ()
-KV_INTERLEAVE = "SS"
-FIRST_SHARED_BANK = 4
-VECTOR_SCALED_HEADS = dict((i, 0) for i in range(FIRST_SHARED_BANK))
-VECTOR_SCALED_HEADS_DEFAULT = 1
-FINISH_LAG = 3
-ADD_LAG = 0
-KV_QUANTISE_AFTER_ROPE = 7
-LOAD_ORDER = (("p", 0, 0), ("p", 0, 1), ("p", 0, 2), ("p", 0, 3), ("u", 2), ("u", 1), ("u", 4), ("u", 5), ("u", 3), ("u", 6), ("x", 0), ("x", 1), ("u", 7), ("x", 2), ("x", 3), ("k",), ("v",), ("c",))
+WIDEN = ("DDDD", "AAAA", "DDDD", "AAAA", "DDDD", "DDDD", "DDDD", "AAAA")
+INTERLEAVE = "XPXPXYYS"
+STREAMS = ((0, 2, 4, 5, 6), (1, 3, 7))
 WIDE_BUFS = (2, 2)
 INTERLEAVED_BUFS = (2, 2)
+LOAD_ORDER = (("p", 0, 0), ("p", 1, 0), ("p", 0, 1), ("p", 1, 1), ("p", 0, 2), ("p", 0, 3), ("p", 1, 2), ("p", 1, 3), ("u", 2), ("u", 3), ("u", 4), ("x", 0), ("x", 1), ("u", 5), ("c",), ("u", 7), ("x", 2), ("x", 3), ("u", 6), ("k",), ("v",))
+BANKS = tuple(("q", block, m) for block in range(4) for m in range(4)) + (("kv", 0), ("kv", 1))
+N_BANKS = len(BANKS)
+LATE_FIRST = 8
+GPSIMD_SCALES = ()
+VECTOR_SCALES = {4: 1, 5: 1, 6: 1, 7: 1, 8: 1, 9: 1, 10: 1, 11: 1, 12: 2, 13: 2, 14: 2, 15: 2, 16: 1, 17: 1}
+VECTOR_LAG = 3
+FILL_AHEAD = 3
+GPSIMD_LAG = 3
 ROTATED_BUFS = 8
-SWAPPED_BUFS = 3
+RESULT_BUFS = 3
+PRODUCTS_BUFS = 3
 SCRATCH_BUFS = 8
-BANK_BUFS = 8
-IL_BUFS = 2
+BANK_BUFS = {"bank": 4, "side": 4}
+SHORT = {
+    "i": "interleave", "q": "quantise", "x": "x_copy", "X": "x_quantise", "T": "transpose", "t": "table_copy", "k": "kv_evacuate",
+    "K": "kv_pe_interleave", "n": "negate_sin", "Q": "kv_quantise", "t": "table_copy", "b": "table_transpose",
+}
+SCALAR_FIRST = "w1 w3 e1 x0 x1 w7a e3 x2 x3 w7b i5 i6 i7"
+VECTOR_FIRST = "w0 w2 i0 w4 q0 i2 w5 n q2 i4 w6 q4 q1 X0 q3 X1"
+TENSOR_FIRST = "p1 T0 T1 p3 T2 T3"
+VECTOR_LATE = {1: "q5", 4: "q6", 6: "q7", 10: "Q"}
+TENSOR_LATE = {7: "K0 K1 K2 K3"}
+SCALAR_LATE = {4: "k0 k1 k2 k3"}
 QUEUE_NAMES = ("scalar", "vector", "tensor", "gpsimd", "sync")
 
 
-def w(u, how):
-    return [("widen", u, t) for t in range(PACK) if WIDEN[u][t] == how]
+def jobs(text):
+    out = []
+    for name in text.split():
+        letter, rest = name[0], name[1:]
+        if letter == "w":
+            planes = range(PACK) if rest[-1] not in "ab" else range(2) if rest[-1] == "a" else range(2, PACK)
+            out.extend([("widen", int(rest[0]), t) for t in planes])
+        elif letter in "ep":
+            out.extend([("evacuate" if letter == "e" else "pe_interleave", int(rest), b) for b in range(IL_PARTS)])
+        elif rest:
+            out.append((SHORT[letter], int(rest)))
+        else:
+            out.append((SHORT[letter],))
+    return out
 
 
-def e(u):
-    return [("evacuate", u, b) for b in range(IL_PARTS)]
+def turned(i):
+    return BANKS[i][0] == "t"
 
 
-def pe(u):
-    return [("pe_interleave", u, b) for b in range(IL_PARTS)]
+def heads_of(i):
+    return 2 if BANKS[i][0] == "kv" else 4
 
 
-def j(kind, *numbers):
-    return [(kind, n) for n in numbers]
+def vector_heads(i):
+    return 0 if i in GPSIMD_SCALES else VECTOR_SCALES.get(i, 0)
 
 
-def make_queues(n_banks):
+def scalar_heads(i):
+    return 0 if i in GPSIMD_SCALES else heads_of(i) - vector_heads(i)
+
+
+def make_queues():
     scalar, vector, tensor, gpsimd, sync = [], [], [], [], []
-    scalar += w(0, "A") + w(2, "A") + w(1, "A") + w(4, "A") + w(5, "A") + w(3, "A") + w(6, "A") + e(1) + w(7, "A")
-    scalar += j("x_copy", 0, 1) + e(3) + j("x_copy", 2, 3) + j("interleave", 7) + j("kv_interleave", 0, 1)
-    for i in range(n_banks + 2):
+    scalar += jobs(SCALAR_FIRST)
+    for i in range(N_BANKS + 2):
         if i >= 2:
             scalar.append(("take_inverse_rms", i - 2))
-        if 1 <= i < n_banks + 1:
+        if 1 <= i < N_BANKS + 1:
             scalar.append(("sum_squares", i - 1))
         if i >= 2:
             scalar.append(("scalar_scales", i - 2))
-    vector += w(0, "B") + w(2, "B") + j("interleave", 0) + w(4, "B") + j("interleave", 2) + j("quantise", 0) + w(5, "B") + j("interleave", 4) + j("quantise", 2)
-    vector += w(6, "B") + j("interleave", 5) + j("quantise", 4) + w(7, "B") + j("interleave", 6) + j("quantise", 5, 1) + j("quantise", 6)
-    vector += j("x_quantise", 0, 1) + j("quantise", 3) + [("negate_sin",)] + j("x_quantise", 2, 3)
-    for i in range(n_banks + FINISH_LAG):
-        if i < n_banks:
+            scalar.extend(jobs(SCALAR_LATE.get(i - 2, "")))
+    vector += jobs(VECTOR_FIRST)
+    for i in range(N_BANKS + VECTOR_LAG):
+        if i < N_BANKS:
             vector.append(("rope", i))
-        if ADD_LAG <= i < n_banks + ADD_LAG and i - ADD_LAG in VECTOR_ADDS:
-            vector.append(("add", i - ADD_LAG))
-        if i == KV_QUANTISE_AFTER_ROPE:
-            vector.extend([("quantise", 7), ("kv_quantise",)])
-        if i >= FINISH_LAG:
-            vector.append(("vector_scales", i - FINISH_LAG))
-    tensor += pe(1) + j("transpose", 0, 1) + pe(3) + j("transpose", 2, 3)
-    tensor.extend([("fill", i) for i in range(n_banks)])
-    gpsimd.extend([("add", i) for i in range(n_banks) if i not in VECTOR_ADDS])
-    for i in range(n_banks):
+        vector.extend(jobs(VECTOR_LATE.get(i, "")))
+        if i >= VECTOR_LAG:
+            vector.append(("vector_scales", i - VECTOR_LAG))
+    tensor += jobs(TENSOR_FIRST)
+    for banks in (range(0, LATE_FIRST), range(LATE_FIRST, N_BANKS)):
+        for i in range(banks.start, banks.stop + FILL_AHEAD):
+            if i < banks.stop:
+                tensor.append(("fill", i))
+                tensor.extend(jobs(TENSOR_LATE.get(i, "")))
+            if i - FILL_AHEAD >= banks.start and turned(i - FILL_AHEAD):
+                tensor.append(("turn_back", i - FILL_AHEAD))
+    for i in range(N_BANKS + GPSIMD_LAG):
+        if i < N_BANKS and not turned(i):
+            gpsimd.append(("add", i))
+        if i - GPSIMD_LAG in GPSIMD_SCALES:
+            gpsimd.append(("gpsimd_scales", i - GPSIMD_LAG))
+    for i in range(N_BANKS):
         sync.append(("store", i))
-        if n_banks - 2 <= i + FINISH_LAG < n_banks:
-            sync.append(("store_v", i + FINISH_LAG))
+        if BANKS[i][0] == "kv":
+            sync.append(("store_v", i))
     return {"scalar": scalar, "vector": vector, "tensor": tensor, "gpsimd": gpsimd, "sync": sync}
 
 
 def tile_multiqueryattention_pa_kernel(tc, x, cos, sin, Wq_bytes, Wq_scale, Wk, Wv, out_0, out_1, out_2):
     nc = tc.nc
-    banks = [("q", block, m) for block in range(HEADS * D // BANK_COLS) for m in range(TOKEN_TILES)]
-    banks += [("kv", pair) for pair in range(TOKEN_TILES // 2)]
-    n_banks = len(banks)
 
     with ExitStack() as ctx:
         keep = ctx.enter_context(tc.tile_pool(name="keep", bufs=1))
         wide_pool = ctx.enter_context(tc.tile_pool(name="wide", bufs=1))
         interleaved_pool = ctx.enter_context(tc.tile_pool(name="interleaved", bufs=1))
         rotated_pool = ctx.enter_context(tc.tile_pool(name="rotated", bufs=ROTATED_BUFS))
-        products_pool = ctx.enter_context(tc.tile_pool(name="products", bufs=SWAPPED_BUFS))
-        stats_pool = ctx.enter_context(tc.tile_pool(name="stats", bufs=ROTATED_BUFS))
+        result_pool = ctx.enter_context(tc.tile_pool(name="result", bufs=RESULT_BUFS))
+        products_pool = ctx.enter_context(tc.tile_pool(name="products", bufs=PRODUCTS_BUFS))
+        stats_pool = ctx.enter_context(tc.tile_pool(name="stats", bufs=8))
         scratch_pool = ctx.enter_context(tc.tile_pool(name="scratch", bufs=SCRATCH_BUFS))
         v_pool = ctx.enter_context(tc.tile_pool(name="v", bufs=2))
-        psum = ctx.enter_context(tc.psum_pool(name="psum", bufs=BANK_BUFS))
+        psum = ctx.enter_context(tc.psum_pool(name="psum", bufs=1))
         ctx.enter_context(tc.manual_schedule())
 
         x_rows = x[0].rearrange("(m p) k -> m p k", p=P)
@@ -126,21 +155,24 @@ def tile_multiqueryattention_pa_kernel(tc, x, cos, sin, Wq_bytes, Wq_scale, Wk, 
         wk_planes = Wk.rearrange("(g p t) n -> p g (t n)", p=P, t=PACK)
         wv_planes = Wv.rearrange("(g p t) n -> p g (t n)", p=P, t=PACK)
         q_out = out_0[0].rearrange("(m p) h d -> m p (h d)", p=P)
+        q_head_out = out_0[0].rearrange("(m p) h d -> h p m d", p=P)
         k_out = out_1[0].rearrange("(m p) d -> p m d", p=P)
         v_out = out_2[0].rearrange("(m p) d -> p m d", p=P)
 
         identity = keep.tile([P, P], F32, name="identity")
+        swap = keep.tile([P, P], F32, name="swap")
         identity_bf = keep.tile([P, P], BF16, name="identity_bf")
         one = keep.tile([P, 1], F32, name="one")
         warm_up = keep.tile([P, 1], F32, name="warm_up")
         unread_sums = keep.tile([P, SCRATCH_BUFS], F32, name="unread_sums")
         plane_scales = keep.tile([P, PASSES, PACK], F32, name="plane_scales")
-        factors = keep.tile([P, TOKEN_TILES, 2, 2, HALF], BF16, name="factors")
+        factors = keep.tile([P, TOKEN_TILES, 5, HALF], BF16, name="factors")
+        table = keep.tile([P, 2, TOKENS], BF16, name="table")
         wq_bytes_t = [keep.tile([P, PASSES, PACK, UNIT_COLS], U8, name="wq_bytes_t%d" % half) for half in range(UNITS // PASSES)]
         x_t = [keep.tile([P, DIM], BF16, name="x_t%d" % m) for m in range(TOKEN_TILES)]
-        x_interleaved = [keep.tile([P, DIM], BF16, name="x_interleaved%d" % m, align_bytes=64) for m in range(TOKEN_TILES)]
-        x_codes = [keep.tile([P, PASSES * P], U32, name="x_codes%d" % m, align_bytes=64) for m in range(TOKEN_TILES)]
-        x_scales = [keep.tile([P, PASSES * P], U8, name="x_scales%d" % m, align_bytes=64) for m in range(TOKEN_TILES)]
+        x_interleaved = keep.tile([P, PASSES, TOKENS, PACK], BF16, name="x_interleaved", align_bytes=64)
+        x_codes = keep.tile([P, PASSES, TOKENS], U32, name="x_codes", align_bytes=64)
+        x_scales = keep.tile([P, PASSES, TOKENS], U8, name="x_scales", align_bytes=64)
         wq_codes = [keep.tile([P, PASSES, UNIT_COLS], U32, name="wq_codes%d" % half, align_bytes=64) for half in range(UNITS // PASSES)]
         wq_scales = [keep.tile([P, PASSES, UNIT_COLS], U8, name="wq_scales%d" % half, align_bytes=64) for half in range(UNITS // PASSES)]
         wk_t = keep.tile([P, PASSES, PACK, D], BF16, name="wk_t")
@@ -150,8 +182,9 @@ def tile_multiqueryattention_pa_kernel(tc, x, cos, sin, Wq_bytes, Wq_scale, Wk, 
         kv_scales = keep.tile([P, PASSES, 2 * D], U8, name="kv_scales", align_bytes=64)
 
         make_identity(nc, identity[:])
-        if "P" in INTERLEAVE:
-            make_identity(nc, identity_bf[:])
+        make_identity(nc, identity_bf[:])
+        nc.gpsimd.tensor_copy(out=swap[:, 0:HALF], in_=identity[:, HALF:D])
+        nc.gpsimd.tensor_copy(out=swap[:, HALF:D], in_=identity[:, 0:HALF])
         nc.vector.memset(one[:], 1.0)
         nc.scalar.activation(out=warm_up[:], in_=one[:], func=ACT.Abs_reciprocal_sqrt)
 
@@ -173,8 +206,9 @@ def tile_multiqueryattention_pa_kernel(tc, x, cos, sin, Wq_bytes, Wq_scale, Wk, 
             nc.sync.dma_start(out=wv_t[:].rearrange("p g t n -> p g (t n)"), in_=wv_planes)
 
         def load_cos_sin():
-            nc.sync.dma_start(out=factors[:, :, 0, 0, :], in_=cos_rows)
-            nc.sync.dma_start(out=factors[:, :, 1, 0, :], in_=sin_rows)
+            for place in (0, 3, 4):
+                nc.sync.dma_start(out=factors[:, :, place, :], in_=cos_rows)
+            nc.sync.dma_start(out=factors[:, :, 2, :], in_=sin_rows)
 
         nc.sync.dma_start(out=plane_scales[:], in_=wq_plane_scales)
         loaders = {"p": load_plane, "u": load_unit, "x": load_x, "k": load_wk, "v": load_wv, "c": load_cos_sin}
@@ -186,26 +220,33 @@ def tile_multiqueryattention_pa_kernel(tc, x, cos, sin, Wq_bytes, Wq_scale, Wk, 
         def transpose(m):
             words = x_t[m][:].bitcast(F32)
             for a in range(2):
-                x_transposed[(m, a)] = psum.tile([P, 2, 2, P], F32, name="bank", tag="bank")
+                x_transposed[(m, a)] = psum.tile([P, 2, 2, P], F32, name="bank", tag="bank", bufs=BANK_BUFS["bank"])
                 for gg in range(2):
                     g = 2 * a + gg
-                    for w in range(2):
+                    for s in range(2):
                         nc.tensor.transpose(
-                            out=x_transposed[(m, a)][:, gg, w, :],
-                            in_=words[:, 256 * g + w:256 * (g + 1):2],
+                            out=x_transposed[(m, a)][:, gg, s, :],
+                            in_=words[:, 256 * g + s:256 * (g + 1):2],
                             identity=identity[:],
                         )
 
         def x_copy(m):
-            words = x_interleaved[m][:].bitcast(F32).rearrange("p (g r w) -> p g r w", g=PASSES, w=2)
             for a in range(2):
-                nc.scalar.copy(out=words[:, 2 * a:2 * a + 2, :, :], in_=x_transposed[(m, a)][:].rearrange("p g w r -> p g r w"))
+                target = x_interleaved[:, 2 * a:2 * a + 2, m * P:(m + 1) * P, :].bitcast(F32)
+                nc.scalar.copy(out=target, in_=x_transposed[(m, a)][:].rearrange("p g w r -> p g r w"))
 
-        def x_quantise(m):
-            nc.vector.quantize_mx(out=x_codes[m][:].bitcast(FP8X4), scales=x_scales[m][:], in_=x_interleaved[m][:])
+        def x_quantise(pair):
+            cols = slice(pair * 2 * P, (pair + 1) * 2 * P)
+            for g in range(PASSES):
+                nc.vector.quantize_mx(
+                    out=x_codes[:, g, cols].bitcast(FP8X4),
+                    scales=x_scales[:, g, cols],
+                    in_=x_interleaved[:, g, cols, :].rearrange("p r t -> p (r t)"),
+                )
 
         wide = {}
         interleaved = {}
+        il_bank = {}
 
         def stream_of(u):
             return [u in stream for stream in STREAMS].index(True)
@@ -214,25 +255,18 @@ def tile_multiqueryattention_pa_kernel(tc, x, cos, sin, Wq_bytes, Wq_scale, Wk, 
             stream = STREAMS[stream_of(u)]
             return [stream[stream.index(u) - steps]] if stream.index(u) >= steps else []
 
-        il_bank = {}
-
         def widen(u, t):
             half, g = divmod(u, PASSES)
             if u not in wide:
-                wide[u] = wide_pool.tile([P, PACK, UNIT_COLS], BF16, name="wide", tag="wide%d" % stream_of(u), bufs=WIDE_BUFS[stream_of(u)])
+                wide[u] = wide_pool.tile([P, PACK * UNIT_COLS], BF16, name="wide", tag="wide%d" % stream_of(u), bufs=WIDE_BUFS[stream_of(u)])
             codes = wq_bytes_t[half][:, g, t, :].bitcast(FP8)
             scale = plane_scales[:, g, t:t + 1]
-            how = WIDEN[u][t]
-            if how == "B":
-                nc.vector.tensor_scalar(out=wide[u][:, t, :], in0=codes, scalar1=scale, scalar2=None, op0=ALU.mult)
-            elif how == "A":
-                nc.scalar.activation(out=wide[u][:, t, :], in_=codes, func=ACT.Copy, scale=scale)
+            if WIDEN[u][t] == "D":
+                pair, place = divmod(t, 2)
+                out = wide[u][:, pair * 2 * UNIT_COLS + place:(pair + 1) * 2 * UNIT_COLS:2]
+                nc.vector.tensor_scalar(out=out, in0=codes, scalar1=scale, scalar2=None, op0=ALU.mult)
             else:
-                nc.scalar.copy(out=wide[u][:, t, :], in_=codes)
-
-        def scale_plane(u, t):
-            g = u % PASSES
-            nc.vector.tensor_scalar(out=wide[u][:, t, :], in0=wide[u][:, t, :], scalar1=plane_scales[:, g, t:t + 1], scalar2=None, op0=ALU.mult)
+                nc.scalar.activation(out=wide[u][:, t * UNIT_COLS:(t + 1) * UNIT_COLS], in_=codes, func=ACT.Copy, scale=scale)
 
         def new_interleaved(u):
             interleaved[u] = interleaved_pool.tile(
@@ -241,21 +275,28 @@ def tile_multiqueryattention_pa_kernel(tc, x, cos, sin, Wq_bytes, Wq_scale, Wk, 
 
         def interleave(u):
             new_interleaved(u)
-            dst = interleaved[u][:].rearrange("p (c i t) -> p c t i", i=4, t=PACK)
-            src = wide[u][:].rearrange("p t (c i) -> p c t i", i=4)
             if INTERLEAVE[u] == "S":
-                nc.scalar.copy(out=dst, in_=src)
+                nc.scalar.copy(
+                    out=interleaved[u][:].rearrange("p (c i t) -> p c t i", i=4, t=PACK),
+                    in_=wide[u][:].rearrange("p (t c i) -> p c t i", t=PACK, i=4),
+                )
+                return
+            words = wide[u][:].bitcast(F32).rearrange("p (a n) -> p n a", a=2)
+            target = interleaved[u][:].bitcast(F32).rearrange("p (n a) -> p n a", a=2)
+            if INTERLEAVE[u] == "X":
+                nc.vector.tensor_copy(out=target, in_=words)
             else:
-                nc.vector.tensor_copy(out=dst, in_=src)
+                nc.scalar.copy(out=target, in_=words)
 
         def pe_interleave(u, b):
-            il_bank[(u, b)] = psum.tile([P, IL_COLS * PACK], BF16, name="bank", tag="bank")
+            il_bank[(u, b)] = psum.tile([P, IL_COLS * PACK], BF16, name="side", tag="side", bufs=BANK_BUFS["side"])
+            planes = wide[u][:].rearrange("p (t n) -> p t n", t=PACK)
             for r in range(2):
                 n0 = b * IL_COLS + r * (IL_COLS // 2)
                 nc.tensor.matmul(
-                    out=il_bank[(u, b)][:, r * BANK_COLS:(r + 1) * BANK_COLS],
+                    out=il_bank[(u, b)][:, r * BANK_COLS:(r + 1) * BANK_COLS].rearrange("p (n t) -> p t n", t=PACK),
                     lhsT=identity_bf[:],
-                    rhs=wide[u][:, :, n0:n0 + IL_COLS // 2].rearrange("p t n -> p n t"),
+                    rhs=planes[:, :, n0:n0 + IL_COLS // 2],
                     start=True,
                     stop=True,
                 )
@@ -263,33 +304,22 @@ def tile_multiqueryattention_pa_kernel(tc, x, cos, sin, Wq_bytes, Wq_scale, Wk, 
         def evacuate(u, b):
             if b == 0:
                 new_interleaved(u)
-            dst = interleaved[u][:, b * IL_COLS * PACK:(b + 1) * IL_COLS * PACK]
-            if EVACUATE[u][b] == "S":
-                nc.scalar.copy(out=dst.bitcast(F32), in_=il_bank[(u, b)][:].bitcast(F32))
-            else:
-                nc.vector.tensor_copy(out=dst, in_=il_bank[(u, b)][:])
+            target = interleaved[u][:, b * IL_COLS * PACK:(b + 1) * IL_COLS * PACK]
+            nc.scalar.copy(out=target.bitcast(F32), in_=il_bank[(u, b)][:].bitcast(F32))
 
         def quantise(u):
             half, g = divmod(u, PASSES)
             nc.vector.quantize_mx(out=wq_codes[half][:, g, :].bitcast(FP8X4), scales=wq_scales[half][:, g, :], in_=interleaved[u][:])
 
-        def kv_interleave(which):
-            planes = wk_t if which == 0 else wv_t
-            if KV_INTERLEAVE[which] == "S":
-                nc.scalar.copy(out=kv_interleaved[:, :, which * D:(which + 1) * D, :], in_=planes[:].rearrange("p g t n -> p g n t"))
-            else:
-                nc.vector.tensor_copy(out=kv_interleaved[:, :, which * D:(which + 1) * D, :], in_=planes[:].rearrange("p g t n -> p g n t"))
-
         kv_bank = {}
 
         def kv_pe_interleave(g):
-            kv_bank[g] = psum.tile([P, 2 * D * PACK], BF16, name="bank", tag="bank")
-            for which in range(2):
-                planes = wk_t if which == 0 else wv_t
+            kv_bank[g] = psum.tile([P, 2 * D * PACK], BF16, name="side", tag="side", bufs=BANK_BUFS["side"])
+            for which, planes in ((0, wk_t), (1, wv_t)):
                 nc.tensor.matmul(
-                    out=kv_bank[g][:, which * BANK_COLS:(which + 1) * BANK_COLS],
+                    out=kv_bank[g][:, which * BANK_COLS:(which + 1) * BANK_COLS].rearrange("p (n t) -> p t n", t=PACK),
                     lhsT=identity_bf[:],
-                    rhs=planes[:, g, :, :].rearrange("p t n -> p n t"),
+                    rhs=planes[:, g, :, :],
                     start=True,
                     stop=True,
                 )
@@ -304,101 +334,152 @@ def tile_multiqueryattention_pa_kernel(tc, x, cos, sin, Wq_bytes, Wq_scale, Wk, 
                 in_=kv_interleaved[:].rearrange("p g n t -> p (g n t)"),
             )
 
+        def negate_sin():
+            nc.vector.tensor_scalar(out=factors[:, :, 1, :], in0=factors[:, :, 2, :], scalar1=-1.0, scalar2=None, op0=ALU.mult)
+
+        table_bank = {}
+
+        def table_transpose():
+            table_bank[0] = psum.tile([P, 2, TOKENS], BF16, name="side", tag="side", bufs=BANK_BUFS["side"])
+            for r, place in ((0, 3), (1, 1)):
+                for m in range(TOKEN_TILES):
+                    nc.tensor.transpose(
+                        out=table_bank[0][:, r, m * P:(m + 1) * P],
+                        in_=factors[:, m, place:place + 2, :].rearrange("p a j -> p (a j)"),
+                        identity=identity_bf[:],
+                    )
+
+        def table_copy():
+            nc.scalar.copy(out=table[:], in_=table_bank[0][:])
+
         bank_t = {}
 
-        def matmul_passes(out, m, codes, scales):
+        def passes_mx(out, stationary, moving):
             for g in range(PASSES):
                 nc.tensor.matmul_mx(
                     out=out,
-                    lhsT=x_codes[m][:, g * P:(g + 1) * P].bitcast(FP8X4),
-                    lhsT_scale=x_scales[m][:, g * P:(g + 1) * P],
-                    rhs=codes[:, g, :].bitcast(FP8X4),
-                    rhs_scale=scales[:, g, :],
+                    lhsT=stationary[0](g).bitcast(FP8X4),
+                    lhsT_scale=stationary[1](g),
+                    rhs=moving[0](g).bitcast(FP8X4),
+                    rhs_scale=moving[1](g),
                     start=(g == 0),
                     stop=(g == PASSES - 1),
                 )
 
+        def x_operand(first, count):
+            return (lambda g: x_codes[:, g, first:first + count], lambda g: x_scales[:, g, first:first + count])
+
+        def wq_operand(half, first, count):
+            return (lambda g: wq_codes[half][:, g, first:first + count], lambda g: wq_scales[half][:, g, first:first + count])
+
         def fill(i):
-            bank_t[i] = psum.tile([P, BANK_COLS], F32, name="bank", tag="bank")
-            if banks[i][0] == "q":
-                block, m = banks[i][1:]
-                half, part = divmod(block, BANKS_PER_UNIT)
-                cols = slice(part * BANK_COLS, (part + 1) * BANK_COLS)
-                matmul_passes(bank_t[i][:], m, wq_codes[half][:, :, cols], wq_scales[half][:, :, cols])
+            bank_t[i] = psum.tile([P, BANK_COLS], F32, name="bank", tag="bank", bufs=BANK_BUFS["bank"])
+            if BANKS[i][0] == "t":
+                half, h = divmod(BANKS[i][1], HEADS_PER_UNIT)
+                passes_mx(bank_t[i][:], wq_operand(half, h * D, D), x_operand(0, TOKENS))
+            elif BANKS[i][0] == "q":
+                block, m = BANKS[i][1:]
+                half, part = divmod(block, UNIT_COLS // BANK_COLS)
+                passes_mx(bank_t[i][:], x_operand(m * P, P), wq_operand(half, part * BANK_COLS, BANK_COLS))
             else:
-                pair = banks[i][1]
+                kv = (lambda g: kv_codes[:, g, :], lambda g: kv_scales[:, g, :])
                 for r in range(2):
-                    matmul_passes(bank_t[i][:, r * 2 * D:(r + 1) * 2 * D], 2 * pair + r, kv_codes, kv_scales)
+                    passes_mx(bank_t[i][:, r * 2 * D:(r + 1) * 2 * D], x_operand((2 * BANKS[i][1] + r) * P, P), kv)
 
         rotated = {}
         products = {}
         v_tiles = {}
-
-        def heads_of(i):
-            return BANK_COLS // D if banks[i][0] == "q" else 2
-
-        def negate_sin():
-            nc.vector.tensor_scalar(out=factors[:, :, 0, 1, :], in0=factors[:, :, 1, 0, :], scalar1=-1.0, scalar2=None, op0=ALU.mult)
-            nc.vector.tensor_copy(out=factors[:, :, 1, 1, :], in_=factors[:, :, 0, 0, :])
+        turned_bank = {}
+        result = {}
 
         def rope(i):
             heads = heads_of(i)
-            products[i] = products_pool.tile([P, BANK_COLS // D, 2, 2, HALF], F32, name="products", tag="products")
-            if banks[i][0] == "q":
-                m = banks[i][2]
+            if BANKS[i][0] == "t":
+                products[i] = products_pool.tile([P, 2, TOKENS], F32, name="products", tag="products")
+                nc.vector.tensor_tensor(out=products[i][:], in0=bank_t[i][:].unsqueeze(1).to_broadcast([P, 2, TOKENS]), in1=table[:], op=ALU.mult)
+                return
+            products[i] = products_pool.tile([P, HEADS_PER_BANK, 2, 2, HALF], F32, name="products", tag="products")
+            if BANKS[i][0] == "q":
+                m = BANKS[i][2]
                 halves = bank_t[i][:].rearrange("p (h w j) -> p h w j", w=2, j=HALF)
-                factor_b = factors[:, m, :, :, :].unsqueeze(1).to_broadcast([P, heads, 2, 2, HALF])
-                nc.vector.tensor_tensor(out=products[i][:], in0=halves.unsqueeze(3).to_broadcast([P, heads, 2, 2, HALF]), in1=factor_b, op=ALU.mult)
-            else:
-                pair = banks[i][1]
-                for h in range(heads):
-                    halves = bank_t[i][:, h * 2 * D:h * 2 * D + D].rearrange("p (w j) -> p w j", j=HALF)
-                    nc.vector.tensor_tensor(out=products[i][:, h, :, :, :], in0=halves.unsqueeze(2).to_broadcast([P, 2, 2, HALF]), in1=factors[:, 2 * pair + h, :, :, :], op=ALU.mult)
-            if banks[i][0] == "kv":
-                v_t = v_pool.tile([P, 2, D], F32, name="v_t", tag="v_t")
-                nc.vector.tensor_copy(out=v_t[:], in_=bank_t[i][:].rearrange("p (h e d) -> p h e d", e=2, d=D)[:, :, 1, :])
-                v_tiles[i] = v_t
+                factor = factors[:, m, 0:4, :].rearrange("p (w r) j -> p w r j", w=2)
+                nc.vector.tensor_tensor(
+                    out=products[i][:],
+                    in0=halves.unsqueeze(3).to_broadcast([P, heads, 2, 2, HALF]),
+                    in1=factor.unsqueeze(1).to_broadcast([P, heads, 2, 2, HALF]),
+                    op=ALU.mult,
+                )
+                return
+            pair = BANKS[i][1]
+            for h in range(heads):
+                halves = bank_t[i][:, h * 2 * D:h * 2 * D + D].rearrange("p (w j) -> p w j", j=HALF)
+                factor = factors[:, 2 * pair + h, 0:4, :].rearrange("p (w r) j -> p w r j", w=2)
+                nc.vector.tensor_tensor(out=products[i][:, h, :, :, :], in0=halves.unsqueeze(2).to_broadcast([P, 2, 2, HALF]), in1=factor, op=ALU.mult)
+            v_t = v_pool.tile([P, 2, D], F32, name="v_t", tag="v_t")
+            nc.vector.tensor_copy(out=v_t[:], in_=bank_t[i][:].rearrange("p (h e d) -> p h e d", e=2, d=D)[:, :, 1, :])
+            v_tiles[i] = v_t
 
         def add(i):
             heads = heads_of(i)
             rotated[i] = rotated_pool.tile([P, BANK_COLS], F32, name="rotated", tag="rotated")
-            engine = nc.vector if i in VECTOR_ADDS else nc.gpsimd
-            engine.tensor_tensor(
+            nc.gpsimd.tensor_tensor(
                 out=rotated[i][:, 0:heads * D].rearrange("p (h d) -> p h d", d=D),
                 in0=products[i][:, 0:heads, 0, :, :].rearrange("p h r j -> p h (r j)"),
                 in1=products[i][:, 0:heads, 1, :, :].rearrange("p h r j -> p h (r j)"),
                 op=ALU.add,
             )
 
+        def turn_back(i):
+            turned_bank[i] = psum.tile([P, TOKEN_TILES, D], F32, name="side", tag="side", bufs=BANK_BUFS["side"])
+            for m in range(TOKEN_TILES):
+                for r, permutation in ((0, identity), (1, swap)):
+                    nc.tensor.matmul(
+                        out=turned_bank[i][:, m, :],
+                        lhsT=products[i][:, r, m * P:(m + 1) * P],
+                        rhs=permutation[:],
+                        is_transpose=True,
+                        start=(r == 0),
+                        stop=(r == 1),
+                    )
+
         square_sums = {}
         inverse_rms = {}
 
-        def head_cols(h):
-            return slice(h * D, (h + 1) * D)
+        def piece(i, h):
+            return turned_bank[i][:, h, :] if turned(i) else rotated[i][:, h * D:(h + 1) * D]
 
         def sum_squares(i):
-            square_sums[i] = stats_pool.tile([P, BANK_COLS // D], F32, name="square_sums", tag="square_sums")
+            square_sums[i] = stats_pool.tile([P, 4], F32, name="square_sums", tag="square_sums")
             for h in range(heads_of(i)):
                 unread = scratch_pool.tile([P, D], BF16, name="unread", tag="unread")
-                nc.scalar.activation(out=unread[:], in_=rotated[i][:, head_cols(h)], func=ACT.Square, accum_out=square_sums[i][:, h:h + 1])
+                nc.scalar.activation(out=unread[:], in_=piece(i, h), func=ACT.Square, accum_out=square_sums[i][:, h:h + 1])
 
         def take_inverse_rms(i):
             heads = heads_of(i)
-            inverse_rms[i] = stats_pool.tile([P, BANK_COLS // D], F32, name="inverse_rms", tag="inverse_rms")
+            inverse_rms[i] = stats_pool.tile([P, 4], F32, name="inverse_rms", tag="inverse_rms")
             nc.scalar.activation(out=inverse_rms[i][:, 0:heads], in_=square_sums[i][:, 0:heads], func=ACT.Abs_reciprocal_sqrt, scale=1.0 / D, bias=EPS)
 
-        def vector_heads(i):
-            return VECTOR_SCALED_HEADS.get(i, VECTOR_SCALED_HEADS_DEFAULT)
-
         def scalar_scales(i):
-            for h in range(heads_of(i) - vector_heads(i)):
-                nc.scalar.activation(out=rotated[i][:, head_cols(h)], in_=rotated[i][:, head_cols(h)], func=ACT.Copy, scale=inverse_rms[i][:, h:h + 1])
+            if turned(i):
+                result[i] = result_pool.tile([P, TOKEN_TILES, D], F32, name="result", tag="result")
+            for h in range(scalar_heads(i)):
+                out = result[i][:, h, :] if turned(i) else piece(i, h)
+                nc.scalar.activation(out=out, in_=piece(i, h), func=ACT.Copy, scale=inverse_rms[i][:, h:h + 1])
 
         def vector_scales(i):
-            for h in range(heads_of(i) - vector_heads(i), heads_of(i)):
+            first, heads = scalar_heads(i), vector_heads(i)
+            if turned(i) and heads:
+                nc.vector.tensor_tensor(
+                    out=result[i][:, first:first + heads, :],
+                    in0=turned_bank[i][:, first:first + heads, :],
+                    in1=inverse_rms[i][:, first:first + heads].unsqueeze(2).to_broadcast([P, heads, D]),
+                    op=ALU.mult,
+                )
+                return
+            for h in range(first, first + heads):
                 nc.vector.tensor_scalar(
-                    out=rotated[i][:, head_cols(h)],
-                    in0=rotated[i][:, head_cols(h)],
+                    out=piece(i, h),
+                    in0=piece(i, h),
                     scalar1=inverse_rms[i][:, h:h + 1],
                     scalar2=None,
                     op0=ALU.mult,
@@ -406,52 +487,69 @@ def tile_multiqueryattention_pa_kernel(tc, x, cos, sin, Wq_bytes, Wq_scale, Wk, 
                     accum_out=unread_sums[:, i % SCRATCH_BUFS:i % SCRATCH_BUFS + 1],
                 )
 
+        def gpsimd_scales(i):
+            heads = heads_of(i)
+            view = rotated[i][:, 0:heads * D].rearrange("p (h d) -> p h d", d=D)
+            nc.gpsimd.tensor_tensor(out=view, in0=view, in1=inverse_rms[i][:, 0:heads].unsqueeze(2).to_broadcast([P, heads, D]), op=ALU.mult)
+
         def store(i):
-            if banks[i][0] == "q":
-                block, m = banks[i][1:]
+            if BANKS[i][0] == "t":
+                nc.sync.dma_start(out=q_head_out[BANKS[i][1]], in_=result[i][:])
+            elif BANKS[i][0] == "q":
+                block, m = BANKS[i][1:]
                 nc.sync.dma_start(out=q_out[m][:, block * BANK_COLS:(block + 1) * BANK_COLS], in_=rotated[i][:])
             else:
-                pair = banks[i][1]
+                pair = BANKS[i][1]
                 nc.sync.dma_start(out=k_out[:, 2 * pair:2 * pair + 2, :], in_=rotated[i][:, 0:2 * D].rearrange("p (h d) -> p h d", d=D))
 
         def store_v(i):
-            pair = banks[i][1]
+            pair = BANKS[i][1]
             nc.sync.dma_start(out=v_out[:, 2 * pair:2 * pair + 2, :], in_=v_tiles[i][:])
 
         actions = {
-            "store_v": store_v, "kv_pe_interleave": kv_pe_interleave, "kv_evacuate": kv_evacuate,
-            "transpose": transpose, "x_copy": x_copy, "x_quantise": x_quantise, "widen": widen, "scale_plane": scale_plane,
-            "interleave": interleave, "pe_interleave": pe_interleave, "evacuate": evacuate, "quantise": quantise,
-            "kv_interleave": kv_interleave, "kv_quantise": kv_quantise, "fill": fill, "negate_sin": negate_sin, "rope": rope, "add": add,
-            "sum_squares": sum_squares, "take_inverse_rms": take_inverse_rms, "scalar_scales": scalar_scales,
-            "vector_scales": vector_scales, "store": store,
+            "transpose": transpose, "x_copy": x_copy, "x_quantise": x_quantise, "widen": widen, "interleave": interleave,
+            "pe_interleave": pe_interleave, "evacuate": evacuate, "quantise": quantise, "kv_pe_interleave": kv_pe_interleave, "kv_evacuate": kv_evacuate, "kv_quantise": kv_quantise,
+            "negate_sin": negate_sin, "table_transpose": table_transpose, "table_copy": table_copy, "fill": fill, "rope": rope, "add": add,
+            "turn_back": turn_back, "sum_squares": sum_squares, "take_inverse_rms": take_inverse_rms, "scalar_scales": scalar_scales,
+            "gpsimd_scales": gpsimd_scales, "vector_scales": vector_scales, "store": store, "store_v": store_v,
         }
 
-        queues = make_queues(n_banks)
-        tile_readers = []
+        queues = make_queues()
+        readers = {"bank": [], "side": []}
         first_tile = {}
         for job in queues["tensor"]:
-            first_tile[job] = len(tile_readers)
+            tag = "bank" if job[0] in ("transpose", "fill") else "side"
+            first_tile[job] = (tag, len(readers[tag]))
             if job[0] == "transpose":
-                tile_readers.extend([("x_copy", job[1])] * 2)
+                readers[tag].extend([("x_copy", job[1])] * 2)
             elif job[0] == "pe_interleave":
-                tile_readers.append(("evacuate",) + job[1:])
+                readers[tag].append(("evacuate",) + job[1:])
             elif job[0] == "kv_pe_interleave":
-                tile_readers.append(("kv_evacuate", job[1]))
+                readers[tag].append(("kv_evacuate", job[1]))
+            elif job[0] == "table_transpose":
+                readers[tag].append(("table_copy",))
+            elif job[0] == "turn_back":
+                readers[tag].append(("vector_scales" if vector_heads(job[1]) else "scalar_scales", job[1]))
             else:
-                tile_readers.append(("rope", job[1]))
+                readers[tag].append(("rope", job[1]))
+        results_in_order = [i for i in range(N_BANKS) if turned(i)]
+        rotated_in_order = [i for i in range(N_BANKS) if not turned(i)]
 
         def buffers_free(job, tiles):
-            return [tile_readers[first_tile[job] + k - BANK_BUFS] for k in range(tiles) if first_tile[job] + k >= BANK_BUFS]
+            tag, first = first_tile[job]
+            return [readers[tag][first + k - BANK_BUFS[tag]] for k in range(tiles) if first + k >= BANK_BUFS[tag]]
 
         def planes_ready(u):
-            return [("scale_plane", u, t) if WIDEN[u][t] == "C" else ("widen", u, t) for t in range(PACK)]
+            return [("widen", u, t) for t in range(PACK)]
 
         def planes_read(u):
             return [("pe_interleave", u, b) for b in range(IL_PARTS)] if INTERLEAVE[u] == "P" else [("interleave", u)]
 
         def interleaved_made(u):
             return [("evacuate", u, b) for b in range(IL_PARTS)] if INTERLEAVE[u] == "P" else [("interleave", u)]
+
+        def earlier(i, order, steps):
+            return [order[order.index(i) - steps]] if order.index(i) >= steps else []
 
         def needs(job):
             kind = job[0]
@@ -460,15 +558,17 @@ def tile_multiqueryattention_pa_kernel(tc, x, cos, sin, Wq_bytes, Wq_scale, Wk, 
             if kind == "x_copy":
                 return [("transpose", job[1])]
             if kind == "x_quantise":
-                return [("x_copy", job[1])]
+                return [("x_copy", 2 * job[1]), ("x_copy", 2 * job[1] + 1)]
+            if kind == "table_transpose":
+                return buffers_free(job, 1) + [("negate_sin",)]
+            if kind == "table_copy":
+                return [("table_transpose",)]
             if kind == "widen":
                 u = job[1]
                 out = [("widen", v, t) for v in back(u, 1) for t in range(PACK)]
                 for v in back(u, WIDE_BUFS[stream_of(u)]):
                     out = out + planes_read(v)
                 return out
-            if kind == "scale_plane":
-                return [("widen", job[1], job[2])]
             if kind == "interleave" or (kind == "evacuate" and job[2] == 0):
                 u = job[1]
                 out = planes_ready(u) if kind == "interleave" else [("pe_interleave", u, 0)]
@@ -482,7 +582,7 @@ def tile_multiqueryattention_pa_kernel(tc, x, cos, sin, Wq_bytes, Wq_scale, Wk, 
             if kind == "quantise":
                 return interleaved_made(job[1])
             if kind == "kv_quantise":
-                return [("kv_evacuate", g) for g in range(PASSES)] if KV_INTERLEAVE == "PP" else [("kv_interleave", 0), ("kv_interleave", 1)]
+                return [("kv_evacuate", g) for g in range(PASSES)]
             if kind == "kv_pe_interleave":
                 return buffers_free(job, 1)
             if kind == "kv_evacuate":
@@ -490,30 +590,46 @@ def tile_multiqueryattention_pa_kernel(tc, x, cos, sin, Wq_bytes, Wq_scale, Wk, 
             if kind == "fill":
                 i = job[1]
                 out = buffers_free(job, 1)
-                if banks[i][0] == "q":
-                    block, m = banks[i][1:]
-                    first_unit = (block // BANKS_PER_UNIT) * PASSES
-                    return out + [("x_quantise", m)] + [("quantise", first_unit + g) for g in range(PASSES)]
-                return out + [("kv_quantise",), ("x_quantise", 2 * banks[i][1]), ("x_quantise", 2 * banks[i][1] + 1)]
+                if BANKS[i][0] == "kv":
+                    return out + [("kv_quantise",), ("x_quantise", BANKS[i][1])]
+                if BANKS[i][0] == "t":
+                    out = out + [("x_quantise", 0), ("x_quantise", 1)]
+                    half = BANKS[i][1] // HEADS_PER_UNIT
+                else:
+                    out = out + [("x_quantise", BANKS[i][2] // 2)]
+                    half = BANKS[i][1] // (UNIT_COLS // BANK_COLS)
+                return out + [("quantise", half * PASSES + g) for g in range(PASSES)]
             if kind == "rope":
                 i = job[1]
                 out = [("fill", i), ("negate_sin",)] + ([("rope", i - 1)] if i else [])
-                return out + ([("add", i - SWAPPED_BUFS)] if i >= SWAPPED_BUFS else [])
+                if turned(i):
+                    out.append(("table_copy",))
+                if i >= PRODUCTS_BUFS:
+                    out.append(("turn_back" if turned(i - PRODUCTS_BUFS) else "add", i - PRODUCTS_BUFS))
+                return out
             if kind == "add":
                 i = job[1]
-                return [("rope", i)] + ([("add", i - 1)] if i else []) + ([("store", i - ROTATED_BUFS)] if i >= ROTATED_BUFS else [])
+                before = earlier(i, rotated_in_order, 1)
+                return [("rope", i)] + [("add", k) for k in before] + [("store", k) for k in earlier(i, rotated_in_order, ROTATED_BUFS)]
+            if kind == "turn_back":
+                return [("rope", job[1])] + buffers_free(job, 1)
             if kind == "sum_squares":
-                return [("add", job[1])]
+                return [("turn_back" if turned(job[1]) else "add", job[1])]
             if kind == "take_inverse_rms":
                 return [("sum_squares", job[1])]
-            if kind == "vector_scales" and vector_heads(job[1]) == 0:
-                return []
-            if kind in ("scalar_scales", "vector_scales"):
+            if kind == "scalar_scales":
+                i = job[1]
+                if not scalar_heads(i) and not turned(i):
+                    return []
+                return [("take_inverse_rms", i)] + ([("store", k) for k in earlier(i, results_in_order, RESULT_BUFS)] if turned(i) else [])
+            if kind == "gpsimd_scales":
                 return [("take_inverse_rms", job[1])]
+            if kind == "vector_scales":
+                return [("scalar_scales", job[1])] if turned(job[1]) else [("take_inverse_rms", job[1])] if vector_heads(job[1]) else []
             if kind == "store_v":
                 return [("rope", job[1])]
             if kind == "store":
-                return [("scalar_scales", job[1]), ("vector_scales", job[1])] + ([("store", job[1] - 1)] if job[1] else [])
+                return [("gpsimd_scales", job[1])] if job[1] in GPSIMD_SCALES else [("scalar_scales", job[1]), ("vector_scales", job[1])]
             return []
 
         written = set()

@@ -34,7 +34,7 @@ INTERLEAVE = "XPXPXYYS"
 STREAMS = ((0, 2, 4, 5, 6), (1, 3, 7))
 WIDE_BUFS = (2, 2)
 INTERLEAVED_BUFS = (2, 2)
-LOAD_ORDER = (("p", 0, 0), ("p", 1, 0), ("p", 0, 1), ("p", 1, 1), ("p", 0, 2), ("p", 0, 3), ("p", 1, 2), ("p", 1, 3), ("u", 2), ("u", 3), ("u", 4), ("x", 0), ("x", 1), ("u", 5), ("c",), ("u", 7), ("x", 2), ("x", 3), ("u", 6), ("k",), ("v",))
+LOAD_ORDER = (("p", 0, 0), ("p", 1, 0), ("p", 0, 2), ("p", 1, 2), ("p", 0, 1), ("p", 0, 3), ("p", 1, 1), ("p", 1, 3), ("u", 2), ("u", 3), ("u", 4), ("x", 0), ("x", 1), ("u", 5), ("c",), ("u", 7), ("x", 2), ("x", 3), ("u", 6), ("k",), ("v",))
 BANKS = tuple(("q", block, m) for block in range(4) for m in range(4)) + (("kv", 0), ("kv", 1))
 N_BANKS = len(BANKS)
 LATE_FIRST = 8
@@ -66,7 +66,8 @@ def jobs(text):
     for name in text.split():
         letter, rest = name[0], name[1:]
         if letter == "w":
-            planes = range(PACK) if rest[-1] not in "ab" else range(2) if rest[-1] == "a" else range(2, PACK)
+            order = (0, 2, 1, 3)
+            planes = order if rest[-1] not in "ab" else order[:2] if rest[-1] == "a" else order[2:]
             out.extend([("widen", int(rest[0]), t) for t in planes])
         elif letter in "ep":
             out.extend([("evacuate" if letter == "e" else "pe_interleave", int(rest), b) for b in range(IL_PARTS)])
@@ -170,7 +171,7 @@ def tile_multiqueryattention_pa_kernel(tc, x, cos, sin, Wq_bytes, Wq_scale, Wk, 
         table = keep.tile([P, 2, TOKENS], BF16, name="table")
         wq_bytes_t = [keep.tile([P, PASSES, PACK, UNIT_COLS], U8, name="wq_bytes_t%d" % half) for half in range(UNITS // PASSES)]
         x_t = [keep.tile([P, DIM], BF16, name="x_t%d" % m) for m in range(TOKEN_TILES)]
-        x_interleaved = keep.tile([P, PASSES, TOKENS, PACK], BF16, name="x_interleaved", align_bytes=64)
+        x_interleaved = [keep.tile([P, PASSES, 2 * P, PACK], BF16, name="x_interleaved%d" % pair, align_bytes=64) for pair in range(TOKEN_TILES // 2)]
         x_codes = keep.tile([P, PASSES, TOKENS], U32, name="x_codes", align_bytes=64)
         x_scales = keep.tile([P, PASSES, TOKENS], U8, name="x_scales", align_bytes=64)
         wq_codes = [keep.tile([P, PASSES, UNIT_COLS], U32, name="wq_codes%d" % half, align_bytes=64) for half in range(UNITS // PASSES)]
@@ -232,7 +233,8 @@ def tile_multiqueryattention_pa_kernel(tc, x, cos, sin, Wq_bytes, Wq_scale, Wk, 
 
         def x_copy(m):
             for a in range(2):
-                target = x_interleaved[:, 2 * a:2 * a + 2, m * P:(m + 1) * P, :].bitcast(F32)
+                pair, r = divmod(m, 2)
+                target = x_interleaved[pair][:, 2 * a:2 * a + 2, r * P:(r + 1) * P, :].bitcast(F32)
                 nc.scalar.copy(out=target, in_=x_transposed[(m, a)][:].rearrange("p g w r -> p g r w"))
 
         def x_quantise(pair):
@@ -241,7 +243,7 @@ def tile_multiqueryattention_pa_kernel(tc, x, cos, sin, Wq_bytes, Wq_scale, Wk, 
                 nc.vector.quantize_mx(
                     out=x_codes[:, g, cols].bitcast(FP8X4),
                     scales=x_scales[:, g, cols],
-                    in_=x_interleaved[:, g, cols, :].rearrange("p r t -> p (r t)"),
+                    in_=x_interleaved[pair][:, g, :, :].rearrange("p r t -> p (r t)"),
                 )
 
         wide = {}

@@ -34,30 +34,30 @@ INTERLEAVE = "XPXPXYYS"
 STREAMS = ((0, 2, 4, 5, 6), (1, 3, 7))
 WIDE_BUFS = (2, 2)
 INTERLEAVED_BUFS = (2, 2)
-LOAD_ORDER = (("p", 0, 0), ("p", 1, 0), ("p", 0, 2), ("p", 1, 2), ("p", 0, 1), ("p", 0, 3), ("p", 1, 1), ("p", 1, 3), ("u", 2), ("u", 3), ("u", 4), ("x", 0), ("x", 1), ("u", 5), ("c",), ("u", 7), ("x", 2), ("x", 3), ("u", 6), ("k",), ("v",))
-BANKS = tuple(("q", block, m) for block in range(4) for m in range(4)) + (("kv", 0), ("kv", 1))
+LOAD_ORDER = (("p", 0, 0), ("p", 1, 0), ("p", 0, 2), ("p", 1, 1), ("p", 0, 1), ("p", 1, 2), ("p", 0, 3), ("p", 1, 3), ("u", 2), ("u", 3), ("u", 4), ("x", 0), ("x", 1), ("c",), ("x", 2), ("x", 3), ("u", 7), ("k",), ("v",), ("u", 5), ("u", 6))
+BANKS = (("q", 1, 0), ("t", 0), ("q", 1, 1), ("t", 1), ("q", 1, 2), ("t", 2), ("q", 1, 3), ("t", 3), ("q", 2, 0), ("q", 2, 1), ("q", 2, 2), ("q", 2, 3), ("q", 3, 0), ("q", 3, 1), ("q", 3, 2), ("q", 3, 3), ("kv", 0), ("kv", 1),)
 N_BANKS = len(BANKS)
 LATE_FIRST = 8
 GPSIMD_SCALES = ()
-VECTOR_SCALES = {4: 1, 5: 1, 6: 1, 7: 1, 8: 1, 9: 1, 10: 1, 11: 1, 12: 2, 13: 2, 14: 2, 15: 2, 16: 1, 17: 1}
+VECTOR_SCALES = {4: 1, 6: 1, 8: 1, 9: 1, 10: 1, 11: 1, 12: 1, 13: 2, 14: 2, 15: 3, 16: 1, 17: 1}
 VECTOR_LAG = 3
 FILL_AHEAD = 3
 GPSIMD_LAG = 3
 ROTATED_BUFS = 8
 RESULT_BUFS = 3
-PRODUCTS_BUFS = 3
+PRODUCTS_BUFS = 4
 SCRATCH_BUFS = 8
 BANK_BUFS = {"bank": 4, "side": 4}
 SHORT = {
     "i": "interleave", "q": "quantise", "x": "x_copy", "X": "x_quantise", "T": "transpose", "t": "table_copy", "k": "kv_evacuate",
     "K": "kv_pe_interleave", "n": "negate_sin", "Q": "kv_quantise", "t": "table_copy", "b": "table_transpose",
 }
-SCALAR_FIRST = "w1 w3 e1 x0 x1 w7a e3 x2 x3 w7b i5 i6 i7"
-VECTOR_FIRST = "w0 w2 i0 w4 q0 i2 w5 n q2 i4 w6 q4 q1 X0 q3 X1"
-TENSOR_FIRST = "p1 T0 T1 p3 T2 T3"
-VECTOR_LATE = {1: "q5", 4: "q6", 6: "q7", 10: "Q"}
-TENSOR_LATE = {7: "K0 K1 K2 K3"}
-SCALAR_LATE = {4: "k0 k1 k2 k3"}
+SCALAR_FIRST = "s1 s3 e1 x0 x1 e3 x2 x3 t s7 k0 k1 k2 k3 i7 i5"
+VECTOR_FIRST = "v0 v2 i0 v4 q0 i2 n q2 q1 i4 X0 q3 X1 v5 q4 v6"
+TENSOR_FIRST = "p1 T0 T1 p3 T2 T3 b K0 K1 K2 K3"
+VECTOR_LATE = {7: "q5 q6 q7 Q"}
+TENSOR_LATE = {}
+SCALAR_LATE = {0: 'i6'}
 QUEUE_NAMES = ("scalar", "vector", "tensor", "gpsimd", "sync")
 
 
@@ -65,10 +65,10 @@ def jobs(text):
     out = []
     for name in text.split():
         letter, rest = name[0], name[1:]
-        if letter == "w":
-            order = (0, 2, 1, 3)
-            planes = order if rest[-1] not in "ab" else order[:2] if rest[-1] == "a" else order[2:]
-            out.extend([("widen", int(rest[0]), t) for t in planes])
+        if letter in "sv":
+            u = int(rest)
+            order = (0, 2, 1, 3) if "D" in WIDEN[u] else range(PACK)
+            out.extend([("widen", u, t) for t in order if (WIDEN[u][t] == "A") == (letter == "s")])
         elif letter in "ep":
             out.extend([("evacuate" if letter == "e" else "pe_interleave", int(rest), b) for b in range(IL_PARTS)])
         elif rest:
@@ -141,7 +141,7 @@ def tile_multiqueryattention_pa_kernel(tc, x, cos, sin, Wq_bytes, Wq_scale, Wk, 
         interleaved_pool = ctx.enter_context(tc.tile_pool(name="interleaved", bufs=1))
         rotated_pool = ctx.enter_context(tc.tile_pool(name="rotated", bufs=ROTATED_BUFS))
         result_pool = ctx.enter_context(tc.tile_pool(name="result", bufs=RESULT_BUFS))
-        products_pool = ctx.enter_context(tc.tile_pool(name="products", bufs=PRODUCTS_BUFS))
+        products_pool = ctx.enter_context(tc.tile_pool(name="products", bufs=1))
         stats_pool = ctx.enter_context(tc.tile_pool(name="stats", bufs=8))
         scratch_pool = ctx.enter_context(tc.tile_pool(name="scratch", bufs=SCRATCH_BUFS))
         v_pool = ctx.enter_context(tc.tile_pool(name="v", bufs=2))
@@ -170,7 +170,7 @@ def tile_multiqueryattention_pa_kernel(tc, x, cos, sin, Wq_bytes, Wq_scale, Wk, 
         factors = keep.tile([P, TOKEN_TILES, 5, HALF], BF16, name="factors")
         table = keep.tile([P, 2, TOKENS], BF16, name="table")
         wq_bytes_t = [keep.tile([P, PASSES, PACK, UNIT_COLS], U8, name="wq_bytes_t%d" % half) for half in range(UNITS // PASSES)]
-        x_t = [keep.tile([P, DIM], BF16, name="x_t%d" % m) for m in range(TOKEN_TILES)]
+        x_t = [products_pool.tile([P, DIM], BF16, name="x_t%d" % m, tag="products", bufs=PRODUCTS_BUFS) for m in range(TOKEN_TILES)]
         x_interleaved = [keep.tile([P, PASSES, 2 * P, PACK], BF16, name="x_interleaved%d" % pair, align_bytes=64) for pair in range(TOKEN_TILES // 2)]
         x_codes = keep.tile([P, PASSES, TOKENS], U32, name="x_codes", align_bytes=64)
         x_scales = keep.tile([P, PASSES, TOKENS], U8, name="x_scales", align_bytes=64)
@@ -267,6 +267,8 @@ def tile_multiqueryattention_pa_kernel(tc, x, cos, sin, Wq_bytes, Wq_scale, Wk, 
                 pair, place = divmod(t, 2)
                 out = wide[u][:, pair * 2 * UNIT_COLS + place:(pair + 1) * 2 * UNIT_COLS:2]
                 nc.vector.tensor_scalar(out=out, in0=codes, scalar1=scale, scalar2=None, op0=ALU.mult)
+            elif WIDEN[u][t] == "B":
+                nc.vector.tensor_scalar(out=wide[u][:, t * UNIT_COLS:(t + 1) * UNIT_COLS], in0=codes, scalar1=scale, scalar2=None, op0=ALU.mult)
             else:
                 nc.scalar.activation(out=wide[u][:, t * UNIT_COLS:(t + 1) * UNIT_COLS], in_=codes, func=ACT.Copy, scale=scale)
 
@@ -277,11 +279,13 @@ def tile_multiqueryattention_pa_kernel(tc, x, cos, sin, Wq_bytes, Wq_scale, Wk, 
 
         def interleave(u):
             new_interleaved(u)
-            if INTERLEAVE[u] == "S":
-                nc.scalar.copy(
-                    out=interleaved[u][:].rearrange("p (c i t) -> p c t i", i=4, t=PACK),
-                    in_=wide[u][:].rearrange("p (t c i) -> p c t i", t=PACK, i=4),
-                )
+            if INTERLEAVE[u] in "SV":
+                target = interleaved[u][:].rearrange("p (c i t) -> p c t i", i=4, t=PACK)
+                planes = wide[u][:].rearrange("p (t c i) -> p c t i", t=PACK, i=4)
+                if INTERLEAVE[u] == "S":
+                    nc.scalar.copy(out=target, in_=planes)
+                else:
+                    nc.vector.tensor_copy(out=target, in_=planes)
                 return
             words = wide[u][:].bitcast(F32).rearrange("p (a n) -> p n a", a=2)
             target = interleaved[u][:].bitcast(F32).rearrange("p (n a) -> p n a", a=2)
@@ -397,10 +401,10 @@ def tile_multiqueryattention_pa_kernel(tc, x, cos, sin, Wq_bytes, Wq_scale, Wk, 
         def rope(i):
             heads = heads_of(i)
             if BANKS[i][0] == "t":
-                products[i] = products_pool.tile([P, 2, TOKENS], F32, name="products", tag="products")
+                products[i] = products_pool.tile([P, 2, TOKENS], F32, name="products", tag="products", bufs=PRODUCTS_BUFS)
                 nc.vector.tensor_tensor(out=products[i][:], in0=bank_t[i][:].unsqueeze(1).to_broadcast([P, 2, TOKENS]), in1=table[:], op=ALU.mult)
                 return
-            products[i] = products_pool.tile([P, HEADS_PER_BANK, 2, 2, HALF], F32, name="products", tag="products")
+            products[i] = products_pool.tile([P, HEADS_PER_BANK, 2, 2, HALF], F32, name="products", tag="products", bufs=PRODUCTS_BUFS)
             if BANKS[i][0] == "q":
                 m = BANKS[i][2]
                 halves = bank_t[i][:].rearrange("p (h w j) -> p h w j", w=2, j=HALF)

@@ -30,17 +30,17 @@ IL_PARTS = UNIT_COLS // IL_COLS
 FLOPS = 2 * TOKENS * DIM * (HEADS * D + 2 * D)
 
 WIDEN = ("DDDD", "AAAA", "DDDD", "AAAA", "DDDD", "DDDD", "DDDD", "AAAA")
-INTERLEAVE = "XPXPXYYS"
+INTERLEAVE = "XPXPXYYH"
 STREAMS = ((0, 2, 4, 5, 6), (1, 3, 7))
 WIDE_BUFS = (2, 2)
 INTERLEAVED_BUFS = (2, 2)
 LOAD_ORDER = (("p", 0, 0), ("p", 1, 0), ("p", 0, 2), ("p", 1, 1), ("p", 0, 1), ("p", 1, 2), ("p", 0, 3), ("p", 1, 3), ("u", 2), ("u", 3), ("u", 4), ("x", 0), ("x", 1), ("c",), ("x", 2), ("x", 3), ("u", 7), ("k",), ("v",), ("u", 5), ("u", 6))
-BANKS = (("q", 1, 0), ("t", 0), ("q", 1, 1), ("t", 1), ("q", 1, 2), ("t", 2), ("q", 1, 3), ("t", 3), ("q", 2, 0), ("q", 2, 1), ("q", 2, 2), ("q", 2, 3), ("q", 3, 0), ("q", 3, 1), ("q", 3, 2), ("q", 3, 3), ("kv", 0), ("kv", 1),)
+BANKS = (("q", 1, 0), ("t", 0), ("q", 1, 1), ("t", 1), ("q", 1, 2), ("t", 2), ("q", 1, 3), ("t", 3), ("q", 2, 0), ("q", 2, 1), ("q", 2, 2), ("q", 2, 3), ("s", 12), ("s", 13), ("s", 14), ("t", 15), ("kv", 0), ("kv", 1),)
 N_BANKS = len(BANKS)
 LATE_FIRST = 8
 GPSIMD_SCALES = ()
-VECTOR_SCALES = {4: 1, 6: 1, 8: 1, 9: 1, 10: 1, 11: 1, 12: 1, 13: 2, 14: 2, 15: 3, 16: 1, 17: 1}
-VECTOR_LAG = 3
+VECTOR_SCALES = {8: 1, 9: 1, 10: 1, 11: 1, 12: 3, 13: 3, 14: 3, 15: 4}
+VECTOR_LAG = 4
 FILL_AHEAD = 3
 GPSIMD_LAG = 3
 ROTATED_BUFS = 8
@@ -52,11 +52,13 @@ SHORT = {
     "i": "interleave", "q": "quantise", "x": "x_copy", "X": "x_quantise", "T": "transpose", "t": "table_copy", "k": "kv_evacuate",
     "K": "kv_pe_interleave", "n": "negate_sin", "Q": "kv_quantise", "t": "table_copy", "b": "table_transpose",
 }
-SCALAR_FIRST = "s1 s3 e1 x0 x1 e3 x2 x3 t s7 k0 k1 k2 k3 i7 i5"
-VECTOR_FIRST = "v0 v2 i0 v4 q0 i2 n q2 q1 i4 X0 q3 X1 v5 q4 v6"
-TENSOR_FIRST = "p1 T0 T1 p3 T2 T3 b K0 K1 K2 K3"
+SCALAR_FIRST = "s1 s3 e1 x0 x1 e3 x2 x3 t s7 k0 k1 k2 k3 i7 e7 i5"
+VECTOR_FIRST = "v0 v2 i0 v4 q0 i2 n q2 q1 i4 v5 q3 X q4 v6"
+TENSOR_FIRST = "p1 T0 T1 p3 T2 T3 b K0 K1 K2 K3 p7"
 VECTOR_LATE = {7: "q5 q6 q7 Q"}
+TENSOR_MIDDLE = ""
 TENSOR_LATE = {}
+SCALAR_BEFORE = {}
 SCALAR_LATE = {0: 'i6'}
 QUEUE_NAMES = ("scalar", "vector", "tensor", "gpsimd", "sync")
 
@@ -70,12 +72,16 @@ def jobs(text):
             order = (0, 2, 1, 3) if "D" in WIDEN[u] else range(PACK)
             out.extend([("widen", u, t) for t in order if (WIDEN[u][t] == "A") == (letter == "s")])
         elif letter in "ep":
-            out.extend([("evacuate" if letter == "e" else "pe_interleave", int(rest), b) for b in range(IL_PARTS)])
+            out.extend([("evacuate" if letter == "e" else "pe_interleave", int(rest), b) for b in turned_parts(int(rest))])
         elif rest:
             out.append((SHORT[letter], int(rest)))
         else:
             out.append((SHORT[letter],))
     return out
+
+
+def turned_parts(u):
+    return range(IL_PARTS) if INTERLEAVE[u] == "P" else range(IL_PARTS // 2) if INTERLEAVE[u] == "H" else ()
 
 
 def turned(i):
@@ -98,13 +104,14 @@ def make_queues():
     scalar, vector, tensor, gpsimd, sync = [], [], [], [], []
     scalar += jobs(SCALAR_FIRST)
     for i in range(N_BANKS + 2):
-        if i >= 2:
-            scalar.append(("take_inverse_rms", i - 2))
-        if 1 <= i < N_BANKS + 1:
-            scalar.append(("sum_squares", i - 1))
+        if i < N_BANKS:
+            scalar.extend(jobs(SCALAR_BEFORE.get(i, "")))
+            scalar.append(("sum_squares", i))
         if i >= 2:
             scalar.append(("scalar_scales", i - 2))
             scalar.extend(jobs(SCALAR_LATE.get(i - 2, "")))
+        if i % 2 and i < N_BANKS:
+            scalar.append(("take_inverse_rms", i // 2))
     vector += jobs(VECTOR_FIRST)
     for i in range(N_BANKS + VECTOR_LAG):
         if i < N_BANKS:
@@ -120,6 +127,8 @@ def make_queues():
                 tensor.extend(jobs(TENSOR_LATE.get(i, "")))
             if i - FILL_AHEAD >= banks.start and turned(i - FILL_AHEAD):
                 tensor.append(("turn_back", i - FILL_AHEAD))
+        if banks.start == 0:
+            tensor.extend(jobs(TENSOR_MIDDLE))
     for i in range(N_BANKS + GPSIMD_LAG):
         if i < N_BANKS and not turned(i):
             gpsimd.append(("add", i))
@@ -127,8 +136,7 @@ def make_queues():
             gpsimd.append(("gpsimd_scales", i - GPSIMD_LAG))
     for i in range(N_BANKS):
         sync.append(("store", i))
-        if BANKS[i][0] == "kv":
-            sync.append(("store_v", i))
+        sync.extend([("store_v", k) for k in range(i + 1, N_BANKS) if BANKS[k][0] == "kv" and k - 3 == i])
     return {"scalar": scalar, "vector": vector, "tensor": tensor, "gpsimd": gpsimd, "sync": sync}
 
 
@@ -171,7 +179,7 @@ def tile_multiqueryattention_pa_kernel(tc, x, cos, sin, Wq_bytes, Wq_scale, Wk, 
         table = keep.tile([P, 2, TOKENS], BF16, name="table")
         wq_bytes_t = [keep.tile([P, PASSES, PACK, UNIT_COLS], U8, name="wq_bytes_t%d" % half) for half in range(UNITS // PASSES)]
         x_t = [products_pool.tile([P, DIM], BF16, name="x_t%d" % m, tag="products", bufs=PRODUCTS_BUFS) for m in range(TOKEN_TILES)]
-        x_interleaved = [keep.tile([P, PASSES, 2 * P, PACK], BF16, name="x_interleaved%d" % pair, align_bytes=64) for pair in range(TOKEN_TILES // 2)]
+        x_interleaved = keep.tile([P, PASSES, TOKENS, PACK], BF16, name="x_interleaved", align_bytes=64)
         x_codes = keep.tile([P, PASSES, TOKENS], U32, name="x_codes", align_bytes=64)
         x_scales = keep.tile([P, PASSES, TOKENS], U8, name="x_scales", align_bytes=64)
         wq_codes = [keep.tile([P, PASSES, UNIT_COLS], U32, name="wq_codes%d" % half, align_bytes=64) for half in range(UNITS // PASSES)]
@@ -233,17 +241,15 @@ def tile_multiqueryattention_pa_kernel(tc, x, cos, sin, Wq_bytes, Wq_scale, Wk, 
 
         def x_copy(m):
             for a in range(2):
-                pair, r = divmod(m, 2)
-                target = x_interleaved[pair][:, 2 * a:2 * a + 2, r * P:(r + 1) * P, :].bitcast(F32)
+                target = x_interleaved[:, 2 * a:2 * a + 2, m * P:(m + 1) * P, :].bitcast(F32)
                 nc.scalar.copy(out=target, in_=x_transposed[(m, a)][:].rearrange("p g w r -> p g r w"))
 
-        def x_quantise(pair):
-            cols = slice(pair * 2 * P, (pair + 1) * 2 * P)
+        def x_quantise():
             for g in range(PASSES):
                 nc.vector.quantize_mx(
-                    out=x_codes[:, g, cols].bitcast(FP8X4),
-                    scales=x_scales[:, g, cols],
-                    in_=x_interleaved[pair][:, g, :, :].rearrange("p r t -> p (r t)"),
+                    out=x_codes[:, g, :].bitcast(FP8X4),
+                    scales=x_scales[:, g, :],
+                    in_=x_interleaved[:, g, :, :].rearrange("p r t -> p (r t)"),
                 )
 
         wide = {}
@@ -279,6 +285,13 @@ def tile_multiqueryattention_pa_kernel(tc, x, cos, sin, Wq_bytes, Wq_scale, Wk, 
 
         def interleave(u):
             new_interleaved(u)
+            if INTERLEAVE[u] == "H":
+                first = UNIT_COLS // 2
+                nc.scalar.copy(
+                    out=interleaved[u][:, first * PACK:].rearrange("p (c i t) -> p c t i", i=4, t=PACK),
+                    in_=wide[u][:].rearrange("p (t n) -> p t n", t=PACK)[:, :, first:].rearrange("p t (c i) -> p c t i", i=4),
+                )
+                return
             if INTERLEAVE[u] in "SV":
                 target = interleaved[u][:].rearrange("p (c i t) -> p c t i", i=4, t=PACK)
                 planes = wide[u][:].rearrange("p (t c i) -> p c t i", t=PACK, i=4)
@@ -308,7 +321,7 @@ def tile_multiqueryattention_pa_kernel(tc, x, cos, sin, Wq_bytes, Wq_scale, Wk, 
                 )
 
         def evacuate(u, b):
-            if b == 0:
+            if b == 0 and INTERLEAVE[u] == "P":
                 new_interleaved(u)
             target = interleaved[u][:, b * IL_COLS * PACK:(b + 1) * IL_COLS * PACK]
             nc.scalar.copy(out=target.bitcast(F32), in_=il_bank[(u, b)][:].bitcast(F32))
@@ -383,6 +396,10 @@ def tile_multiqueryattention_pa_kernel(tc, x, cos, sin, Wq_bytes, Wq_scale, Wk, 
             if BANKS[i][0] == "t":
                 half, h = divmod(BANKS[i][1], HEADS_PER_UNIT)
                 passes_mx(bank_t[i][:], wq_operand(half, h * D, D), x_operand(0, TOKENS))
+            elif BANKS[i][0] == "s":
+                half, h = divmod(BANKS[i][1], HEADS_PER_UNIT)
+                for m in range(TOKEN_TILES):
+                    passes_mx(bank_t[i][:, m * D:(m + 1) * D], x_operand(m * P, P), wq_operand(half, h * D, D))
             elif BANKS[i][0] == "q":
                 block, m = BANKS[i][1:]
                 half, part = divmod(block, UNIT_COLS // BANK_COLS)
@@ -405,16 +422,13 @@ def tile_multiqueryattention_pa_kernel(tc, x, cos, sin, Wq_bytes, Wq_scale, Wk, 
                 nc.vector.tensor_tensor(out=products[i][:], in0=bank_t[i][:].unsqueeze(1).to_broadcast([P, 2, TOKENS]), in1=table[:], op=ALU.mult)
                 return
             products[i] = products_pool.tile([P, HEADS_PER_BANK, 2, 2, HALF], F32, name="products", tag="products", bufs=PRODUCTS_BUFS)
-            if BANKS[i][0] == "q":
-                m = BANKS[i][2]
+            if BANKS[i][0] in "qs":
                 halves = bank_t[i][:].rearrange("p (h w j) -> p h w j", w=2, j=HALF)
-                factor = factors[:, m, 0:4, :].rearrange("p (w r) j -> p w r j", w=2)
-                nc.vector.tensor_tensor(
-                    out=products[i][:],
-                    in0=halves.unsqueeze(3).to_broadcast([P, heads, 2, 2, HALF]),
-                    in1=factor.unsqueeze(1).to_broadcast([P, heads, 2, 2, HALF]),
-                    op=ALU.mult,
-                )
+                if BANKS[i][0] == "q":
+                    factor = factors[:, BANKS[i][2], 0:4, :].rearrange("p (w r) j -> p w r j", w=2).unsqueeze(1).to_broadcast([P, heads, 2, 2, HALF])
+                else:
+                    factor = factors[:, :, 0:4, :].rearrange("p m (w r) j -> p m w r j", w=2)
+                nc.vector.tensor_tensor(out=products[i][:], in0=halves.unsqueeze(3).to_broadcast([P, heads, 2, 2, HALF]), in1=factor, op=ALU.mult)
                 return
             pair = BANKS[i][1]
             for h in range(heads):
@@ -455,15 +469,18 @@ def tile_multiqueryattention_pa_kernel(tc, x, cos, sin, Wq_bytes, Wq_scale, Wk, 
             return turned_bank[i][:, h, :] if turned(i) else rotated[i][:, h * D:(h + 1) * D]
 
         def sum_squares(i):
-            square_sums[i] = stats_pool.tile([P, 4], F32, name="square_sums", tag="square_sums")
+            if i % 2 == 0:
+                square_sums[i // 2] = stats_pool.tile([P, 2, 4], F32, name="square_sums", tag="square_sums")
             for h in range(heads_of(i)):
                 unread = scratch_pool.tile([P, D], BF16, name="unread", tag="unread")
-                nc.scalar.activation(out=unread[:], in_=piece(i, h), func=ACT.Square, accum_out=square_sums[i][:, h:h + 1])
+                nc.scalar.activation(out=unread[:], in_=piece(i, h), func=ACT.Square, accum_out=square_sums[i // 2][:, i % 2, h:h + 1])
 
-        def take_inverse_rms(i):
-            heads = heads_of(i)
-            inverse_rms[i] = stats_pool.tile([P, 4], F32, name="inverse_rms", tag="inverse_rms")
-            nc.scalar.activation(out=inverse_rms[i][:, 0:heads], in_=square_sums[i][:, 0:heads], func=ACT.Abs_reciprocal_sqrt, scale=1.0 / D, bias=EPS)
+        def take_inverse_rms(pair):
+            heads = heads_of(2 * pair)
+            both = stats_pool.tile([P, 2, 4], F32, name="inverse_rms", tag="inverse_rms")
+            nc.scalar.activation(out=both[:, :, 0:heads], in_=square_sums[pair][:, :, 0:heads], func=ACT.Abs_reciprocal_sqrt, scale=1.0 / D, bias=EPS)
+            for r in range(2):
+                inverse_rms[2 * pair + r] = both[:, r, :]
 
         def scalar_scales(i):
             if turned(i):
@@ -501,6 +518,8 @@ def tile_multiqueryattention_pa_kernel(tc, x, cos, sin, Wq_bytes, Wq_scale, Wk, 
         def store(i):
             if BANKS[i][0] == "t":
                 nc.sync.dma_start(out=q_head_out[BANKS[i][1]], in_=result[i][:])
+            elif BANKS[i][0] == "s":
+                nc.sync.dma_start(out=q_head_out[BANKS[i][1]], in_=rotated[i][:].rearrange("p (m d) -> p m d", d=D))
             elif BANKS[i][0] == "q":
                 block, m = BANKS[i][1:]
                 nc.sync.dma_start(out=q_out[m][:, block * BANK_COLS:(block + 1) * BANK_COLS], in_=rotated[i][:])
@@ -549,10 +568,10 @@ def tile_multiqueryattention_pa_kernel(tc, x, cos, sin, Wq_bytes, Wq_scale, Wk, 
             return [("widen", u, t) for t in range(PACK)]
 
         def planes_read(u):
-            return [("pe_interleave", u, b) for b in range(IL_PARTS)] if INTERLEAVE[u] == "P" else [("interleave", u)]
+            return [("pe_interleave", u, b) for b in turned_parts(u)] + ([("interleave", u)] if INTERLEAVE[u] != "P" else [])
 
         def interleaved_made(u):
-            return [("evacuate", u, b) for b in range(IL_PARTS)] if INTERLEAVE[u] == "P" else [("interleave", u)]
+            return ([("interleave", u)] if INTERLEAVE[u] != "P" else []) + [("evacuate", u, b) for b in turned_parts(u)]
 
         def earlier(i, order, steps):
             return [order[order.index(i) - steps]] if order.index(i) >= steps else []
@@ -564,7 +583,7 @@ def tile_multiqueryattention_pa_kernel(tc, x, cos, sin, Wq_bytes, Wq_scale, Wk, 
             if kind == "x_copy":
                 return [("transpose", job[1])]
             if kind == "x_quantise":
-                return [("x_copy", 2 * job[1]), ("x_copy", 2 * job[1] + 1)]
+                return [("x_copy", m) for m in range(TOKEN_TILES)]
             if kind == "table_transpose":
                 return buffers_free(job, 1) + [("negate_sin",)]
             if kind == "table_copy":
@@ -575,14 +594,14 @@ def tile_multiqueryattention_pa_kernel(tc, x, cos, sin, Wq_bytes, Wq_scale, Wk, 
                 for v in back(u, WIDE_BUFS[stream_of(u)]):
                     out = out + planes_read(v)
                 return out
-            if kind == "interleave" or (kind == "evacuate" and job[2] == 0):
+            if kind == "interleave" or (kind == "evacuate" and job[2] == 0 and INTERLEAVE[job[1]] == "P"):
                 u = job[1]
                 out = planes_ready(u) if kind == "interleave" else [("pe_interleave", u, 0)]
                 for v in back(u, 1):
                     out = out + interleaved_made(v)[0:1]
                 return out + [("quantise", v) for v in back(u, INTERLEAVED_BUFS[stream_of(u)])]
             if kind == "evacuate":
-                return [("pe_interleave", job[1], job[2]), ("evacuate", job[1], 0)]
+                return [("pe_interleave", job[1], job[2]), ("interleave", job[1]) if INTERLEAVE[job[1]] == "H" else ("evacuate", job[1], 0)]
             if kind == "pe_interleave":
                 return planes_ready(job[1]) + buffers_free(job, 1)
             if kind == "quantise":
@@ -596,13 +615,12 @@ def tile_multiqueryattention_pa_kernel(tc, x, cos, sin, Wq_bytes, Wq_scale, Wk, 
             if kind == "fill":
                 i = job[1]
                 out = buffers_free(job, 1)
+                out = out + [("x_quantise",)]
                 if BANKS[i][0] == "kv":
-                    return out + [("kv_quantise",), ("x_quantise", BANKS[i][1])]
-                if BANKS[i][0] == "t":
-                    out = out + [("x_quantise", 0), ("x_quantise", 1)]
+                    return out + [("kv_quantise",)]
+                if BANKS[i][0] in "ts":
                     half = BANKS[i][1] // HEADS_PER_UNIT
                 else:
-                    out = out + [("x_quantise", BANKS[i][2] // 2)]
                     half = BANKS[i][1] // (UNIT_COLS // BANK_COLS)
                 return out + [("quantise", half * PASSES + g) for g in range(PASSES)]
             if kind == "rope":
@@ -622,16 +640,16 @@ def tile_multiqueryattention_pa_kernel(tc, x, cos, sin, Wq_bytes, Wq_scale, Wk, 
             if kind == "sum_squares":
                 return [("turn_back" if turned(job[1]) else "add", job[1])]
             if kind == "take_inverse_rms":
-                return [("sum_squares", job[1])]
+                return [("sum_squares", 2 * job[1]), ("sum_squares", 2 * job[1] + 1)]
             if kind == "scalar_scales":
                 i = job[1]
                 if not scalar_heads(i) and not turned(i):
                     return []
-                return [("take_inverse_rms", i)] + ([("store", k) for k in earlier(i, results_in_order, RESULT_BUFS)] if turned(i) else [])
+                return [("take_inverse_rms", i // 2)] + ([("store", k) for k in earlier(i, results_in_order, RESULT_BUFS)] if turned(i) else [])
             if kind == "gpsimd_scales":
-                return [("take_inverse_rms", job[1])]
+                return [("take_inverse_rms", job[1] // 2)]
             if kind == "vector_scales":
-                return [("scalar_scales", job[1])] if turned(job[1]) else [("take_inverse_rms", job[1])] if vector_heads(job[1]) else []
+                return [("scalar_scales", job[1])] if turned(job[1]) else [("take_inverse_rms", job[1] // 2)] if vector_heads(job[1]) else []
             if kind == "store_v":
                 return [("rope", job[1])]
             if kind == "store":

@@ -39,7 +39,7 @@ BANKS = (("q", 1, 0), ("t", 0), ("q", 1, 1), ("t", 1), ("q", 1, 2), ("t", 2), ("
 N_BANKS = len(BANKS)
 LATE_FIRST = 8
 GPSIMD_SCALES = ()
-VECTOR_SCALES = {8: 1, 9: 1, 10: 1, 11: 1, 12: 3, 13: 3, 14: 3, 15: 4}
+VECTOR_SCALES = {15: 4}
 VECTOR_LAG = 4
 FILL_AHEAD = 3
 GPSIMD_LAG = 3

@@ -35,13 +35,13 @@ STREAMS = ((0, 2, 4, 5, 6), (1, 3, 7))
 WIDE_BUFS = (2, 2)
 INTERLEAVED_BUFS = (2, 2)
 LOAD_ORDER = (("p", 0, 0), ("p", 1, 0), ("p", 0, 2), ("p", 1, 1), ("p", 0, 1), ("p", 1, 2), ("p", 0, 3), ("p", 1, 3), ("u", 2), ("u", 3), ("u", 4), ("x", 0), ("x", 1), ("c",), ("x", 2), ("x", 3), ("u", 7), ("k",), ("v",), ("u", 5), ("u", 6))
-BANKS = (("q", 1, 0), ("t", 0), ("q", 1, 1), ("t", 1), ("q", 1, 2), ("t", 2), ("q", 1, 3), ("t", 3), ("q", 2, 0), ("q", 2, 1), ("q", 2, 2), ("q", 2, 3), ("s", 12), ("s", 13), ("s", 14), ("t", 15), ("kv", 0), ("kv", 1),)
+BANKS = (("q", 1, 0), ("t", 0), ("q", 1, 1), ("t", 1), ("q", 1, 2), ("t", 2), ("q", 1, 3), ("t", 3), ("t", 15), ("q", 2, 0), ("q", 2, 1), ("q", 2, 2), ("q", 2, 3), ("s", 12), ("s", 13), ("s", 14), ("kv", 0), ("kv", 1),)
 N_BANKS = len(BANKS)
-LATE_FIRST = 8
+LATE_FIRST = N_BANKS
 GPSIMD_SCALES = ()
-VECTOR_SCALES = {15: 4}
+VECTOR_SCALES = {13: 2, 14: 2, 15: 2, 16: 1, 17: 1}
 VECTOR_LAG = 4
-FILL_AHEAD = 3
+FILL_AHEAD = 2
 GPSIMD_LAG = 3
 ROTATED_BUFS = 8
 RESULT_BUFS = 3
@@ -55,11 +55,11 @@ SHORT = {
 SCALAR_FIRST = "s1 s3 e1 x0 x1 e3 x2 x3 t s7 k0 k1 k2 k3 i7 e7 i5"
 VECTOR_FIRST = "v0 v2 i0 v4 q0 i2 n q2 q1 i4 v5 q3 X q4 v6"
 TENSOR_FIRST = "p1 T0 T1 p3 T2 T3 b K0 K1 K2 K3 p7"
-VECTOR_LATE = {7: "q5 q6 q7 Q"}
+VECTOR_LATE = {1: "q5", 3: "q6", 5: "q7", 7: "Q"}
 TENSOR_MIDDLE = ""
 TENSOR_LATE = {}
-SCALAR_BEFORE = {}
-SCALAR_LATE = {0: 'i6'}
+SCALAR_BEFORE = {0: 'i6'}
+SCALAR_LATE = {}
 QUEUE_NAMES = ("scalar", "vector", "tensor", "gpsimd", "sync")
 
 
@@ -89,7 +89,7 @@ def turned(i):
 
 
 def heads_of(i):
-    return 2 if BANKS[i][0] == "kv" else 4
+    return {"kv": 2, "v": 0}.get(BANKS[i][0], 4)
 
 
 def vector_heads(i):
@@ -106,7 +106,8 @@ def make_queues():
     for i in range(N_BANKS + 2):
         if i < N_BANKS:
             scalar.extend(jobs(SCALAR_BEFORE.get(i, "")))
-            scalar.append(("sum_squares", i))
+            if heads_of(i):
+                scalar.append(("sum_squares", i))
         if i >= 2:
             scalar.append(("scalar_scales", i - 2))
             scalar.extend(jobs(SCALAR_LATE.get(i - 2, "")))
@@ -130,13 +131,14 @@ def make_queues():
         if banks.start == 0:
             tensor.extend(jobs(TENSOR_MIDDLE))
     for i in range(N_BANKS + GPSIMD_LAG):
-        if i < N_BANKS and not turned(i):
+        if i < N_BANKS and not turned(i) and BANKS[i][0] != "v":
             gpsimd.append(("add", i))
         if i - GPSIMD_LAG in GPSIMD_SCALES:
             gpsimd.append(("gpsimd_scales", i - GPSIMD_LAG))
     for i in range(N_BANKS):
-        sync.append(("store", i))
-        sync.extend([("store_v", k) for k in range(i + 1, N_BANKS) if BANKS[k][0] == "kv" and k - 3 == i])
+        if heads_of(i):
+            sync.append(("store", i))
+        sync.extend([("store_v", k) for k in range(i + 1, N_BANKS) if BANKS[k][0] in ("kv", "v") and (k - 3 == i or i == 0 and k < 3)])
     return {"scalar": scalar, "vector": vector, "tensor": tensor, "gpsimd": gpsimd, "sync": sync}
 
 
@@ -391,11 +393,19 @@ def tile_multiqueryattention_pa_kernel(tc, x, cos, sin, Wq_bytes, Wq_scale, Wk, 
         def wq_operand(half, first, count):
             return (lambda g: wq_codes[half][:, g, first:first + count], lambda g: wq_scales[half][:, g, first:first + count])
 
+        def kv_operand(first, count):
+            return (lambda g: kv_codes[:, g, first:first + count], lambda g: kv_scales[:, g, first:first + count])
+
         def fill(i):
             bank_t[i] = psum.tile([P, BANK_COLS], F32, name="bank", tag="bank", bufs=BANK_BUFS["bank"])
-            if BANKS[i][0] == "t":
+            if BANKS[i] == ("t", HEADS):
+                passes_mx(bank_t[i][:], kv_operand(0, D), x_operand(0, TOKENS))
+            elif BANKS[i][0] == "t":
                 half, h = divmod(BANKS[i][1], HEADS_PER_UNIT)
                 passes_mx(bank_t[i][:], wq_operand(half, h * D, D), x_operand(0, TOKENS))
+            elif BANKS[i][0] == "v":
+                for m in range(TOKEN_TILES):
+                    passes_mx(bank_t[i][:, m * D:(m + 1) * D], x_operand(m * P, P), kv_operand(D, D))
             elif BANKS[i][0] == "s":
                 half, h = divmod(BANKS[i][1], HEADS_PER_UNIT)
                 for m in range(TOKEN_TILES):
@@ -405,9 +415,8 @@ def tile_multiqueryattention_pa_kernel(tc, x, cos, sin, Wq_bytes, Wq_scale, Wk, 
                 half, part = divmod(block, UNIT_COLS // BANK_COLS)
                 passes_mx(bank_t[i][:], x_operand(m * P, P), wq_operand(half, part * BANK_COLS, BANK_COLS))
             else:
-                kv = (lambda g: kv_codes[:, g, :], lambda g: kv_scales[:, g, :])
                 for r in range(2):
-                    passes_mx(bank_t[i][:, r * 2 * D:(r + 1) * 2 * D], x_operand((2 * BANKS[i][1] + r) * P, P), kv)
+                    passes_mx(bank_t[i][:, r * 2 * D:(r + 1) * 2 * D], x_operand((2 * BANKS[i][1] + r) * P, P), kv_operand(0, 2 * D))
 
         rotated = {}
         products = {}
@@ -417,6 +426,10 @@ def tile_multiqueryattention_pa_kernel(tc, x, cos, sin, Wq_bytes, Wq_scale, Wk, 
 
         def rope(i):
             heads = heads_of(i)
+            if BANKS[i][0] == "v":
+                v_tiles[i] = v_pool.tile([P, TOKEN_TILES, D], F32, name="v_t", tag="v_t")
+                nc.vector.tensor_copy(out=v_tiles[i][:], in_=bank_t[i][:].rearrange("p (m d) -> p m d", d=D))
+                return
             if BANKS[i][0] == "t":
                 products[i] = products_pool.tile([P, 2, TOKENS], F32, name="products", tag="products", bufs=PRODUCTS_BUFS)
                 nc.vector.tensor_tensor(out=products[i][:], in0=bank_t[i][:].unsqueeze(1).to_broadcast([P, 2, TOKENS]), in1=table[:], op=ALU.mult)
@@ -469,16 +482,17 @@ def tile_multiqueryattention_pa_kernel(tc, x, cos, sin, Wq_bytes, Wq_scale, Wk, 
             return turned_bank[i][:, h, :] if turned(i) else rotated[i][:, h * D:(h + 1) * D]
 
         def sum_squares(i):
-            if i % 2 == 0:
+            if i // 2 not in square_sums:
                 square_sums[i // 2] = stats_pool.tile([P, 2, 4], F32, name="square_sums", tag="square_sums")
             for h in range(heads_of(i)):
                 unread = scratch_pool.tile([P, D], BF16, name="unread", tag="unread")
                 nc.scalar.activation(out=unread[:], in_=piece(i, h), func=ACT.Square, accum_out=square_sums[i // 2][:, i % 2, h:h + 1])
 
         def take_inverse_rms(pair):
-            heads = heads_of(2 * pair)
             both = stats_pool.tile([P, 2, 4], F32, name="inverse_rms", tag="inverse_rms")
-            nc.scalar.activation(out=both[:, :, 0:heads], in_=square_sums[pair][:, :, 0:heads], func=ACT.Abs_reciprocal_sqrt, scale=1.0 / D, bias=EPS)
+            rows = slice(0 if heads_of(2 * pair) else 1, 2 if heads_of(2 * pair + 1) else 1)
+            heads = heads_of(2 * pair) or heads_of(2 * pair + 1)
+            nc.scalar.activation(out=both[:, rows, 0:heads], in_=square_sums[pair][:, rows, 0:heads], func=ACT.Abs_reciprocal_sqrt, scale=1.0 / D, bias=EPS)
             for r in range(2):
                 inverse_rms[2 * pair + r] = both[:, r, :]
 
@@ -516,7 +530,9 @@ def tile_multiqueryattention_pa_kernel(tc, x, cos, sin, Wq_bytes, Wq_scale, Wk, 
             nc.gpsimd.tensor_tensor(out=view, in0=view, in1=inverse_rms[i][:, 0:heads].unsqueeze(2).to_broadcast([P, heads, D]), op=ALU.mult)
 
         def store(i):
-            if BANKS[i][0] == "t":
+            if BANKS[i] == ("t", HEADS):
+                nc.sync.dma_start(out=k_out, in_=result[i][:])
+            elif BANKS[i][0] == "t":
                 nc.sync.dma_start(out=q_head_out[BANKS[i][1]], in_=result[i][:])
             elif BANKS[i][0] == "s":
                 nc.sync.dma_start(out=q_head_out[BANKS[i][1]], in_=rotated[i][:].rearrange("p (m d) -> p m d", d=D))
@@ -528,8 +544,8 @@ def tile_multiqueryattention_pa_kernel(tc, x, cos, sin, Wq_bytes, Wq_scale, Wk, 
                 nc.sync.dma_start(out=k_out[:, 2 * pair:2 * pair + 2, :], in_=rotated[i][:, 0:2 * D].rearrange("p (h d) -> p h d", d=D))
 
         def store_v(i):
-            pair = BANKS[i][1]
-            nc.sync.dma_start(out=v_out[:, 2 * pair:2 * pair + 2, :], in_=v_tiles[i][:])
+            rows = slice(0, TOKEN_TILES) if BANKS[i][0] == "v" else slice(2 * BANKS[i][1], 2 * BANKS[i][1] + 2)
+            nc.sync.dma_start(out=v_out[:, rows, :], in_=v_tiles[i][:])
 
         actions = {
             "transpose": transpose, "x_copy": x_copy, "x_quantise": x_quantise, "widen": widen, "interleave": interleave,
@@ -558,7 +574,7 @@ def tile_multiqueryattention_pa_kernel(tc, x, cos, sin, Wq_bytes, Wq_scale, Wk, 
             else:
                 readers[tag].append(("rope", job[1]))
         results_in_order = [i for i in range(N_BANKS) if turned(i)]
-        rotated_in_order = [i for i in range(N_BANKS) if not turned(i)]
+        rotated_in_order = [i for i in range(N_BANKS) if not turned(i) and BANKS[i][0] != "v"]
 
         def buffers_free(job, tiles):
             tag, first = first_tile[job]
@@ -574,7 +590,7 @@ def tile_multiqueryattention_pa_kernel(tc, x, cos, sin, Wq_bytes, Wq_scale, Wk, 
             return ([("interleave", u)] if INTERLEAVE[u] != "P" else []) + [("evacuate", u, b) for b in turned_parts(u)]
 
         def earlier(i, order, steps):
-            return [order[order.index(i) - steps]] if order.index(i) >= steps else []
+            return [order[order.index(i) - steps]] if i in order and order.index(i) >= steps else []
 
         def needs(job):
             kind = job[0]
@@ -616,7 +632,7 @@ def tile_multiqueryattention_pa_kernel(tc, x, cos, sin, Wq_bytes, Wq_scale, Wk, 
                 i = job[1]
                 out = buffers_free(job, 1)
                 out = out + [("x_quantise",)]
-                if BANKS[i][0] == "kv":
+                if BANKS[i][0] in ("kv", "v") or BANKS[i] == ("t", HEADS):
                     return out + [("kv_quantise",)]
                 if BANKS[i][0] in "ts":
                     half = BANKS[i][1] // HEADS_PER_UNIT
@@ -628,8 +644,8 @@ def tile_multiqueryattention_pa_kernel(tc, x, cos, sin, Wq_bytes, Wq_scale, Wk, 
                 out = [("fill", i), ("negate_sin",)] + ([("rope", i - 1)] if i else [])
                 if turned(i):
                     out.append(("table_copy",))
-                if i >= PRODUCTS_BUFS:
-                    out.append(("turn_back" if turned(i - PRODUCTS_BUFS) else "add", i - PRODUCTS_BUFS))
+                with_products = [k for k in range(N_BANKS) if BANKS[k][0] != "v"]
+                out.extend([("turn_back" if turned(k) else "add", k) for k in earlier(i, with_products, PRODUCTS_BUFS)])
                 return out
             if kind == "add":
                 i = job[1]
@@ -640,7 +656,7 @@ def tile_multiqueryattention_pa_kernel(tc, x, cos, sin, Wq_bytes, Wq_scale, Wk, 
             if kind == "sum_squares":
                 return [("turn_back" if turned(job[1]) else "add", job[1])]
             if kind == "take_inverse_rms":
-                return [("sum_squares", 2 * job[1]), ("sum_squares", 2 * job[1] + 1)]
+                return [("sum_squares", k) for k in (2 * job[1], 2 * job[1] + 1) if heads_of(k)]
             if kind == "scalar_scales":
                 i = job[1]
                 if not scalar_heads(i) and not turned(i):

@@ -30,11 +30,11 @@ IL_PARTS = UNIT_COLS // IL_COLS
 FLOPS = 2 * TOKENS * DIM * (HEADS * D + 2 * D)
 
 WIDEN = ("DDDD", "AAAA", "DDDD", "AAAA", "DDDD", "DDDD", "DDDD", "AAAA")
-INTERLEAVE = "XPXPXYYH"
+INTERLEAVE = "XPXPXYYS"
 STREAMS = ((0, 2, 4, 5, 6), (1, 3, 7))
 WIDE_BUFS = (2, 2)
 INTERLEAVED_BUFS = (2, 2)
-LOAD_ORDER = (("p", 0, 0), ("p", 1, 0), ("p", 0, 2), ("p", 1, 1), ("p", 0, 1), ("p", 1, 2), ("p", 0, 3), ("p", 1, 3), ("u", 2), ("u", 3), ("u", 4), ("x", 0), ("x", 1), ("c",), ("x", 2), ("x", 3), ("u", 7), ("k",), ("v",), ("u", 5), ("u", 6))
+LOAD_ORDER = (("p", 0, 0), ("p", 1, 0), ("p", 0, 2), ("p", 1, 1), ("p", 0, 1), ("p", 1, 2), ("p", 0, 3), ("p", 1, 3), ("u", 2), ("u", 3), ("u", 4), ("u", 7), ("x", 0), ("x", 1), ("c",), ("x", 2), ("x", 3), ("u", 5), ("k",), ("v",), ("u", 6))
 BANKS = (("q", 1, 0), ("t", 0), ("q", 1, 1), ("t", 1), ("q", 1, 2), ("t", 2), ("q", 1, 3), ("t", 3), ("t", 15), ("q", 2, 0), ("q", 2, 1), ("q", 2, 2), ("q", 2, 3), ("s", 12), ("s", 13), ("s", 14), ("kv", 0), ("kv", 1),)
 N_BANKS = len(BANKS)
 LATE_FIRST = N_BANKS
@@ -47,14 +47,15 @@ ROTATED_BUFS = 8
 RESULT_BUFS = 3
 PRODUCTS_BUFS = 4
 SCRATCH_BUFS = 8
+KV = "P"
 BANK_BUFS = {"bank": 4, "side": 4}
 SHORT = {
     "i": "interleave", "q": "quantise", "x": "x_copy", "X": "x_quantise", "T": "transpose", "t": "table_copy", "k": "kv_evacuate",
     "K": "kv_pe_interleave", "n": "negate_sin", "Q": "kv_quantise", "t": "table_copy", "b": "table_transpose",
 }
-SCALAR_FIRST = "s1 s3 e1 x0 x1 e3 x2 x3 t s7 k0 k1 k2 k3 i7 e7 i5"
-VECTOR_FIRST = "v0 v2 i0 v4 q0 i2 n q2 q1 i4 v5 q3 X q4 v6"
-TENSOR_FIRST = "p1 T0 T1 p3 T2 T3 b K0 K1 K2 K3 p7"
+SCALAR_FIRST = "s1 s3 s7a e1 x0 x1 s7b e3 x2 x3 t i7 i5 k0 k1 k2 k3"
+VECTOR_FIRST = "v0 i0 v2 q0 i2 v4 n q2 i4 v5 q1 q4 q3 X v6"
+TENSOR_FIRST = "p1 T0 T1 p3 T2 T3 b K0 K1 K2 K3"
 VECTOR_LATE = {1: "q5", 3: "q6", 5: "q7", 7: "Q"}
 TENSOR_MIDDLE = ""
 TENSOR_LATE = {}
@@ -68,9 +69,10 @@ def jobs(text):
     for name in text.split():
         letter, rest = name[0], name[1:]
         if letter in "sv":
-            u = int(rest)
-            order = (0, 2, 1, 3) if "D" in WIDEN[u] else range(PACK)
-            out.extend([("widen", u, t) for t in order if (WIDEN[u][t] == "A") == (letter == "s")])
+            u = int(rest[0])
+            order = [t for t in ((0, 2, 1, 3) if "D" in WIDEN[u] else range(PACK)) if (WIDEN[u][t] == "A") == (letter == "s")]
+            half = len(order) // 2
+            out.extend([("widen", u, t) for t in {"a": order[:half], "b": order[half:]}.get(rest[1:], order)])
         elif letter in "ep":
             out.extend([("evacuate" if letter == "e" else "pe_interleave", int(rest), b) for b in turned_parts(int(rest))])
         elif rest:
@@ -346,6 +348,13 @@ def tile_multiqueryattention_pa_kernel(tc, x, cos, sin, Wq_bytes, Wq_scale, Wk, 
                 )
 
         def kv_evacuate(g):
+            if KV == "S":
+                for which, planes in ((0, wk_t), (1, wv_t)):
+                    nc.scalar.copy(
+                        out=kv_interleaved[:, g, which * D:(which + 1) * D, :].rearrange("p (c i) t -> p c t i", i=4),
+                        in_=planes[:, g, :, :].rearrange("p t (c i) -> p c t i", i=4),
+                    )
+                return
             nc.scalar.copy(out=kv_interleaved[:, g, :, :].rearrange("p n t -> p (n t)").bitcast(F32), in_=kv_bank[g][:].bitcast(F32))
 
         def kv_quantise():
@@ -627,7 +636,7 @@ def tile_multiqueryattention_pa_kernel(tc, x, cos, sin, Wq_bytes, Wq_scale, Wk, 
             if kind == "kv_pe_interleave":
                 return buffers_free(job, 1)
             if kind == "kv_evacuate":
-                return [("kv_pe_interleave", job[1])]
+                return [("kv_pe_interleave", job[1])] if KV == "P" else []
             if kind == "fill":
                 i = job[1]
                 out = buffers_free(job, 1)

@@ -35,11 +35,11 @@ STREAMS = ((0, 2, 4, 5, 6), (1, 3, 7))
 WIDE_BUFS = (2, 2)
 INTERLEAVED_BUFS = (2, 2)
 LOAD_ORDER = (("p", 0, 0), ("p", 1, 0), ("p", 0, 2), ("p", 1, 1), ("p", 0, 1), ("p", 1, 2), ("p", 0, 3), ("p", 1, 3), ("u", 2), ("u", 3), ("u", 4), ("u", 7), ("x", 0), ("x", 1), ("c",), ("x", 2), ("x", 3), ("u", 5), ("k",), ("v",), ("u", 6))
-BANKS = (("q", 1, 0), ("t", 0), ("q", 1, 1), ("t", 1), ("q", 1, 2), ("t", 2), ("q", 1, 3), ("t", 3), ("t", 15), ("q", 2, 0), ("q", 2, 1), ("q", 2, 2), ("q", 2, 3), ("s", 12), ("s", 13), ("s", 14), ("kv", 0), ("kv", 1),)
+BANKS = (("q", 1, 0), ("q", 1, 1), ("t", 0), ("t", 1), ("q", 1, 2), ("q", 1, 3), ("t", 2), ("t", 3), ("q", 2, 0), ("q", 2, 1), ("q", 2, 2), ("q", 2, 3), ("q", 3, 0), ("q", 3, 1), ("q", 3, 2), ("q", 3, 3), ("kv", 0), ("kv", 1),)
 N_BANKS = len(BANKS)
 LATE_FIRST = N_BANKS
 GPSIMD_SCALES = ()
-VECTOR_SCALES = {13: 2, 14: 2, 15: 2, 16: 1, 17: 1}
+VECTOR_SCALES = {12: 1, 13: 2, 14: 2, 15: 3, 16: 1, 17: 1}
 VECTOR_LAG = 4
 FILL_AHEAD = 2
 GPSIMD_LAG = 3
@@ -53,13 +53,13 @@ SHORT = {
     "i": "interleave", "q": "quantise", "x": "x_copy", "X": "x_quantise", "T": "transpose", "t": "table_copy", "k": "kv_evacuate",
     "K": "kv_pe_interleave", "n": "negate_sin", "Q": "kv_quantise", "t": "table_copy", "b": "table_transpose",
 }
-SCALAR_FIRST = "s1 s3 s7a e1 x0 x1 s7b e3 x2 x3 t i7 i5 k0 k1 k2 k3"
+SCALAR_FIRST = "s1 s3 s7a e1 x0 x1 s7b e3 x2 x3 t i7 i5 k0 k1"
 VECTOR_FIRST = "v0 i0 v2 q0 i2 v4 n q2 i4 v5 q1 q4 q3 X v6"
 TENSOR_FIRST = "p1 T0 T1 p3 T2 T3 b K0 K1 K2 K3"
-VECTOR_LATE = {1: "q5", 3: "q6", 5: "q7", 7: "Q"}
+VECTOR_LATE = {3: "q5 q6 q7", 7: "Q"}
 TENSOR_MIDDLE = ""
 TENSOR_LATE = {}
-SCALAR_BEFORE = {0: 'i6'}
+SCALAR_BEFORE = {0: 'i6', 4: 'k2 k3'}
 SCALAR_LATE = {}
 QUEUE_NAMES = ("scalar", "vector", "tensor", "gpsimd", "sync")
 

@@ -39,7 +39,7 @@ BANKS = (("q", 1, 0), ("q", 1, 1), ("t", 0), ("t", 1), ("q", 1, 2), ("q", 1, 3),
 N_BANKS = len(BANKS)
 LATE_FIRST = N_BANKS
 GPSIMD_SCALES = ()
-VECTOR_SCALES = {12: 1, 13: 2, 14: 2, 15: 3, 16: 1, 17: 1}
+VECTOR_SCALES = {8: 1, 9: 1, 10: 1, 11: 1, 12: 2, 13: 2, 14: 2, 15: 3, 16: 1, 17: 1}
 VECTOR_LAG = 4
 FILL_AHEAD = 2
 GPSIMD_LAG = 3
@@ -59,6 +59,8 @@ TENSOR_FIRST = "p1 T0 T1 p3 T2 T3 b K0 K1 K2 K3"
 VECTOR_LATE = {3: "q5 q6 q7", 7: "Q"}
 TENSOR_MIDDLE = ""
 TENSOR_LATE = {}
+SCALAR_DRAINS = (4,)
+DRAINED = [i - k for i in SCALAR_DRAINS for k in (1, 2)]
 SCALAR_BEFORE = {0: 'i6', 4: 'k2 k3'}
 SCALAR_LATE = {}
 QUEUE_NAMES = ("scalar", "vector", "tensor", "gpsimd", "sync")
@@ -110,11 +112,13 @@ def make_queues():
             scalar.extend(jobs(SCALAR_BEFORE.get(i, "")))
             if heads_of(i):
                 scalar.append(("sum_squares", i))
-        if i >= 2:
+        if i >= 2 and i - 2 not in DRAINED:
             scalar.append(("scalar_scales", i - 2))
             scalar.extend(jobs(SCALAR_LATE.get(i - 2, "")))
         if i % 2 and i < N_BANKS:
             scalar.append(("take_inverse_rms", i // 2))
+        if i + 1 in SCALAR_DRAINS:
+            scalar.extend([("scalar_scales", i - 1), ("scalar_scales", i)])
     vector += jobs(VECTOR_FIRST)
     for i in range(N_BANKS + VECTOR_LAG):
         if i < N_BANKS:

from contextlib import ExitStack

import concourse.mybir as mybir
from concourse.masks import make_identity

F32 = mybir.dt.float32
BF16 = mybir.dt.bfloat16
U32 = mybir.dt.uint32
U8 = mybir.dt.uint8
FP8 = mybir.dt.float8_e4m3fn
FP8X4 = mybir.dt.float8_e4m3fn_x4
ACT = mybir.ActivationFunctionType
ALU = mybir.AluOpType

TOKENS, DIM, HEADS, D = 512, 2048, 16, 128
HALF = D // 2
EPS = 1e-6
P = 128
PACK = 4
PASSES = DIM // (P * PACK)
TOKEN_TILES = TOKENS // P
BANK_COLS = 512
UNIT_COLS = 1024
UNITS = PASSES * (HEADS * D // UNIT_COLS)
HEADS_PER_UNIT = UNIT_COLS // D
HEADS_PER_BANK = BANK_COLS // D
IL_COLS = 256
IL_PARTS = UNIT_COLS // IL_COLS

FLOPS = 2 * TOKENS * DIM * (HEADS * D + 2 * D)

WIDEN = ("DDDD", "AAAA", "DDDD", "AAAA", "DDDD", "DDDD", "DDDD", "AAAA")
INTERLEAVE = "XPXPXYYS"
STREAMS = ((0, 2, 4, 5, 6), (1, 3, 7))
WIDE_BUFS = (2, 2)
INTERLEAVED_BUFS = (2, 2)
LOAD_ORDER = (("p", 0, 0), ("p", 1, 0), ("p", 0, 2), ("p", 1, 1), ("p", 0, 1), ("p", 1, 2), ("p", 0, 3), ("p", 1, 3), ("u", 2), ("u", 3), ("u", 4), ("u", 7), ("x", 0), ("x", 1), ("c",), ("x", 2), ("x", 3), ("u", 5), ("k",), ("v",), ("u", 6))
BANKS = (("q", 1, 0), ("q", 1, 1), ("t", 0), ("t", 1), ("q", 1, 2), ("q", 1, 3), ("t", 2), ("t", 3), ("q", 2, 0), ("q", 2, 1), ("q", 2, 2), ("q", 2, 3), ("q", 3, 0), ("q", 3, 1), ("q", 3, 2), ("q", 3, 3), ("kv", 0), ("kv", 1),)
N_BANKS = len(BANKS)
LATE_FIRST = N_BANKS
GPSIMD_SCALES = ()
VECTOR_SCALES = {8: 1, 9: 1, 10: 1, 11: 1, 12: 2, 13: 2, 14: 2, 15: 3, 16: 1, 17: 1}
VECTOR_LAG = 4
FILL_AHEAD = 2
GPSIMD_LAG = 3
ROTATED_BUFS = 8
RESULT_BUFS = 3
PRODUCTS_BUFS = 4
SCRATCH_BUFS = 8
KV = "P"
BANK_BUFS = {"bank": 4, "side": 4}
SHORT = {
    "i": "interleave", "q": "quantise", "x": "x_copy", "X": "x_quantise", "T": "transpose", "t": "table_copy", "k": "kv_evacuate",
    "K": "kv_pe_interleave", "n": "negate_sin", "Q": "kv_quantise", "t": "table_copy", "b": "table_transpose",
}
SCALAR_FIRST = "s1 s3 s7a e1 x0 x1 s7b e3 x2 x3 t i7 i5 k0 k1"
VECTOR_FIRST = "v0 i0 v2 q0 i2 v4 n q2 i4 v5 q1 q4 q3 X v6"
TENSOR_FIRST = "p1 T0 T1 p3 T2 T3 b K0 K1 K2 K3"
VECTOR_LATE = {3: "q5 q6 q7", 7: "Q"}
TENSOR_MIDDLE = ""
TENSOR_LATE = {}
SCALAR_DRAINS = (4,)
DRAINED = [i - k for i in SCALAR_DRAINS for k in (1, 2)]
SCALAR_BEFORE = {0: 'i6', 4: 'k2 k3'}
SCALAR_LATE = {}
QUEUE_NAMES = ("scalar", "vector", "tensor", "gpsimd", "sync")


def jobs(text):
    out = []
    for name in text.split():
        letter, rest = name[0], name[1:]
        if letter in "sv":
            u = int(rest[0])
            order = [t for t in ((0, 2, 1, 3) if "D" in WIDEN[u] else range(PACK)) if (WIDEN[u][t] == "A") == (letter == "s")]
            half = len(order) // 2
            out.extend([("widen", u, t) for t in {"a": order[:half], "b": order[half:]}.get(rest[1:], order)])
        elif letter in "ep":
            out.extend([("evacuate" if letter == "e" else "pe_interleave", int(rest), b) for b in turned_parts(int(rest))])
        elif rest:
            out.append((SHORT[letter], int(rest)))
        else:
            out.append((SHORT[letter],))
    return out


def turned_parts(u):
    return range(IL_PARTS) if INTERLEAVE[u] == "P" else range(IL_PARTS // 2) if INTERLEAVE[u] == "H" else ()


def turned(i):
    return BANKS[i][0] == "t"


def heads_of(i):
    return {"kv": 2, "v": 0}.get(BANKS[i][0], 4)


def vector_heads(i):
    return 0 if i in GPSIMD_SCALES else VECTOR_SCALES.get(i, 0)


def scalar_heads(i):
    return 0 if i in GPSIMD_SCALES else heads_of(i) - vector_heads(i)


def make_queues():
    scalar, vector, tensor, gpsimd, sync = [], [], [], [], []
    scalar += jobs(SCALAR_FIRST)
    for i in range(N_BANKS + 2):
        if i < N_BANKS:
            scalar.extend(jobs(SCALAR_BEFORE.get(i, "")))
            if heads_of(i):
                scalar.append(("sum_squares", i))
        if i >= 2 and i - 2 not in DRAINED:
            scalar.append(("scalar_scales", i - 2))
            scalar.extend(jobs(SCALAR_LATE.get(i - 2, "")))
        if i % 2 and i < N_BANKS:
            scalar.append(("take_inverse_rms", i // 2))
        if i + 1 in SCALAR_DRAINS:
            scalar.extend([("scalar_scales", i - 1), ("scalar_scales", i)])
    vector += jobs(VECTOR_FIRST)
    for i in range(N_BANKS + VECTOR_LAG):
        if i < N_BANKS:
            vector.append(("rope", i))
        vector.extend(jobs(VECTOR_LATE.get(i, "")))
        if i >= VECTOR_LAG:
            vector.append(("vector_scales", i - VECTOR_LAG))
    tensor += jobs(TENSOR_FIRST)
    for banks in (range(0, LATE_FIRST), range(LATE_FIRST, N_BANKS)):
        for i in range(banks.start, banks.stop + FILL_AHEAD):
            if i < banks.stop:
                tensor.append(("fill", i))
                tensor.extend(jobs(TENSOR_LATE.get(i, "")))
            if i - FILL_AHEAD >= banks.start and turned(i - FILL_AHEAD):
                tensor.append(("turn_back", i - FILL_AHEAD))
        if banks.start == 0:
            tensor.extend(jobs(TENSOR_MIDDLE))
    for i in range(N_BANKS + GPSIMD_LAG):
        if i < N_BANKS and not turned(i) and BANKS[i][0] != "v":
            gpsimd.append(("add", i))
        if i - GPSIMD_LAG in GPSIMD_SCALES:
            gpsimd.append(("gpsimd_scales", i - GPSIMD_LAG))
    for i in range(N_BANKS):
        if heads_of(i):
            sync.append(("store", i))
        sync.extend([("store_v", k) for k in range(i + 1, N_BANKS) if BANKS[k][0] in ("kv", "v") and (k - 3 == i or i == 0 and k < 3)])
    return {"scalar": scalar, "vector": vector, "tensor": tensor, "gpsimd": gpsimd, "sync": sync}


def tile_multiqueryattention_pa_kernel(tc, x, cos, sin, Wq_bytes, Wq_scale, Wk, Wv, out_0, out_1, out_2):
    nc = tc.nc

    with ExitStack() as ctx:
        keep = ctx.enter_context(tc.tile_pool(name="keep", bufs=1))
        wide_pool = ctx.enter_context(tc.tile_pool(name="wide", bufs=1))
        interleaved_pool = ctx.enter_context(tc.tile_pool(name="interleaved", bufs=1))
        rotated_pool = ctx.enter_context(tc.tile_pool(name="rotated", bufs=ROTATED_BUFS))
        result_pool = ctx.enter_context(tc.tile_pool(name="result", bufs=RESULT_BUFS))
        products_pool = ctx.enter_context(tc.tile_pool(name="products", bufs=1))
        stats_pool = ctx.enter_context(tc.tile_pool(name="stats", bufs=8))
        scratch_pool = ctx.enter_context(tc.tile_pool(name="scratch", bufs=SCRATCH_BUFS))
        v_pool = ctx.enter_context(tc.tile_pool(name="v", bufs=2))
        psum = ctx.enter_context(tc.psum_pool(name="psum", bufs=1))
        ctx.enter_context(tc.manual_schedule())

        x_rows = x[0].rearrange("(m p) k -> m p k", p=P)
        cos_rows = cos.rearrange("(m p) o j -> p m (o j)", p=P)
        sin_rows = sin.rearrange("(m p) o j -> p m (o j)", p=P)
        wq_planes = Wq_bytes.rearrange("(g p t) n -> g p t n", p=P, t=PACK)
        wq_plane_scales = Wq_scale.rearrange("(g p t) o -> p g (t o)", p=P, t=PACK)
        wk_planes = Wk.rearrange("(g p t) n -> p g (t n)", p=P, t=PACK)
        wv_planes = Wv.rearrange("(g p t) n -> p g (t n)", p=P, t=PACK)
        q_out = out_0[0].rearrange("(m p) h d -> m p (h d)", p=P)
        q_head_out = out_0[0].rearrange("(m p) h d -> h p m d", p=P)
        k_out = out_1[0].rearrange("(m p) d -> p m d", p=P)
        v_out = out_2[0].rearrange("(m p) d -> p m d", p=P)

        identity = keep.tile([P, P], F32, name="identity")
        swap = keep.tile([P, P], F32, name="swap")
        identity_bf = keep.tile([P, P], BF16, name="identity_bf")
        one = keep.tile([P, 1], F32, name="one")
        warm_up = keep.tile([P, 1], F32, name="warm_up")
        unread_sums = keep.tile([P, SCRATCH_BUFS], F32, name="unread_sums")
        plane_scales = keep.tile([P, PASSES, PACK], F32, name="plane_scales")
        factors = keep.tile([P, TOKEN_TILES, 5, HALF], BF16, name="factors")
        table = keep.tile([P, 2, TOKENS], BF16, name="table")
        wq_bytes_t = [keep.tile([P, PASSES, PACK, UNIT_COLS], U8, name="wq_bytes_t%d" % half) for half in range(UNITS // PASSES)]
        x_t = [products_pool.tile([P, DIM], BF16, name="x_t%d" % m, tag="products", bufs=PRODUCTS_BUFS) for m in range(TOKEN_TILES)]
        x_interleaved = keep.tile([P, PASSES, TOKENS, PACK], BF16, name="x_interleaved", align_bytes=64)
        x_codes = keep.tile([P, PASSES, TOKENS], U32, name="x_codes", align_bytes=64)
        x_scales = keep.tile([P, PASSES, TOKENS], U8, name="x_scales", align_bytes=64)
        wq_codes = [keep.tile([P, PASSES, UNIT_COLS], U32, name="wq_codes%d" % half, align_bytes=64) for half in range(UNITS // PASSES)]
        wq_scales = [keep.tile([P, PASSES, UNIT_COLS], U8, name="wq_scales%d" % half, align_bytes=64) for half in range(UNITS // PASSES)]
        wk_t = keep.tile([P, PASSES, PACK, D], BF16, name="wk_t")
        wv_t = keep.tile([P, PASSES, PACK, D], BF16, name="wv_t")
        kv_interleaved = keep.tile([P, PASSES, 2 * D, PACK], BF16, name="kv_interleaved", align_bytes=64)
        kv_codes = keep.tile([P, PASSES, 2 * D], U32, name="kv_codes", align_bytes=64)
        kv_scales = keep.tile([P, PASSES, 2 * D], U8, name="kv_scales", align_bytes=64)

        make_identity(nc, identity[:])
        make_identity(nc, identity_bf[:])
        nc.gpsimd.tensor_copy(out=swap[:, 0:HALF], in_=identity[:, HALF:D])
        nc.gpsimd.tensor_copy(out=swap[:, HALF:D], in_=identity[:, 0:HALF])
        nc.vector.memset(one[:], 1.0)
        nc.scalar.activation(out=warm_up[:], in_=one[:], func=ACT.Abs_reciprocal_sqrt)

        def load_plane(u, t):
            half, g = divmod(u, PASSES)
            nc.sync.dma_start(out=wq_bytes_t[half][:, g, t, :], in_=wq_planes[g][:, t, half * UNIT_COLS:(half + 1) * UNIT_COLS])

        def load_unit(u):
            half, g = divmod(u, PASSES)
            nc.sync.dma_start(out=wq_bytes_t[half][:, g, :, :], in_=wq_planes[g][:, :, half * UNIT_COLS:(half + 1) * UNIT_COLS])

        def load_x(m):
            nc.sync.dma_start(out=x_t[m][:], in_=x_rows[m])

        def load_wk():
            nc.sync.dma_start(out=wk_t[:].rearrange("p g t n -> p g (t n)"), in_=wk_planes)

        def load_wv():
            nc.sync.dma_start(out=wv_t[:].rearrange("p g t n -> p g (t n)"), in_=wv_planes)

        def load_cos_sin():
            for place in (0, 3, 4):
                nc.sync.dma_start(out=factors[:, :, place, :], in_=cos_rows)
            nc.sync.dma_start(out=factors[:, :, 2, :], in_=sin_rows)

        nc.sync.dma_start(out=plane_scales[:], in_=wq_plane_scales)
        loaders = {"p": load_plane, "u": load_unit, "x": load_x, "k": load_wk, "v": load_wv, "c": load_cos_sin}
        for item in LOAD_ORDER:
            loaders[item[0]](*item[1:])

        x_transposed = {}

        def transpose(m):
            words = x_t[m][:].bitcast(F32)
            for a in range(2):
                x_transposed[(m, a)] = psum.tile([P, 2, 2, P], F32, name="bank", tag="bank", bufs=BANK_BUFS["bank"])
                for gg in range(2):
                    g = 2 * a + gg
                    for s in range(2):
                        nc.tensor.transpose(
                            out=x_transposed[(m, a)][:, gg, s, :],
                            in_=words[:, 256 * g + s:256 * (g + 1):2],
                            identity=identity[:],
                        )

        def x_copy(m):
            for a in range(2):
                target = x_interleaved[:, 2 * a:2 * a + 2, m * P:(m + 1) * P, :].bitcast(F32)
                nc.scalar.copy(out=target, in_=x_transposed[(m, a)][:].rearrange("p g w r -> p g r w"))

        def x_quantise():
            for g in range(PASSES):
                nc.vector.quantize_mx(
                    out=x_codes[:, g, :].bitcast(FP8X4),
                    scales=x_scales[:, g, :],
                    in_=x_interleaved[:, g, :, :].rearrange("p r t -> p (r t)"),
                )

        wide = {}
        interleaved = {}
        il_bank = {}

        def stream_of(u):
            return [u in stream for stream in STREAMS].index(True)

        def back(u, steps):
            stream = STREAMS[stream_of(u)]
            return [stream[stream.index(u) - steps]] if stream.index(u) >= steps else []

        def widen(u, t):
            half, g = divmod(u, PASSES)
            if u not in wide:
                wide[u] = wide_pool.tile([P, PACK * UNIT_COLS], BF16, name="wide", tag="wide%d" % stream_of(u), bufs=WIDE_BUFS[stream_of(u)])
            codes = wq_bytes_t[half][:, g, t, :].bitcast(FP8)
            scale = plane_scales[:, g, t:t + 1]
            if WIDEN[u][t] == "D":
                pair, place = divmod(t, 2)
                out = wide[u][:, pair * 2 * UNIT_COLS + place:(pair + 1) * 2 * UNIT_COLS:2]
                nc.vector.tensor_scalar(out=out, in0=codes, scalar1=scale, scalar2=None, op0=ALU.mult)
            elif WIDEN[u][t] == "B":
                nc.vector.tensor_scalar(out=wide[u][:, t * UNIT_COLS:(t + 1) * UNIT_COLS], in0=codes, scalar1=scale, scalar2=None, op0=ALU.mult)
            else:
                nc.scalar.activation(out=wide[u][:, t * UNIT_COLS:(t + 1) * UNIT_COLS], in_=codes, func=ACT.Copy, scale=scale)

        def new_interleaved(u):
            interleaved[u] = interleaved_pool.tile(
                [P, UNIT_COLS * PACK], BF16, name="interleaved", tag="interleaved%d" % stream_of(u), bufs=INTERLEAVED_BUFS[stream_of(u)], align_bytes=64
            )

        def interleave(u):
            new_interleaved(u)
            if INTERLEAVE[u] == "H":
                first = UNIT_COLS // 2
                nc.scalar.copy(
                    out=interleaved[u][:, first * PACK:].rearrange("p (c i t) -> p c t i", i=4, t=PACK),
                    in_=wide[u][:].rearrange("p (t n) -> p t n", t=PACK)[:, :, first:].rearrange("p t (c i) -> p c t i", i=4),
                )
                return
            if INTERLEAVE[u] in "SV":
                target = interleaved[u][:].rearrange("p (c i t) -> p c t i", i=4, t=PACK)
                planes = wide[u][:].rearrange("p (t c i) -> p c t i", t=PACK, i=4)
                if INTERLEAVE[u] == "S":
                    nc.scalar.copy(out=target, in_=planes)
                else:
                    nc.vector.tensor_copy(out=target, in_=planes)
                return
            words = wide[u][:].bitcast(F32).rearrange("p (a n) -> p n a", a=2)
            target = interleaved[u][:].bitcast(F32).rearrange("p (n a) -> p n a", a=2)
            if INTERLEAVE[u] == "X":
                nc.vector.tensor_copy(out=target, in_=words)
            else:
                nc.scalar.copy(out=target, in_=words)

        def pe_interleave(u, b):
            il_bank[(u, b)] = psum.tile([P, IL_COLS * PACK], BF16, name="side", tag="side", bufs=BANK_BUFS["side"])
            planes = wide[u][:].rearrange("p (t n) -> p t n", t=PACK)
            for r in range(2):
                n0 = b * IL_COLS + r * (IL_COLS // 2)
                nc.tensor.matmul(
                    out=il_bank[(u, b)][:, r * BANK_COLS:(r + 1) * BANK_COLS].rearrange("p (n t) -> p t n", t=PACK),
                    lhsT=identity_bf[:],
                    rhs=planes[:, :, n0:n0 + IL_COLS // 2],
                    start=True,
                    stop=True,
                )

        def evacuate(u, b):
            if b == 0 and INTERLEAVE[u] == "P":
                new_interleaved(u)
            target = interleaved[u][:, b * IL_COLS * PACK:(b + 1) * IL_COLS * PACK]
            nc.scalar.copy(out=target.bitcast(F32), in_=il_bank[(u, b)][:].bitcast(F32))

        def quantise(u):
            half, g = divmod(u, PASSES)
            nc.vector.quantize_mx(out=wq_codes[half][:, g, :].bitcast(FP8X4), scales=wq_scales[half][:, g, :], in_=interleaved[u][:])

        kv_bank = {}

        def kv_pe_interleave(g):
            kv_bank[g] = psum.tile([P, 2 * D * PACK], BF16, name="side", tag="side", bufs=BANK_BUFS["side"])
            for which, planes in ((0, wk_t), (1, wv_t)):
                nc.tensor.matmul(
                    out=kv_bank[g][:, which * BANK_COLS:(which + 1) * BANK_COLS].rearrange("p (n t) -> p t n", t=PACK),
                    lhsT=identity_bf[:],
                    rhs=planes[:, g, :, :],
                    start=True,
                    stop=True,
                )

        def kv_evacuate(g):
            if KV == "S":
                for which, planes in ((0, wk_t), (1, wv_t)):
                    nc.scalar.copy(
                        out=kv_interleaved[:, g, which * D:(which + 1) * D, :].rearrange("p (c i) t -> p c t i", i=4),
                        in_=planes[:, g, :, :].rearrange("p t (c i) -> p c t i", i=4),
                    )
                return
            nc.scalar.copy(out=kv_interleaved[:, g, :, :].rearrange("p n t -> p (n t)").bitcast(F32), in_=kv_bank[g][:].bitcast(F32))

        def kv_quantise():
            nc.vector.quantize_mx(
                out=kv_codes[:].rearrange("p g n -> p (g n)").bitcast(FP8X4),
                scales=kv_scales[:].rearrange("p g n -> p (g n)"),
                in_=kv_interleaved[:].rearrange("p g n t -> p (g n t)"),
            )

        def negate_sin():
            nc.vector.tensor_scalar(out=factors[:, :, 1, :], in0=factors[:, :, 2, :], scalar1=-1.0, scalar2=None, op0=ALU.mult)

        table_bank = {}

        def table_transpose():
            table_bank[0] = psum.tile([P, 2, TOKENS], BF16, name="side", tag="side", bufs=BANK_BUFS["side"])
            for r, place in ((0, 3), (1, 1)):
                for m in range(TOKEN_TILES):
                    nc.tensor.transpose(
                        out=table_bank[0][:, r, m * P:(m + 1) * P],
                        in_=factors[:, m, place:place + 2, :].rearrange("p a j -> p (a j)"),
                        identity=identity_bf[:],
                    )

        def table_copy():
            nc.scalar.copy(out=table[:], in_=table_bank[0][:])

        bank_t = {}

        def passes_mx(out, stationary, moving):
            for g in range(PASSES):
                nc.tensor.matmul_mx(
                    out=out,
                    lhsT=stationary[0](g).bitcast(FP8X4),
                    lhsT_scale=stationary[1](g),
                    rhs=moving[0](g).bitcast(FP8X4),
                    rhs_scale=moving[1](g),
                    start=(g == 0),
                    stop=(g == PASSES - 1),
                )

        def x_operand(first, count):
            return (lambda g: x_codes[:, g, first:first + count], lambda g: x_scales[:, g, first:first + count])

        def wq_operand(half, first, count):
            return (lambda g: wq_codes[half][:, g, first:first + count], lambda g: wq_scales[half][:, g, first:first + count])

        def kv_operand(first, count):
            return (lambda g: kv_codes[:, g, first:first + count], lambda g: kv_scales[:, g, first:first + count])

        def fill(i):
            bank_t[i] = psum.tile([P, BANK_COLS], F32, name="bank", tag="bank", bufs=BANK_BUFS["bank"])
            if BANKS[i] == ("t", HEADS):
                passes_mx(bank_t[i][:], kv_operand(0, D), x_operand(0, TOKENS))
            elif BANKS[i][0] == "t":
                half, h = divmod(BANKS[i][1], HEADS_PER_UNIT)
                passes_mx(bank_t[i][:], wq_operand(half, h * D, D), x_operand(0, TOKENS))
            elif BANKS[i][0] == "v":
                for m in range(TOKEN_TILES):
                    passes_mx(bank_t[i][:, m * D:(m + 1) * D], x_operand(m * P, P), kv_operand(D, D))
            elif BANKS[i][0] == "s":
                half, h = divmod(BANKS[i][1], HEADS_PER_UNIT)
                for m in range(TOKEN_TILES):
                    passes_mx(bank_t[i][:, m * D:(m + 1) * D], x_operand(m * P, P), wq_operand(half, h * D, D))
            elif BANKS[i][0] == "q":
                block, m = BANKS[i][1:]
                half, part = divmod(block, UNIT_COLS // BANK_COLS)
                passes_mx(bank_t[i][:], x_operand(m * P, P), wq_operand(half, part * BANK_COLS, BANK_COLS))
            else:
                for r in range(2):
                    passes_mx(bank_t[i][:, r * 2 * D:(r + 1) * 2 * D], x_operand((2 * BANKS[i][1] + r) * P, P), kv_operand(0, 2 * D))

        rotated = {}
        products = {}
        v_tiles = {}
        turned_bank = {}
        result = {}

        def rope(i):
            heads = heads_of(i)
            if BANKS[i][0] == "v":
                v_tiles[i] = v_pool.tile([P, TOKEN_TILES, D], F32, name="v_t", tag="v_t")
                nc.vector.tensor_copy(out=v_tiles[i][:], in_=bank_t[i][:].rearrange("p (m d) -> p m d", d=D))
                return
            if BANKS[i][0] == "t":
                products[i] = products_pool.tile([P, 2, TOKENS], F32, name="products", tag="products", bufs=PRODUCTS_BUFS)
                nc.vector.tensor_tensor(out=products[i][:], in0=bank_t[i][:].unsqueeze(1).to_broadcast([P, 2, TOKENS]), in1=table[:], op=ALU.mult)
                return
            products[i] = products_pool.tile([P, HEADS_PER_BANK, 2, 2, HALF], F32, name="products", tag="products", bufs=PRODUCTS_BUFS)
            if BANKS[i][0] in "qs":
                halves = bank_t[i][:].rearrange("p (h w j) -> p h w j", w=2, j=HALF)
                if BANKS[i][0] == "q":
                    factor = factors[:, BANKS[i][2], 0:4, :].rearrange("p (w r) j -> p w r j", w=2).unsqueeze(1).to_broadcast([P, heads, 2, 2, HALF])
                else:
                    factor = factors[:, :, 0:4, :].rearrange("p m (w r) j -> p m w r j", w=2)
                nc.vector.tensor_tensor(out=products[i][:], in0=halves.unsqueeze(3).to_broadcast([P, heads, 2, 2, HALF]), in1=factor, op=ALU.mult)
                return
            pair = BANKS[i][1]
            for h in range(heads):
                halves = bank_t[i][:, h * 2 * D:h * 2 * D + D].rearrange("p (w j) -> p w j", j=HALF)
                factor = factors[:, 2 * pair + h, 0:4, :].rearrange("p (w r) j -> p w r j", w=2)
                nc.vector.tensor_tensor(out=products[i][:, h, :, :, :], in0=halves.unsqueeze(2).to_broadcast([P, 2, 2, HALF]), in1=factor, op=ALU.mult)
            v_t = v_pool.tile([P, 2, D], F32, name="v_t", tag="v_t")
            nc.vector.tensor_copy(out=v_t[:], in_=bank_t[i][:].rearrange("p (h e d) -> p h e d", e=2, d=D)[:, :, 1, :])
            v_tiles[i] = v_t

        def add(i):
            heads = heads_of(i)
            rotated[i] = rotated_pool.tile([P, BANK_COLS], F32, name="rotated", tag="rotated")
            nc.gpsimd.tensor_tensor(
                out=rotated[i][:, 0:heads * D].rearrange("p (h d) -> p h d", d=D),
                in0=products[i][:, 0:heads, 0, :, :].rearrange("p h r j -> p h (r j)"),
                in1=products[i][:, 0:heads, 1, :, :].rearrange("p h r j -> p h (r j)"),
                op=ALU.add,
            )

        def turn_back(i):
            turned_bank[i] = psum.tile([P, TOKEN_TILES, D], F32, name="side", tag="side", bufs=BANK_BUFS["side"])
            for m in range(TOKEN_TILES):
                for r, permutation in ((0, identity), (1, swap)):
                    nc.tensor.matmul(
                        out=turned_bank[i][:, m, :],
                        lhsT=products[i][:, r, m * P:(m + 1) * P],
                        rhs=permutation[:],
                        is_transpose=True,
                        start=(r == 0),
                        stop=(r == 1),
                    )

        square_sums = {}
        inverse_rms = {}

        def piece(i, h):
            return turned_bank[i][:, h, :] if turned(i) else rotated[i][:, h * D:(h + 1) * D]

        def sum_squares(i):
            if i // 2 not in square_sums:
                square_sums[i // 2] = stats_pool.tile([P, 2, 4], F32, name="square_sums", tag="square_sums")
            for h in range(heads_of(i)):
                unread = scratch_pool.tile([P, D], BF16, name="unread", tag="unread")
                nc.scalar.activation(out=unread[:], in_=piece(i, h), func=ACT.Square, accum_out=square_sums[i // 2][:, i % 2, h:h + 1])

        def take_inverse_rms(pair):
            both = stats_pool.tile([P, 2, 4], F32, name="inverse_rms", tag="inverse_rms")
            rows = slice(0 if heads_of(2 * pair) else 1, 2 if heads_of(2 * pair + 1) else 1)
            heads = heads_of(2 * pair) or heads_of(2 * pair + 1)
            nc.scalar.activation(out=both[:, rows, 0:heads], in_=square_sums[pair][:, rows, 0:heads], func=ACT.Abs_reciprocal_sqrt, scale=1.0 / D, bias=EPS)
            for r in range(2):
                inverse_rms[2 * pair + r] = both[:, r, :]

        def scalar_scales(i):
            if turned(i):
                result[i] = result_pool.tile([P, TOKEN_TILES, D], F32, name="result", tag="result")
            for h in range(scalar_heads(i)):
                out = result[i][:, h, :] if turned(i) else piece(i, h)
                nc.scalar.activation(out=out, in_=piece(i, h), func=ACT.Copy, scale=inverse_rms[i][:, h:h + 1])

        def vector_scales(i):
            first, heads = scalar_heads(i), vector_heads(i)
            if turned(i) and heads:
                nc.vector.tensor_tensor(
                    out=result[i][:, first:first + heads, :],
                    in0=turned_bank[i][:, first:first + heads, :],
                    in1=inverse_rms[i][:, first:first + heads].unsqueeze(2).to_broadcast([P, heads, D]),
                    op=ALU.mult,
                )
                return
            for h in range(first, first + heads):
                nc.vector.tensor_scalar(
                    out=piece(i, h),
                    in0=piece(i, h),
                    scalar1=inverse_rms[i][:, h:h + 1],
                    scalar2=None,
                    op0=ALU.mult,
                    op1=ALU.add,
                    accum_out=unread_sums[:, i % SCRATCH_BUFS:i % SCRATCH_BUFS + 1],
                )

        def gpsimd_scales(i):
            heads = heads_of(i)
            view = rotated[i][:, 0:heads * D].rearrange("p (h d) -> p h d", d=D)
            nc.gpsimd.tensor_tensor(out=view, in0=view, in1=inverse_rms[i][:, 0:heads].unsqueeze(2).to_broadcast([P, heads, D]), op=ALU.mult)

        def store(i):
            if BANKS[i] == ("t", HEADS):
                nc.sync.dma_start(out=k_out, in_=result[i][:])
            elif BANKS[i][0] == "t":
                nc.sync.dma_start(out=q_head_out[BANKS[i][1]], in_=result[i][:])
            elif BANKS[i][0] == "s":
                nc.sync.dma_start(out=q_head_out[BANKS[i][1]], in_=rotated[i][:].rearrange("p (m d) -> p m d", d=D))
            elif BANKS[i][0] == "q":
                block, m = BANKS[i][1:]
                nc.sync.dma_start(out=q_out[m][:, block * BANK_COLS:(block + 1) * BANK_COLS], in_=rotated[i][:])
            else:
                pair = BANKS[i][1]
                nc.sync.dma_start(out=k_out[:, 2 * pair:2 * pair + 2, :], in_=rotated[i][:, 0:2 * D].rearrange("p (h d) -> p h d", d=D))

        def store_v(i):
            rows = slice(0, TOKEN_TILES) if BANKS[i][0] == "v" else slice(2 * BANKS[i][1], 2 * BANKS[i][1] + 2)
            nc.sync.dma_start(out=v_out[:, rows, :], in_=v_tiles[i][:])

        actions = {
            "transpose": transpose, "x_copy": x_copy, "x_quantise": x_quantise, "widen": widen, "interleave": interleave,
            "pe_interleave": pe_interleave, "evacuate": evacuate, "quantise": quantise, "kv_pe_interleave": kv_pe_interleave, "kv_evacuate": kv_evacuate, "kv_quantise": kv_quantise,
            "negate_sin": negate_sin, "table_transpose": table_transpose, "table_copy": table_copy, "fill": fill, "rope": rope, "add": add,
            "turn_back": turn_back, "sum_squares": sum_squares, "take_inverse_rms": take_inverse_rms, "scalar_scales": scalar_scales,
            "gpsimd_scales": gpsimd_scales, "vector_scales": vector_scales, "store": store, "store_v": store_v,
        }

        queues = make_queues()
        readers = {"bank": [], "side": []}
        first_tile = {}
        for job in queues["tensor"]:
            tag = "bank" if job[0] in ("transpose", "fill") else "side"
            first_tile[job] = (tag, len(readers[tag]))
            if job[0] == "transpose":
                readers[tag].extend([("x_copy", job[1])] * 2)
            elif job[0] == "pe_interleave":
                readers[tag].append(("evacuate",) + job[1:])
            elif job[0] == "kv_pe_interleave":
                readers[tag].append(("kv_evacuate", job[1]))
            elif job[0] == "table_transpose":
                readers[tag].append(("table_copy",))
            elif job[0] == "turn_back":
                readers[tag].append(("vector_scales" if vector_heads(job[1]) else "scalar_scales", job[1]))
            else:
                readers[tag].append(("rope", job[1]))
        results_in_order = [i for i in range(N_BANKS) if turned(i)]
        rotated_in_order = [i for i in range(N_BANKS) if not turned(i) and BANKS[i][0] != "v"]

        def buffers_free(job, tiles):
            tag, first = first_tile[job]
            return [readers[tag][first + k - BANK_BUFS[tag]] for k in range(tiles) if first + k >= BANK_BUFS[tag]]

        def planes_ready(u):
            return [("widen", u, t) for t in range(PACK)]

        def planes_read(u):
            return [("pe_interleave", u, b) for b in turned_parts(u)] + ([("interleave", u)] if INTERLEAVE[u] != "P" else [])

        def interleaved_made(u):
            return ([("interleave", u)] if INTERLEAVE[u] != "P" else []) + [("evacuate", u, b) for b in turned_parts(u)]

        def earlier(i, order, steps):
            return [order[order.index(i) - steps]] if i in order and order.index(i) >= steps else []

        def needs(job):
            kind = job[0]
            if kind == "transpose":
                return buffers_free(job, 2)
            if kind == "x_copy":
                return [("transpose", job[1])]
            if kind == "x_quantise":
                return [("x_copy", m) for m in range(TOKEN_TILES)]
            if kind == "table_transpose":
                return buffers_free(job, 1) + [("negate_sin",)]
            if kind == "table_copy":
                return [("table_transpose",)]
            if kind == "widen":
                u = job[1]
                out = [("widen", v, t) for v in back(u, 1) for t in range(PACK)]
                for v in back(u, WIDE_BUFS[stream_of(u)]):
                    out = out + planes_read(v)
                return out
            if kind == "interleave" or (kind == "evacuate" and job[2] == 0 and INTERLEAVE[job[1]] == "P"):
                u = job[1]
                out = planes_ready(u) if kind == "interleave" else [("pe_interleave", u, 0)]
                for v in back(u, 1):
                    out = out + interleaved_made(v)[0:1]
                return out + [("quantise", v) for v in back(u, INTERLEAVED_BUFS[stream_of(u)])]
            if kind == "evacuate":
                return [("pe_interleave", job[1], job[2]), ("interleave", job[1]) if INTERLEAVE[job[1]] == "H" else ("evacuate", job[1], 0)]
            if kind == "pe_interleave":
                return planes_ready(job[1]) + buffers_free(job, 1)
            if kind == "quantise":
                return interleaved_made(job[1])
            if kind == "kv_quantise":
                return [("kv_evacuate", g) for g in range(PASSES)]
            if kind == "kv_pe_interleave":
                return buffers_free(job, 1)
            if kind == "kv_evacuate":
                return [("kv_pe_interleave", job[1])] if KV == "P" else []
            if kind == "fill":
                i = job[1]
                out = buffers_free(job, 1)
                out = out + [("x_quantise",)]
                if BANKS[i][0] in ("kv", "v") or BANKS[i] == ("t", HEADS):
                    return out + [("kv_quantise",)]
                if BANKS[i][0] in "ts":
                    half = BANKS[i][1] // HEADS_PER_UNIT
                else:
                    half = BANKS[i][1] // (UNIT_COLS // BANK_COLS)
                return out + [("quantise", half * PASSES + g) for g in range(PASSES)]
            if kind == "rope":
                i = job[1]
                out = [("fill", i), ("negate_sin",)] + ([("rope", i - 1)] if i else [])
                if turned(i):
                    out.append(("table_copy",))
                with_products = [k for k in range(N_BANKS) if BANKS[k][0] != "v"]
                out.extend([("turn_back" if turned(k) else "add", k) for k in earlier(i, with_products, PRODUCTS_BUFS)])
                return out
            if kind == "add":
                i = job[1]
                before = earlier(i, rotated_in_order, 1)
                return [("rope", i)] + [("add", k) for k in before] + [("store", k) for k in earlier(i, rotated_in_order, ROTATED_BUFS)]
            if kind == "turn_back":
                return [("rope", job[1])] + buffers_free(job, 1)
            if kind == "sum_squares":
                return [("turn_back" if turned(job[1]) else "add", job[1])]
            if kind == "take_inverse_rms":
                return [("sum_squares", k) for k in (2 * job[1], 2 * job[1] + 1) if heads_of(k)]
            if kind == "scalar_scales":
                i = job[1]
                if not scalar_heads(i) and not turned(i):
                    return []
                return [("take_inverse_rms", i // 2)] + ([("store", k) for k in earlier(i, results_in_order, RESULT_BUFS)] if turned(i) else [])
            if kind == "gpsimd_scales":
                return [("take_inverse_rms", job[1] // 2)]
            if kind == "vector_scales":
                return [("scalar_scales", job[1])] if turned(job[1]) else [("take_inverse_rms", job[1] // 2)] if vector_heads(job[1]) else []
            if kind == "store_v":
                return [("rope", job[1])]
            if kind == "store":
                return [("gpsimd_scales", job[1])] if job[1] in GPSIMD_SCALES else [("scalar_scales", job[1]), ("vector_scales", job[1])]
            return []

        written = set()
        place = dict((name, 0) for name in queues)
        left = sum(len(queues[name]) for name in queues)
        while left:
            moved = False
            for name in QUEUE_NAMES:
                while place[name] < len(queues[name]) and all(need in written for need in needs(queues[name][place[name]])):
                    job = queues[name][place[name]]
                    actions[job[0]](*job[1:])
                    written.add(job)
                    place[name] += 1
                    left -= 1
                    moved = True
            assert moved, "the queues wait for each other: %s" % str([queues[name][place[name]] for name in QUEUE_NAMES if place[name] < len(queues[name])])
